import numpy as np
import ml_dtypes


def mxq(x, axis, fmt="e4m3"):
    dtype, down = {"e4m3": (ml_dtypes.float8_e4m3fn, 7), "e5m2": (ml_dtypes.float8_e5m2, 14)}[fmt]
    v = np.moveaxis(np.asarray(x, np.float32).astype(ml_dtypes.bfloat16).astype(np.float64), axis, -1)
    blocks = v.reshape(v.shape[:-1] + (-1, 32))
    amax = np.abs(blocks).max(-1, keepdims=True)
    byte = np.maximum(np.where(amax > 0, np.frexp(amax)[1] - 1 + 127, 0) - down, 1)
    scale = np.exp2(byte - 127.0)
    codes = (blocks / scale).astype(np.float32).astype(dtype).astype(np.float64)
    return np.moveaxis((codes * scale).reshape(v.shape), -1, axis)


WIDE = False


def mx_kscale(k):
    if not WIDE:
        return np.ones(k)
    levels = np.array([10, -10, 5, -5, 0])
    a = np.random.permutation(np.resize(levels, k // 512 * 4)).reshape(k // 512, 4)
    idx = np.arange(k)
    return np.exp2(a[idx // 512, idx % 128 // 32])


BF16 = ml_dtypes.bfloat16


def bf(x):
    return np.asarray(x, np.float32).astype(BF16)


def f64(x):
    return np.asarray(x).astype(np.float64)


B, G, M, S, H = 64, 10, 4, 8192, 64
ALPHA = 1.1


def entmax(alpha, v):
    v = v - np.max(v, axis=-1, keepdims=True)
    e = np.exp(v)
    s = (np.sum(e ** alpha, axis=-1, keepdims=True) + 1e-5) ** (1.0 / alpha)
    return e / s


def layernorm(h, w, b):
    mu = np.mean(h, axis=-1, keepdims=True)
    var = np.mean((h - mu) ** 2, axis=-1, keepdims=True)
    return (h - mu) * (1.0 / np.sqrt(var + 1e-5)) * w + b


def sigmoid(v):
    return 1.0 / (1.0 + np.exp(-v))


def group_matmul(a, w):
    nb, ng, nm, ns = a.shape
    y = a.transpose(1, 0, 2, 3).reshape(ng, nb * nm, ns) @ w.transpose(0, 2, 1)
    return y.reshape(ng, nb, nm, w.shape[1]).transpose(1, 0, 2, 3)


def setup_inputs():
    k = mx_kscale(S)
    ws = 0.003 * S ** (1.0 / ALPHA - 0.5)
    return {"x": bf(np.random.standard_normal((B, G * S)) * np.tile(k, G)),
            "W_masks": bf(np.random.standard_normal((G, M, S))),
            "W1": bf((np.random.standard_normal((G, H, S)) + 0.3) * ws / k),
            "W2": bf((np.random.standard_normal((G, H, S)) + 0.3) * ws / k),
            "ln1_w": bf(1.0 + 0.2 * np.random.standard_normal((G, H))),
            "ln1_b": bf(0.2 * np.random.standard_normal((G, H))),
            "ln2_w": bf(1.0 + 0.2 * np.random.standard_normal((G, H))),
            "ln2_b": bf(0.2 * np.random.standard_normal((G, H)))}


def reference(x, W_masks, W1, W2, ln1_w, ln1_b, ln2_w, ln2_b):
    g, m, s = W_masks.shape
    b = x.shape[0]
    xg = f64(x).reshape(b, g, s)
    mask = entmax(ALPHA, f64(W_masks))
    weighted = xg[:, :, None, :] * mask[None]
    wq = mxq(weighted, 3, "e4m3")
    h1 = group_matmul(wq, mxq(f64(W1), 2, "e4m3"))
    h2 = group_matmul(wq, mxq(f64(W2), 2, "e4m3"))
    n1 = layernorm(h1, f64(ln1_w)[None, :, None, :], f64(ln1_b)[None, :, None, :])
    n2 = layernorm(h2, f64(ln2_w)[None, :, None, :], f64(ln2_b)[None, :, None, :])
    activated = np.maximum(sigmoid(n1) * n2, 0.0)
    group_out = np.sum(activated, axis=2)
    return group_out.reshape(b, g * group_out.shape[-1])

@@ -1,0 +1,348 @@
+from contextlib import ExitStack
+
+import concourse.mybir as mybir
+from concourse.masks import make_identity
+
+F32 = mybir.dt.float32
+BF16 = mybir.dt.bfloat16
+U32 = mybir.dt.uint32
+U8 = mybir.dt.uint8
+FP8X4 = mybir.dt.float8_e4m3fn_x4
+ALU = mybir.AluOpType
+FUNC = mybir.ActivationFunctionType
+AXIS_X = mybir.AxisListType.X
+
+B, G, M, S, H = 64, 10, 4, 8192, 64
+ALPHA = 1.1
+EPS = 1e-5
+FLOPS = 2 * 2 * B * G * M * S * H
+
+P = 128
+PACK = 4
+K_PASS = P * PACK
+PASSES = S // K_PASS
+BANK = 512
+PAIRS = G // 2
+UNIT_PASSES = 4
+UNITS = PASSES // UNIT_PASSES
+UNIT_K = UNIT_PASSES * K_PASS
+ROWS = G * M
+MASK_COLS = ROWS * S // P
+ROW_PASSES = MASK_COLS // K_PASS
+
+
+LOAD_AHEAD = 3
+N_UNITS = PAIRS * UNITS
+PER_ROW = PASSES * PACK
+LN_ROWS = 8
+
+
+def tile_dynamicfeaturegroupinglayer_k_kernel(
+    tc, x, W_masks, W1, W2, ln1_w, ln1_b, ln2_w, ln2_b, out
+):
+    nc = tc.nc
+    with ExitStack() as ctx:
+        const = ctx.enter_context(tc.tile_pool(name="const", bufs=1))
+        loads = ctx.enter_context(tc.tile_pool(name="loads", bufs=LOAD_AHEAD + 1))
+        stage = ctx.enter_context(tc.tile_pool(name="stage", bufs=3))
+        quant = ctx.enter_context(tc.tile_pool(name="quant", bufs=4))
+        small = ctx.enter_context(tc.tile_pool(name="small", bufs=2))
+        banks = ctx.enter_context(tc.psum_pool(name="banks", bufs=4))
+        sums = ctx.enter_context(tc.psum_pool(name="sums", bufs=1))
+        ctx.enter_context(tc.manual_schedule())
+
+        x_rows = x.rearrange("b (h c) -> (b h) c", h=2)
+        out_view = out.rearrange("b (h gi j) -> b h gi j", h=2, gi=PAIRS)
+
+        x_loaded, w_loaded = {}, {}
+        x_ready, w_ready, w_quantised = {}, {}, {}
+        acc, normed_of = {}, {}
+
+        def load(n):
+            gi, unit = divmod(n, UNITS)
+            first_s = unit * UNIT_K
+            x_sb = loads.tile([P, UNIT_K], BF16, name="x_sb", tag="x_sb")
+            nc.sync.dma_start(
+                out=x_sb[:], in_=x_rows[:, gi * S + first_s : gi * S + first_s + UNIT_K]
+            )
+            x_loaded[n] = x_sb
+            for h in range(2):
+                g = gi + PAIRS * h
+                w_sb = loads.tile([P, UNIT_K], BF16, name="w_sb", tag="w_sb", bufs=2 * (LOAD_AHEAD + 1))
+                nc.sync.dma_start(out=w_sb[0:P:2, :], in_=W1[g, :, first_s : first_s + UNIT_K])
+                nc.sync.dma_start(out=w_sb[1:P:2, :], in_=W2[g, :, first_s : first_s + UNIT_K])
+                w_loaded[(n, h)] = w_sb
+
+        logits_bf = const.tile([P, MASK_COLS], BF16, name="logits_bf")
+        nc.sync.dma_start(
+            out=logits_bf[:],
+            in_=W_masks.rearrange("g m s -> (g m s)").rearrange("(r f) -> r f", r=P),
+        )
+        for n in range(LOAD_AHEAD):
+            load(n)
+
+        ident = const.tile([P, P], F32, name="ident")
+        make_identity(nc, ident[:])
+        ln_raw = const.tile([P, 4, G * H], BF16, name="ln_raw")
+        for n, vec in enumerate((ln1_w, ln2_w, ln1_b, ln2_b)):
+            nc.gpsimd.dma_start(
+                out=ln_raw[:, n, :], in_=vec.rearrange("g j -> (g j)").partition_broadcast(P)
+            )
+        unzip = const.tile([P, P], F32, name="unzip")
+        nc.vector.tensor_copy(
+            out=unzip[:].rearrange("p (h a) -> p h a", h=2),
+            in_=ident[:].rearrange("p (a h) -> p h a", h=2),
+        )
+        ones = const.tile([P, P], F32, name="ones")
+        nc.vector.memset(ones[:], 1.0)
+        fold = const.tile([P, P], F32, name="fold")
+        for half in range(2):
+            nc.vector.tensor_tensor(
+                out=fold[:, half * H : (half + 1) * H],
+                in0=ident[:, 0:H],
+                in1=ident[:, H : 2 * H],
+                op=ALU.add,
+            )
+        part_max = const.tile([P, P], F32, name="part_max")
+        nc.vector.memset(part_max[:], 0.0)
+        part_sum = const.tile([P, P], F32, name="part_sum")
+        nc.vector.memset(part_sum[:], 0.0)
+
+        def transpose_and_group(rows, grouped):
+            words = rows[:].bitcast(F32)
+            grouped_words = grouped[:].bitcast(F32)
+            for half in range(UNIT_PASSES // 2):
+                bank = banks.tile([P, BANK], F32, name="bank", tag="bank")
+                for k in range(4):
+                    first = half * BANK + k * P
+                    nc.tensor.transpose(
+                        out=bank[:, k * P : (k + 1) * P],
+                        in_=words[:, first : first + P],
+                        identity=unzip[:],
+                    )
+                nc.scalar.copy(
+                    out=grouped_words[:, half * BANK : (half + 1) * BANK].rearrange(
+                        "p (c col u) -> p c col u", c=2, u=2
+                    ),
+                    in_=bank[:].rearrange("p (c u col) -> p c col u", c=2, u=2),
+                )
+
+        def prepare(n):
+            for h in range(2):
+                w_grouped = stage.tile([P, UNIT_K], BF16, name="w_grouped", tag="w_grouped", bufs=4, align_bytes=64)
+                transpose_and_group(w_loaded[(n, h)], w_grouped)
+                w_ready[(n, h)] = w_grouped
+            x_grouped = stage.tile([P, UNIT_K], BF16, name="x_grouped", tag="x_grouped")
+            transpose_and_group(x_loaded[n], x_grouped)
+            x_ready[n] = x_grouped
+
+        def quantise(values, tag):
+            codes = quant.tile([P, UNIT_K // PACK], U32, name="codes_" + tag, tag="codes_" + tag, align_bytes=64)
+            scales = quant.tile([P, UNIT_K // PACK], U8, name="scales_" + tag, tag="scales_" + tag, align_bytes=64)
+            nc.vector.quantize_mx(out=codes[:].bitcast(FP8X4), scales=scales[:], in_=values[:])
+            return codes, scales
+
+        logit_words = logits_bf[:].bitcast(F32)
+        logits = const.tile([P, MASK_COLS], F32, name="logits")
+        logits_by_i = logits[:].rearrange("p (r i u e) -> p i r u e", i=ROW_PASSES, u=2, e=2)
+        for i in range(ROW_PASSES):
+            bank = banks.tile([P, BANK], F32, name="bank", tag="bank")
+            for u in range(2):
+                k = 2 * i + u
+                nc.tensor.transpose(
+                    out=bank[:, u * P : (u + 1) * P],
+                    in_=logit_words[:, k * P : (k + 1) * P],
+                    identity=ident[:],
+                )
+            nc.scalar.copy(
+                out=logits_by_i[:, i],
+                in_=bank[:, 0 : 2 * P].bitcast(BF16).rearrange("p (u r e) -> p r u e", u=2, e=2),
+            )
+        logits_rows = logits[:].rearrange("p (row k) -> p row k", k=PER_ROW)
+
+        prepare(0)
+
+        nc.vector.tensor_reduce(out=part_max[:, 0:ROWS], in_=logits_rows, axis=AXIS_X, op=ALU.max)
+        bank = banks.tile([P, BANK], F32, name="bank", tag="bank")
+        nc.tensor.transpose(out=bank[:, 0:P], in_=part_max[:], identity=ident[:])
+        row_max = const.tile([P, 1], F32, name="row_max")
+        nc.vector.tensor_reduce(out=row_max[:], in_=bank[:, 0:P], axis=AXIS_X, op=ALU.max)
+        max_bank = banks.tile([P, BANK], F32, name="max_bank", tag="bank")
+        nc.tensor.matmul(
+            out=max_bank[:, 0:P],
+            lhsT=row_max[:, 0:1].to_broadcast([P, P]),
+            rhs=ident[:],
+            start=True,
+            stop=True,
+        )
+        shifted = const.tile([P, MASK_COLS], F32, name="shifted")
+        nc.vector.tensor_tensor(
+            out=shifted[:].rearrange("p (row k) -> p row k", k=PER_ROW),
+            in0=logits_rows,
+            in1=max_bank[:, 0:ROWS].unsqueeze(2).to_broadcast([P, ROWS, PER_ROW]),
+            op=ALU.subtract,
+        )
+        e_alpha = const.tile([P, MASK_COLS], F32, name="e_alpha")
+        nc.scalar.activation(out=e_alpha[:], in_=shifted[:], func=FUNC.Exp, scale=ALPHA)
+        e = const.tile([P, MASK_COLS], F32, name="e")
+        nc.scalar.activation(out=e[:], in_=shifted[:], func=FUNC.Exp)
+        for h in range(2):
+            w_quantised[(0, h)] = quantise(w_ready[(0, h)], "w")
+        nc.vector.tensor_reduce(
+            out=part_sum[:, 0:ROWS],
+            in_=e_alpha[:].rearrange("p (row k) -> p row k", k=PER_ROW),
+            axis=AXIS_X,
+            op=ALU.add,
+        )
+        sum_bank = banks.tile([P, BANK], F32, name="sum_bank", tag="bank")
+        nc.tensor.matmul(out=sum_bank[:, 0:P], lhsT=ones[:], rhs=part_sum[:], start=True, stop=True)
+        norm = const.tile([P, ROWS], F32, name="norm")
+        nc.vector.tensor_scalar_add(out=norm[:], in0=sum_bank[:, 0:ROWS], scalar1=EPS)
+        nc.scalar.activation(out=norm[:], in_=norm[:], func=FUNC.Ln)
+        inv_norm = const.tile([P, ROWS], F32, name="inv_norm")
+        nc.scalar.activation(out=inv_norm[:], in_=norm[:], func=FUNC.Exp, scale=-1.0 / ALPHA)
+        mask = const.tile([P, G * 2, PASSES, 2, PACK], F32, name="mask")
+        e_view = e[:].rearrange("p (gm m2 c t) -> p gm m2 c t", m2=2, c=PASSES, t=PACK)
+        inv_view = inv_norm[:].rearrange("p (gm m2) -> p gm m2", m2=2)
+        for m2 in range(2):
+            nc.vector.tensor_tensor(
+                out=mask[:, :, :, m2, :],
+                in0=e_view[:, :, m2],
+                in1=inv_view[:, :, m2].unsqueeze(2).unsqueeze(3).to_broadcast([P, G * 2, PASSES, PACK]),
+                op=ALU.mult,
+            )
+
+        gain = const.tile([P, G, 2, H], F32, name="gain")
+        shift = const.tile([P, G, 2, H], F32, name="shift")
+        nc.scalar.copy(out=gain[:], in_=ln_raw[:, 0:2, :].rearrange("p w (g j) -> p g w j", j=H))
+        nc.scalar.copy(out=shift[:], in_=ln_raw[:, 2:4, :].rearrange("p w (g j) -> p g w j", j=H))
+
+        def multiply(n, h, mt):
+            gi, unit = divmod(n, UNITS)
+            g = gi + PAIRS * h
+            shape = [P, UNIT_PASSES, 2, B, PACK]
+            x_view = x_ready[n][:].rearrange("p (c h b t) -> p c h b t", c=UNIT_PASSES, h=2, t=PACK)
+            weighted = stage.tile([P, UNIT_K], BF16, name="weighted", tag="weighted", align_bytes=64)
+            nc.vector.tensor_tensor(
+                out=weighted[:].rearrange("p (c m b t) -> p c m b t", c=UNIT_PASSES, m=2, t=PACK),
+                in0=x_view[:, :, h].unsqueeze(2).to_broadcast(shape),
+                in1=mask[:, 2 * g + mt, unit * UNIT_PASSES : (unit + 1) * UNIT_PASSES]
+                .unsqueeze(3)
+                .to_broadcast(shape),
+                op=ALU.mult,
+            )
+            return weighted
+
+        def contract(n, h, mt, weighted):
+            unit = n % UNITS
+            if unit == 0:
+                acc_tile = sums.tile([P, P], F32, name="acc%d%d" % (h, mt), tag="acc%d%d" % (h, mt))
+                acc[(h, mt)] = acc_tile
+            a_codes, a_scales = quantise(weighted, "a")
+            w_codes, w_scales = w_quantised[(n, h)]
+            for c in range(UNIT_PASSES):
+                cols = slice(c * P, (c + 1) * P)
+                nc.tensor.matmul_mx(
+                    out=acc[(h, mt)][:],
+                    lhsT=a_codes[:, cols].bitcast(FP8X4),
+                    lhsT_scale=a_scales[:, cols],
+                    rhs=w_codes[:, cols].bitcast(FP8X4),
+                    rhs_scale=w_scales[:, cols],
+                    start=(unit == 0 and c == 0),
+                    stop=(unit == UNITS - 1 and c == UNIT_PASSES - 1),
+                )
+
+        def normalise(gi):
+            scratch = small.tile([P, H], F32, name="scratch", tag="scratch")
+            row_sum = small.tile([P, LN_ROWS], F32, name="row_sum", tag="row_sum")
+            neg_mean = small.tile([P, LN_ROWS], F32, name="neg_mean", tag="neg_mean")
+            sq_sum = small.tile([P, LN_ROWS], F32, name="sq_sum", tag="sq_sum")
+            rstd = small.tile([P, LN_ROWS], F32, name="rstd", tag="rstd")
+            centred = small.tile([P, LN_ROWS, H], F32, name="centred", tag="centred")
+            normed = small.tile([P, LN_ROWS, H], F32, name="normed", tag="normed")
+            pieces = [
+                (4 * h + 2 * mt + w, acc[(h, mt)][:, w * H : (w + 1) * H])
+                for h in range(2)
+                for mt in range(2)
+                for w in range(2)
+            ]
+            for i, piece in pieces:
+                nc.scalar.activation(
+                    out=scratch[:], in_=piece, func=FUNC.Identity, accum_out=row_sum[:, i : i + 1]
+                )
+            nc.scalar.mul(out=neg_mean[:], in_=row_sum[:], mul=-1.0 / H)
+            for i, piece in pieces:
+                nc.scalar.activation(
+                    out=centred[:, i, :], in_=piece, func=FUNC.Identity, bias=neg_mean[:, i : i + 1]
+                )
+            for i in range(LN_ROWS):
+                nc.scalar.activation(
+                    out=scratch[:], in_=centred[:, i, :], func=FUNC.Square, accum_out=sq_sum[:, i : i + 1]
+                )
+            nc.scalar.activation(out=rstd[:], in_=sq_sum[:], func=FUNC.Copy, scale=1.0 / H, bias=EPS)
+            nc.scalar.activation(out=rstd[:], in_=rstd[:], func=FUNC.Abs_reciprocal_sqrt)
+            for i in range(LN_ROWS):
+                nc.scalar.mul(out=normed[:, i, :], in_=centred[:, i, :], mul=rstd[:, i : i + 1])
+            normed_of[gi] = normed
+
+        def gate_and_store(gi):
+            normed = normed_of[gi]
+            normed_view = normed[:].rearrange("p (h mt w) j -> p h mt (w j)", h=2, mt=2)
+            for table, op in ((gain, ALU.mult), (shift, ALU.add)):
+                nc.vector.tensor_tensor(
+                    out=normed_view,
+                    in0=normed_view,
+                    in1=table[:].rearrange("p g w j -> p g (w j)")[:, gi:G:PAIRS, :]
+                    .unsqueeze(2)
+                    .to_broadcast([P, 2, 2, 2 * H]),
+                    op=op,
+                )
+            by_w = normed[:].rearrange("p (hm w) j -> p hm w j", w=2)
+            gate = small.tile([P, 4, H], F32, name="gate", tag="gate")
+            nc.scalar.activation(out=gate[:], in_=by_w[:, :, 0, :], func=FUNC.Sigmoid)
+            gated = small.tile([P, 2, 2, H], F32, name="gated", tag="gated")
+            nc.vector.scalar_tensor_tensor(
+                out=gated[:].rearrange("p h mt j -> p (h mt) j"),
+                in0=by_w[:, :, 1, :],
+                scalar=0.0,
+                in1=gate[:],
+                op0=ALU.max,
+                op1=ALU.mult,
+            )
+            two_masks = small.tile([P, 2, H], F32, name="two_masks", tag="two_masks")
+            nc.vector.tensor_tensor(
+                out=two_masks[:], in0=gated[:, :, 0, :], in1=gated[:, :, 1, :], op=ALU.add
+            )
+            out_bank = banks.tile([P, BANK], F32, name="out_bank", tag="bank")
+            nc.tensor.matmul(
+                out=out_bank[:, 0:P],
+                lhsT=fold[:],
+                rhs=two_masks[:].rearrange("p h j -> p (h j)"),
+                start=True,
+                stop=True,
+            )
+            result = small.tile([P, 2, H], F32, name="result", tag="result")
+            nc.scalar.copy(out=result[0:B].rearrange("b h j -> b (h j)"), in_=out_bank[0:B, 0:P])
+            nc.sync.dma_start(out=out_view[:, :, gi, :], in_=result[0:B])
+
+        waiting = None
+        for n in range(N_UNITS):
+            if n + LOAD_AHEAD < N_UNITS:
+                load(n + LOAD_AHEAD)
+            if n + 1 < N_UNITS:
+                prepare(n + 1)
+            for h in range(2):
+                for mt in range(2):
+                    weighted = multiply(n, h, mt)
+                    if waiting is not None:
+                        contract(*waiting)
+                        if waiting[0] % UNITS == UNITS - 1 and waiting[1:3] == (1, 1):
+                            normalise(waiting[0] // UNITS)
+                    waiting = (n, h, mt, weighted)
+                if n + 1 < N_UNITS:
+                    w_quantised[(n + 1, h)] = quantise(w_ready[(n + 1, h)], "w")
+            if n % UNITS == 0 and n > 0:
+                gate_and_store(n // UNITS - 1)
+        contract(*waiting)
+        normalise(PAIRS - 1)
+        gate_and_store(PAIRS - 1)

@@ -47,7 +47,8 @@ def tile_dynamicfeaturegroupinglayer_k_kernel(
         stage = ctx.enter_context(tc.tile_pool(name="stage", bufs=3))
         quant = ctx.enter_context(tc.tile_pool(name="quant", bufs=4))
         small = ctx.enter_context(tc.tile_pool(name="small", bufs=2))
-        banks = ctx.enter_context(tc.psum_pool(name="banks", bufs=4))
+        banks = ctx.enter_context(tc.psum_pool(name="banks", bufs=2))
+        mask_banks = ctx.enter_context(tc.psum_pool(name="mask_banks", bufs=2))
         sums = ctx.enter_context(tc.psum_pool(name="sums", bufs=1))
         ctx.enter_context(tc.manual_schedule())
 
@@ -56,7 +57,7 @@ def tile_dynamicfeaturegroupinglayer_k_kernel(
 
         x_loaded, w_loaded = {}, {}
         x_ready, w_ready, w_quantised = {}, {}, {}
-        acc, normed_of = {}, {}
+        acc, normed_of, mask_of = {}, {}, {}
 
         def load(n):
             gi, unit = divmod(n, UNITS)
@@ -217,18 +218,35 @@ def tile_dynamicfeaturegroupinglayer_k_kernel(
         nc.scalar.copy(out=gain[:], in_=ln_raw[:, 0:2, :].rearrange("p w (g j) -> p g w j", j=H))
         nc.scalar.copy(out=shift[:], in_=ln_raw[:, 2:4, :].rearrange("p w (g j) -> p g w j", j=H))
 
+        def masks_to_psum(gi):
+            mask_bank = mask_banks.tile([P, 4, PASSES, 2, PACK], F32, name="mask_bank", tag="mask_bank")
+            for h in range(2):
+                g = gi + PAIRS * h
+                nc.tensor.matmul(
+                    out=mask_bank[:, 2 * h : 2 * h + 2].rearrange("p a c m t -> p (a c m t)"),
+                    lhsT=ident[:],
+                    rhs=mask[:, 2 * g : 2 * g + 2].rearrange("p a c m t -> p (a c m t)"),
+                    start=True,
+                    stop=True,
+                )
+            mask_of[gi] = mask_bank
+
         def multiply(n, h, mt):
             gi, unit = divmod(n, UNITS)
             g = gi + PAIRS * h
+            passes = slice(unit * UNIT_PASSES, (unit + 1) * UNIT_PASSES)
             shape = [P, UNIT_PASSES, 2, B, PACK]
             x_view = x_ready[n][:].rearrange("p (c h b t) -> p c h b t", c=UNIT_PASSES, h=2, t=PACK)
-            weighted = stage.tile([P, UNIT_K], BF16, name="weighted", tag="weighted", align_bytes=64)
-            nc.vector.tensor_tensor(
+            if (h, mt) == (1, 1):
+                weighted = stage.tile([P, UNIT_K], BF16, name="weighted_g", tag="weighted_g", bufs=2, align_bytes=64)
+                engine, mask_view = nc.gpsimd, mask[:, 2 * g + mt, passes]
+            else:
+                weighted = stage.tile([P, UNIT_K], BF16, name="weighted", tag="weighted", align_bytes=64)
+                engine, mask_view = nc.vector, mask_of[gi][:, 2 * h + mt, passes]
+            engine.tensor_tensor(
                 out=weighted[:].rearrange("p (c m b t) -> p c m b t", c=UNIT_PASSES, m=2, t=PACK),
                 in0=x_view[:, :, h].unsqueeze(2).to_broadcast(shape),
-                in1=mask[:, 2 * g + mt, unit * UNIT_PASSES : (unit + 1) * UNIT_PASSES]
-                .unsqueeze(3)
-                .to_broadcast(shape),
+                in1=mask_view.unsqueeze(3).to_broadcast(shape),
                 op=ALU.mult,
             )
             return weighted
@@ -325,12 +343,15 @@ def tile_dynamicfeaturegroupinglayer_k_kernel(
             nc.scalar.copy(out=result[0:B].rearrange("b h j -> b (h j)"), in_=out_bank[0:B, 0:P])
             nc.sync.dma_start(out=out_view[:, :, gi, :], in_=result[0:B])
 
+        masks_to_psum(0)
         waiting = None
         for n in range(N_UNITS):
             if n + LOAD_AHEAD < N_UNITS:
                 load(n + LOAD_AHEAD)
             if n + 1 < N_UNITS:
                 prepare(n + 1)
+                if (n + 1) % UNITS == 0:
+                    masks_to_psum((n + 1) // UNITS)
             for h in range(2):
                 for mt in range(2):
                     weighted = multiply(n, h, mt)

@@ -47,8 +47,7 @@ def tile_dynamicfeaturegroupinglayer_k_kernel(
         stage = ctx.enter_context(tc.tile_pool(name="stage", bufs=3))
         quant = ctx.enter_context(tc.tile_pool(name="quant", bufs=4))
         small = ctx.enter_context(tc.tile_pool(name="small", bufs=2))
-        banks = ctx.enter_context(tc.psum_pool(name="banks", bufs=2))
-        mask_banks = ctx.enter_context(tc.psum_pool(name="mask_banks", bufs=2))
+        banks = ctx.enter_context(tc.psum_pool(name="banks", bufs=4))
         sums = ctx.enter_context(tc.psum_pool(name="sums", bufs=1))
         ctx.enter_context(tc.manual_schedule())
 
@@ -57,7 +56,7 @@ def tile_dynamicfeaturegroupinglayer_k_kernel(
 
         x_loaded, w_loaded = {}, {}
         x_ready, w_ready, w_quantised = {}, {}, {}
-        acc, normed_of, mask_of = {}, {}, {}
+        acc, normed_of, shared_of = {}, {}, {}
 
         def load(n):
             gi, unit = divmod(n, UNITS)
@@ -218,35 +217,40 @@ def tile_dynamicfeaturegroupinglayer_k_kernel(
         nc.scalar.copy(out=gain[:], in_=ln_raw[:, 0:2, :].rearrange("p w (g j) -> p g w j", j=H))
         nc.scalar.copy(out=shift[:], in_=ln_raw[:, 2:4, :].rearrange("p w (g j) -> p g w j", j=H))
 
-        def masks_to_psum(gi):
-            mask_bank = mask_banks.tile([P, 4, PASSES, 2, PACK], F32, name="mask_bank", tag="mask_bank")
-            for h in range(2):
-                g = gi + PAIRS * h
-                nc.tensor.matmul(
-                    out=mask_bank[:, 2 * h : 2 * h + 2].rearrange("p a c m t -> p (a c m t)"),
-                    lhsT=ident[:],
-                    rhs=mask[:, 2 * g : 2 * g + 2].rearrange("p a c m t -> p (a c m t)"),
-                    start=True,
-                    stop=True,
-                )
-            mask_of[gi] = mask_bank
+        def scalar_multiply(n):
+            gi, unit = divmod(n, UNITS)
+            g = gi + PAIRS
+            x_view = x_ready[n][:].rearrange("p (c h b t) -> p c h b t", c=UNIT_PASSES, h=2, t=PACK)
+            shared = stage.tile([P, UNIT_K], BF16, name="shared", tag="shared", bufs=2, align_bytes=64)
+            shared_view = shared[:].rearrange("p (c m b t) -> p c m b t", c=UNIT_PASSES, m=2, t=PACK)
+            for c in range(UNIT_PASSES):
+                for t in range(PACK):
+                    nc.scalar.activation(
+                        out=shared_view[:, c, 1, :, t],
+                        in_=x_view[:, c, 1, :, t],
+                        func=FUNC.Copy,
+                        scale=mask[:, 2 * g + 1, unit * UNIT_PASSES + c, 1, t : t + 1],
+                    )
+            shared_of[n] = shared
 
         def multiply(n, h, mt):
             gi, unit = divmod(n, UNITS)
             g = gi + PAIRS * h
-            passes = slice(unit * UNIT_PASSES, (unit + 1) * UNIT_PASSES)
-            shape = [P, UNIT_PASSES, 2, B, PACK]
             x_view = x_ready[n][:].rearrange("p (c h b t) -> p c h b t", c=UNIT_PASSES, h=2, t=PACK)
             if (h, mt) == (1, 1):
-                weighted = stage.tile([P, UNIT_K], BF16, name="weighted_g", tag="weighted_g", bufs=2, align_bytes=64)
-                engine, mask_view = nc.gpsimd, mask[:, 2 * g + mt, passes]
+                weighted, masks_here = shared_of[n], 1
             else:
                 weighted = stage.tile([P, UNIT_K], BF16, name="weighted", tag="weighted", align_bytes=64)
-                engine, mask_view = nc.vector, mask_of[gi][:, 2 * h + mt, passes]
-            engine.tensor_tensor(
-                out=weighted[:].rearrange("p (c m b t) -> p c m b t", c=UNIT_PASSES, m=2, t=PACK),
+                masks_here = 2
+            shape = [P, UNIT_PASSES, masks_here, B, PACK]
+            nc.vector.tensor_tensor(
+                out=weighted[:].rearrange("p (c m b t) -> p c m b t", c=UNIT_PASSES, m=2, t=PACK)[
+                    :, :, 0:masks_here
+                ],
                 in0=x_view[:, :, h].unsqueeze(2).to_broadcast(shape),
-                in1=mask_view.unsqueeze(3).to_broadcast(shape),
+                in1=mask[:, 2 * g + mt, unit * UNIT_PASSES : (unit + 1) * UNIT_PASSES, 0:masks_here]
+                .unsqueeze(3)
+                .to_broadcast(shape),
                 op=ALU.mult,
             )
             return weighted
@@ -343,15 +347,14 @@ def tile_dynamicfeaturegroupinglayer_k_kernel(
             nc.scalar.copy(out=result[0:B].rearrange("b h j -> b (h j)"), in_=out_bank[0:B, 0:P])
             nc.sync.dma_start(out=out_view[:, :, gi, :], in_=result[0:B])
 
-        masks_to_psum(0)
+        scalar_multiply(0)
         waiting = None
         for n in range(N_UNITS):
             if n + LOAD_AHEAD < N_UNITS:
                 load(n + LOAD_AHEAD)
             if n + 1 < N_UNITS:
                 prepare(n + 1)
-                if (n + 1) % UNITS == 0:
-                    masks_to_psum((n + 1) // UNITS)
+                scalar_multiply(n + 1)
             for h in range(2):
                 for mt in range(2):
                     weighted = multiply(n, h, mt)

@@ -34,6 +34,7 @@ ROW_PASSES = MASK_COLS // K_PASS
 LOAD_AHEAD = 3
 N_UNITS = PAIRS * UNITS
 PER_ROW = PASSES * PACK
+PAIR_ROWS = 2 * M
 LN_ROWS = 8
 
 
@@ -56,7 +57,7 @@ def tile_dynamicfeaturegroupinglayer_k_kernel(
 
         x_loaded, w_loaded = {}, {}
         x_ready, w_ready, w_quantised = {}, {}, {}
-        acc, normed_of, shared_of = {}, {}, {}
+        acc, mask_of, shared_of = {}, {}, {}
 
         def load(n):
             gi, unit = divmod(n, UNITS)
@@ -107,6 +108,16 @@ def tile_dynamicfeaturegroupinglayer_k_kernel(
         nc.vector.memset(part_max[:], 0.0)
         part_sum = const.tile([P, P], F32, name="part_sum")
         nc.vector.memset(part_sum[:], 0.0)
+        norm_power = const.tile([P, PAIR_ROWS], F32, name="norm_power")
+        nc.vector.tensor_scalar(
+            out=norm_power[:], in0=part_max[:, 0:PAIR_ROWS], scalar1=0.0, scalar2=-1.0 / ALPHA,
+            op0=ALU.mult, op1=ALU.add,
+        )
+        rsqrt_power = const.tile([P, LN_ROWS], F32, name="rsqrt_power")
+        nc.vector.tensor_scalar(
+            out=rsqrt_power[:], in0=part_max[:, 0:LN_ROWS], scalar1=0.0, scalar2=-0.5,
+            op0=ALU.mult, op1=ALU.add,
+        )
 
         def transpose_and_group(rows, grouped):
             words = rows[:].bitcast(F32)
@@ -158,87 +169,100 @@ def tile_dynamicfeaturegroupinglayer_k_kernel(
                 out=logits_by_i[:, i],
                 in_=bank[:, 0 : 2 * P].bitcast(BF16).rearrange("p (u r e) -> p r u e", u=2, e=2),
             )
-        logits_rows = logits[:].rearrange("p (row k) -> p row k", k=PER_ROW)
 
-        prepare(0)
+        def entmax_steps(gi):
+            rows = logits[:].rearrange("p (h gi m k) -> p h gi m k", h=2, gi=PAIRS, m=M)[:, :, gi]
+            kept = {}
 
-        nc.vector.tensor_reduce(out=part_max[:, 0:ROWS], in_=logits_rows, axis=AXIS_X, op=ALU.max)
-        bank = banks.tile([P, BANK], F32, name="bank", tag="bank")
-        nc.tensor.transpose(out=bank[:, 0:P], in_=part_max[:], identity=ident[:])
-        row_max = const.tile([P, 1], F32, name="row_max")
-        nc.vector.tensor_reduce(out=row_max[:], in_=bank[:, 0:P], axis=AXIS_X, op=ALU.max)
-        max_bank = banks.tile([P, BANK], F32, name="max_bank", tag="bank")
-        nc.tensor.matmul(
-            out=max_bank[:, 0:P],
-            lhsT=row_max[:, 0:1].to_broadcast([P, P]),
-            rhs=ident[:],
-            start=True,
-            stop=True,
-        )
-        shifted = const.tile([P, MASK_COLS], F32, name="shifted")
-        nc.vector.tensor_tensor(
-            out=shifted[:].rearrange("p (row k) -> p row k", k=PER_ROW),
-            in0=logits_rows,
-            in1=max_bank[:, 0:ROWS].unsqueeze(2).to_broadcast([P, ROWS, PER_ROW]),
-            op=ALU.subtract,
-        )
-        e_alpha = const.tile([P, MASK_COLS], F32, name="e_alpha")
-        nc.scalar.activation(out=e_alpha[:], in_=shifted[:], func=FUNC.Exp, scale=ALPHA)
-        e = const.tile([P, MASK_COLS], F32, name="e")
-        nc.scalar.activation(out=e[:], in_=shifted[:], func=FUNC.Exp)
-        for h in range(2):
-            w_quantised[(0, h)] = quantise(w_ready[(0, h)], "w")
-        nc.vector.tensor_reduce(
-            out=part_sum[:, 0:ROWS],
-            in_=e_alpha[:].rearrange("p (row k) -> p row k", k=PER_ROW),
-            axis=AXIS_X,
-            op=ALU.add,
-        )
-        sum_bank = banks.tile([P, BANK], F32, name="sum_bank", tag="bank")
-        nc.tensor.matmul(out=sum_bank[:, 0:P], lhsT=ones[:], rhs=part_sum[:], start=True, stop=True)
-        norm = const.tile([P, ROWS], F32, name="norm")
-        nc.vector.tensor_scalar_add(out=norm[:], in0=sum_bank[:, 0:ROWS], scalar1=EPS)
-        nc.scalar.activation(out=norm[:], in_=norm[:], func=FUNC.Ln)
-        inv_norm = const.tile([P, ROWS], F32, name="inv_norm")
-        nc.scalar.activation(out=inv_norm[:], in_=norm[:], func=FUNC.Exp, scale=-1.0 / ALPHA)
-        mask = const.tile([P, G * 2, PASSES, 2, PACK], F32, name="mask")
-        e_view = e[:].rearrange("p (gm m2 c t) -> p gm m2 c t", m2=2, c=PASSES, t=PACK)
-        inv_view = inv_norm[:].rearrange("p (gm m2) -> p gm m2", m2=2)
-        for m2 in range(2):
-            nc.vector.tensor_tensor(
-                out=mask[:, :, :, m2, :],
-                in0=e_view[:, :, m2],
-                in1=inv_view[:, :, m2].unsqueeze(2).unsqueeze(3).to_broadcast([P, G * 2, PASSES, PACK]),
-                op=ALU.mult,
-            )
+            def partition_maxima():
+                nc.vector.tensor_reduce(
+                    out=part_max[:, 0:PAIR_ROWS].rearrange("p (h m) -> p h m", h=2),
+                    in_=rows, axis=AXIS_X, op=ALU.max,
+                )
+                turned = banks.tile([P, BANK], F32, name="turned", tag="bank")
+                nc.tensor.transpose(out=turned[:, 0:P], in_=part_max[:], identity=ident[:])
+                kept["turned"] = turned
 
-        gain = const.tile([P, G, 2, H], F32, name="gain")
-        shift = const.tile([P, G, 2, H], F32, name="shift")
-        nc.scalar.copy(out=gain[:], in_=ln_raw[:, 0:2, :].rearrange("p w (g j) -> p g w j", j=H))
-        nc.scalar.copy(out=shift[:], in_=ln_raw[:, 2:4, :].rearrange("p w (g j) -> p g w j", j=H))
+            def row_maxima():
+                row_max = small.tile([P, 1], F32, name="row_max", tag="row_max")
+                nc.vector.tensor_reduce(out=row_max[:], in_=kept["turned"][:, 0:P], axis=AXIS_X, op=ALU.max)
+                max_bank = banks.tile([P, BANK], F32, name="max_bank", tag="bank")
+                nc.tensor.matmul(
+                    out=max_bank[:, 0:P], lhsT=row_max[:, 0:1].to_broadcast([P, P]), rhs=ident[:],
+                    start=True, stop=True,
+                )
+                kept["max_bank"] = max_bank
 
-        def scalar_multiply(n):
+            def exponentials():
+                shifted = small.tile([P, PAIR_ROWS * PER_ROW], F32, name="shifted", tag="shifted")
+                nc.vector.tensor_tensor(
+                    out=shifted[:].rearrange("p (h m k) -> p h m k", h=2, m=M),
+                    in0=rows,
+                    in1=kept["max_bank"][:, 0:PAIR_ROWS]
+                    .rearrange("p (h m) -> p h m", h=2)
+                    .unsqueeze(3)
+                    .to_broadcast([P, 2, M, PER_ROW]),
+                    op=ALU.subtract,
+                )
+                e_alpha = small.tile([P, PAIR_ROWS * PER_ROW], F32, name="e_alpha", tag="e_alpha")
+                nc.scalar.activation(out=e_alpha[:], in_=shifted[:], func=FUNC.Exp, scale=ALPHA)
+                e = small.tile([P, PAIR_ROWS * PER_ROW], F32, name="e", tag="e")
+                nc.scalar.activation(out=e[:], in_=shifted[:], func=FUNC.Exp)
+                kept["e_alpha"], kept["e"] = e_alpha, e
+
+            def norms():
+                nc.vector.tensor_reduce(
+                    out=part_sum[:, 0:PAIR_ROWS],
+                    in_=kept["e_alpha"][:].rearrange("p (row k) -> p row k", k=PER_ROW),
+                    axis=AXIS_X, op=ALU.add,
+                )
+                sum_bank = banks.tile([P, BANK], F32, name="sum_bank", tag="bank")
+                nc.tensor.matmul(out=sum_bank[:, 0:P], lhsT=ones[:], rhs=part_sum[:], start=True, stop=True)
+                padded = small.tile([P, PAIR_ROWS], F32, name="padded", tag="padded")
+                nc.scalar.activation(out=padded[:], in_=sum_bank[:, 0:PAIR_ROWS], func=FUNC.Copy, bias=EPS)
+                inv_norm = small.tile([P, PAIR_ROWS], F32, name="inv_norm", tag="inv_norm")
+                nc.gpsimd.tensor_tensor(out=inv_norm[:], in0=padded[:], in1=norm_power[:], op=ALU.pow)
+                kept["inv_norm"] = inv_norm
+
+            def scale_masks():
+                mask = small.tile([P, 4, PASSES, 2, PACK], F32, name="mask", tag="mask")
+                e_view = kept["e"][:].rearrange("p (a m2 c t) -> p a m2 c t", m2=2, c=PASSES, t=PACK)
+                inv_view = kept["inv_norm"][:].rearrange("p (a m2) -> p a m2", m2=2)
+                for m2 in range(2):
+                    nc.vector.tensor_tensor(
+                        out=mask[:, :, :, m2, :],
+                        in0=e_view[:, :, m2],
+                        in1=inv_view[:, :, m2].unsqueeze(2).unsqueeze(3).to_broadcast([P, 4, PASSES, PACK]),
+                        op=ALU.mult,
+                    )
+                mask_of[gi] = mask
+
+            return [partition_maxima, row_maxima, exponentials, norms, scale_masks]
+
+        def scalar_multiply(n, h):
             gi, unit = divmod(n, UNITS)
-            g = gi + PAIRS
             x_view = x_ready[n][:].rearrange("p (c h b t) -> p c h b t", c=UNIT_PASSES, h=2, t=PACK)
-            shared = stage.tile([P, UNIT_K], BF16, name="shared", tag="shared", bufs=2, align_bytes=64)
-            shared_view = shared[:].rearrange("p (c m b t) -> p c m b t", c=UNIT_PASSES, m=2, t=PACK)
+            planes = stage.tile([P, UNIT_PASSES, PACK, B], BF16, name="planes", tag="planes", bufs=2)
             for c in range(UNIT_PASSES):
                 for t in range(PACK):
                     nc.scalar.activation(
-                        out=shared_view[:, c, 1, :, t],
-                        in_=x_view[:, c, 1, :, t],
+                        out=planes[:, c, t, :],
+                        in_=x_view[:, c, h, :, t],
                         func=FUNC.Copy,
-                        scale=mask[:, 2 * g + 1, unit * UNIT_PASSES + c, 1, t : t + 1],
+                        scale=mask_of[gi][:, 2 * h + 1, unit * UNIT_PASSES + c, 1, t : t + 1],
                     )
-            shared_of[n] = shared
+            shared = stage.tile([P, UNIT_K], BF16, name="shared", tag="shared", bufs=6, align_bytes=64)
+            nc.scalar.copy(
+                out=shared[:].rearrange("p (c m b t) -> p c m b t", c=UNIT_PASSES, m=2, t=PACK)[:, :, 1],
+                in_=planes[:].rearrange("p c t b -> p c b t"),
+            )
+            shared_of[(n, h)] = shared
 
         def multiply(n, h, mt):
             gi, unit = divmod(n, UNITS)
-            g = gi + PAIRS * h
             x_view = x_ready[n][:].rearrange("p (c h b t) -> p c h b t", c=UNIT_PASSES, h=2, t=PACK)
-            if (h, mt) == (1, 1):
-                weighted, masks_here = shared_of[n], 1
+            if mt == 1:
+                weighted, masks_here = shared_of[(n, h)], 1
             else:
                 weighted = stage.tile([P, UNIT_K], BF16, name="weighted", tag="weighted", align_bytes=64)
                 masks_here = 2
@@ -248,7 +272,7 @@ def tile_dynamicfeaturegroupinglayer_k_kernel(
                     :, :, 0:masks_here
                 ],
                 in0=x_view[:, :, h].unsqueeze(2).to_broadcast(shape),
-                in1=mask[:, 2 * g + mt, unit * UNIT_PASSES : (unit + 1) * UNIT_PASSES, 0:masks_here]
+                in1=mask_of[gi][:, 2 * h + mt, unit * UNIT_PASSES : (unit + 1) * UNIT_PASSES, 0:masks_here]
                 .unsqueeze(3)
                 .to_broadcast(shape),
                 op=ALU.mult,
@@ -274,43 +298,52 @@ def tile_dynamicfeaturegroupinglayer_k_kernel(
                     stop=(unit == UNITS - 1 and c == UNIT_PASSES - 1),
                 )
 
-        def normalise(gi):
+        gain = const.tile([P, G, 2, H], F32, name="gain")
+        shift = const.tile([P, G, 2, H], F32, name="shift")
+
+        def layer_norm_steps(gi):
             scratch = small.tile([P, H], F32, name="scratch", tag="scratch")
             row_sum = small.tile([P, LN_ROWS], F32, name="row_sum", tag="row_sum")
             neg_mean = small.tile([P, LN_ROWS], F32, name="neg_mean", tag="neg_mean")
             sq_sum = small.tile([P, LN_ROWS], F32, name="sq_sum", tag="sq_sum")
+            var_eps = small.tile([P, LN_ROWS], F32, name="var_eps", tag="var_eps")
             rstd = small.tile([P, LN_ROWS], F32, name="rstd", tag="rstd")
+            raw = small.tile([P, LN_ROWS, H], F32, name="raw", tag="raw")
             centred = small.tile([P, LN_ROWS, H], F32, name="centred", tag="centred")
             normed = small.tile([P, LN_ROWS, H], F32, name="normed", tag="normed")
-            pieces = [
-                (4 * h + 2 * mt + w, acc[(h, mt)][:, w * H : (w + 1) * H])
-                for h in range(2)
-                for mt in range(2)
-                for w in range(2)
-            ]
-            for i, piece in pieces:
+            for h in range(2):
+                for mt in range(2):
+                    first = 4 * h + 2 * mt
+                    nc.scalar.copy(
+                        out=raw[:, first : first + 2, :].rearrange("p w j -> p (w j)"), in_=acc[(h, mt)][:]
+                    )
+            for i in range(LN_ROWS):
                 nc.scalar.activation(
-                    out=scratch[:], in_=piece, func=FUNC.Identity, accum_out=row_sum[:, i : i + 1]
+                    out=scratch[:], in_=raw[:, i, :], func=FUNC.Identity, accum_out=row_sum[:, i : i + 1]
                 )
             nc.scalar.mul(out=neg_mean[:], in_=row_sum[:], mul=-1.0 / H)
-            for i, piece in pieces:
+            for i in range(LN_ROWS):
                 nc.scalar.activation(
-                    out=centred[:, i, :], in_=piece, func=FUNC.Identity, bias=neg_mean[:, i : i + 1]
+                    out=centred[:, i, :], in_=raw[:, i, :], func=FUNC.Identity, bias=neg_mean[:, i : i + 1]
                 )
             for i in range(LN_ROWS):
                 nc.scalar.activation(
                     out=scratch[:], in_=centred[:, i, :], func=FUNC.Square, accum_out=sq_sum[:, i : i + 1]
                 )
-            nc.scalar.activation(out=rstd[:], in_=sq_sum[:], func=FUNC.Copy, scale=1.0 / H, bias=EPS)
-            nc.scalar.activation(out=rstd[:], in_=rstd[:], func=FUNC.Abs_reciprocal_sqrt)
-            for i in range(LN_ROWS):
-                nc.scalar.mul(out=normed[:, i, :], in_=centred[:, i, :], mul=rstd[:, i : i + 1])
-            normed_of[gi] = normed
+            nc.scalar.activation(out=var_eps[:], in_=sq_sum[:], func=FUNC.Copy, scale=1.0 / H, bias=EPS)
+            nc.gpsimd.tensor_tensor(out=rstd[:], in0=var_eps[:], in1=rsqrt_power[:], op=ALU.pow)
 
-        def gate_and_store(gi):
-            normed = normed_of[gi]
             normed_view = normed[:].rearrange("p (h mt w) j -> p h mt (w j)", h=2, mt=2)
-            for table, op in ((gain, ALU.mult), (shift, ALU.add)):
+            by_w = normed[:].rearrange("p (hm w) j -> p hm w j", w=2)
+            half_tanh = small.tile([P, 4, H], F32, name="half_tanh", tag="half_tanh")
+            half_relu = small.tile([P, 4, H], F32, name="half_relu", tag="half_relu")
+            gated = small.tile([P, 2, 2, H], F32, name="gated", tag="gated")
+
+            def divide():
+                for i in range(LN_ROWS):
+                    nc.scalar.mul(out=normed[:, i, :], in_=centred[:, i, :], mul=rstd[:, i : i + 1])
+
+            def affine(table, op):
                 nc.vector.tensor_tensor(
                     out=normed_view,
                     in0=normed_view,
@@ -319,54 +352,74 @@ def tile_dynamicfeaturegroupinglayer_k_kernel(
                     .to_broadcast([P, 2, 2, 2 * H]),
                     op=op,
                 )
-            by_w = normed[:].rearrange("p (hm w) j -> p hm w j", w=2)
-            gate = small.tile([P, 4, H], F32, name="gate", tag="gate")
-            nc.scalar.activation(out=gate[:], in_=by_w[:, :, 0, :], func=FUNC.Sigmoid)
-            gated = small.tile([P, 2, 2, H], F32, name="gated", tag="gated")
-            nc.vector.scalar_tensor_tensor(
-                out=gated[:].rearrange("p h mt j -> p (h mt) j"),
-                in0=by_w[:, :, 1, :],
-                scalar=0.0,
-                in1=gate[:],
-                op0=ALU.max,
-                op1=ALU.mult,
-            )
-            two_masks = small.tile([P, 2, H], F32, name="two_masks", tag="two_masks")
-            nc.vector.tensor_tensor(
-                out=two_masks[:], in0=gated[:, :, 0, :], in1=gated[:, :, 1, :], op=ALU.add
-            )
-            out_bank = banks.tile([P, BANK], F32, name="out_bank", tag="bank")
-            nc.tensor.matmul(
-                out=out_bank[:, 0:P],
-                lhsT=fold[:],
-                rhs=two_masks[:].rearrange("p h j -> p (h j)"),
-                start=True,
-                stop=True,
-            )
-            result = small.tile([P, 2, H], F32, name="result", tag="result")
-            nc.scalar.copy(out=result[0:B].rearrange("b h j -> b (h j)"), in_=out_bank[0:B, 0:P])
-            nc.sync.dma_start(out=out_view[:, :, gi, :], in_=result[0:B])
 
-        scalar_multiply(0)
+            def apply_gain():
+                affine(gain, ALU.mult)
+
+            def apply_shift():
+                affine(shift, ALU.add)
+                nc.scalar.activation(out=half_tanh[:], in_=by_w[:, :, 0, :], func=FUNC.Tanh, scale=0.5)
+                nc.scalar.activation(out=half_relu[:], in_=by_w[:, :, 1, :], func=FUNC.Relu, scale=0.5)
+
+            def gate():
+                nc.vector.scalar_tensor_tensor(
+                    out=gated[:].rearrange("p h mt j -> p (h mt) j"),
+                    in0=half_tanh[:], scalar=1.0, in1=half_relu[:], op0=ALU.add, op1=ALU.mult,
+                )
+
+            def add_masks_and_store():
+                two_masks = small.tile([P, 2, H], F32, name="two_masks", tag="two_masks")
+                nc.vector.tensor_tensor(
+                    out=two_masks[:], in0=gated[:, :, 0, :], in1=gated[:, :, 1, :], op=ALU.add
+                )
+                out_bank = banks.tile([P, BANK], F32, name="out_bank", tag="bank")
+                nc.tensor.matmul(
+                    out=out_bank[:, 0:P], lhsT=fold[:], rhs=two_masks[:].rearrange("p h j -> p (h j)"),
+                    start=True, stop=True,
+                )
+                result = small.tile([P, 2, H], F32, name="result", tag="result")
+                nc.scalar.copy(out=result[0:B].rearrange("b h j -> b (h j)"), in_=out_bank[0:B, 0:P])
+                nc.sync.dma_start(out=out_view[:, :, gi, :], in_=result[0:B])
+
+            return [divide, apply_gain, apply_shift, gate, add_masks_and_store]
+
+        prepare(0)
+        first_masks = entmax_steps(0)
+        for step in first_masks[0:3]:
+            step()
+        for h in range(2):
+            w_quantised[(0, h)] = quantise(w_ready[(0, h)], "w")
+        for step in first_masks[3:]:
+            step()
+        nc.scalar.copy(out=gain[:], in_=ln_raw[:, 0:2, :].rearrange("p w (g j) -> p g w j", j=H))
+        nc.scalar.copy(out=shift[:], in_=ln_raw[:, 2:4, :].rearrange("p w (g j) -> p g w j", j=H))
+        for h in range(2):
+            scalar_multiply(0, h)
+
+        steps = []
         waiting = None
         for n in range(N_UNITS):
+            gi, unit = divmod(n, UNITS)
             if n + LOAD_AHEAD < N_UNITS:
                 load(n + LOAD_AHEAD)
+            if unit == 0 and gi + 1 < PAIRS:
+                steps.extend(entmax_steps(gi + 1))
             if n + 1 < N_UNITS:
                 prepare(n + 1)
-                scalar_multiply(n + 1)
             for h in range(2):
                 for mt in range(2):
                     weighted = multiply(n, h, mt)
                     if waiting is not None:
                         contract(*waiting)
-                        if waiting[0] % UNITS == UNITS - 1 and waiting[1:3] == (1, 1):
-                            normalise(waiting[0] // UNITS)
+                        if unit == 0 and (h, mt) == (0, 0):
+                            steps.extend(layer_norm_steps(gi - 1))
                     waiting = (n, h, mt, weighted)
+                    if steps:
+                        steps[0]()
+                        steps = steps[1:]
                 if n + 1 < N_UNITS:
                     w_quantised[(n + 1, h)] = quantise(w_ready[(n + 1, h)], "w")
-            if n % UNITS == 0 and n > 0:
-                gate_and_store(n // UNITS - 1)
+                    scalar_multiply(n + 1, h)
         contract(*waiting)
-        normalise(PAIRS - 1)
-        gate_and_store(PAIRS - 1)
+        for step in layer_norm_steps(PAIRS - 1):
+            step()

@@ -20,22 +20,23 @@ FLOPS = 2 * 2 * B * G * M * S * H
 P = 128
 PACK = 4
 K_PASS = P * PACK
-PASSES = S // K_PASS
 BANK = 512
-PAIRS = G // 2
-UNIT_PASSES = 4
-UNITS = PASSES // UNIT_PASSES
-UNIT_K = UNIT_PASSES * K_PASS
-ROWS = G * M
-MASK_COLS = ROWS * S // P
-ROW_PASSES = MASK_COLS // K_PASS
-
-
+HALVES = 2
+HALF = S // HALVES
+UNIT_K = 2048
+UNITS = HALF // UNIT_K
+UNIT_PASSES = UNIT_K // K_PASS
+N_UNITS = G * UNITS
+PASSES = S // K_PASS
+SHV = HALVES * UNITS
+CC = 2
+TILE = CC * M * B * PACK
+SCALAR_MASKS = 2
+VECTOR_MASKS = M - SCALAR_MASKS
 LOAD_AHEAD = 3
-N_UNITS = PAIRS * UNITS
-PER_ROW = PASSES * PACK
-PAIR_ROWS = 2 * M
-LN_ROWS = 8
+PAIR = 2
+PAIR_ROWS = PAIR * M
+LN_ROWS = 4
 
 
 def tile_dynamicfeaturegroupinglayer_k_kernel(
@@ -49,377 +50,428 @@ def tile_dynamicfeaturegroupinglayer_k_kernel(
         quant = ctx.enter_context(tc.tile_pool(name="quant", bufs=4))
         small = ctx.enter_context(tc.tile_pool(name="small", bufs=2))
         banks = ctx.enter_context(tc.psum_pool(name="banks", bufs=4))
+        x_banks = ctx.enter_context(tc.psum_pool(name="x_banks", bufs=2))
         sums = ctx.enter_context(tc.psum_pool(name="sums", bufs=1))
         ctx.enter_context(tc.manual_schedule())
 
-        x_rows = x.rearrange("b (h c) -> (b h) c", h=2)
-        out_view = out.rearrange("b (h gi j) -> b h gi j", h=2, gi=PAIRS)
+        x_loaded, w_loaded, logits_of = {}, {}, {}
+        x_psum, x_ready, w_ready, w_quantised = {}, {}, {}, {}
+        acc, mask_of, planes_of, shared_of = {}, {}, {}, {}
 
-        x_loaded, w_loaded = {}, {}
-        x_ready, w_ready, w_quantised = {}, {}, {}
-        acc, mask_of, shared_of = {}, {}, {}
+        def load_logits(pair):
+            logits = small.tile([P, K_PASS], BF16, name="logits", tag="logits")
+            nc.sync.dma_start(
+                out=logits[:],
+                in_=W_masks[PAIR * pair : PAIR * (pair + 1)]
+                .rearrange("g m s -> (g m s)")
+                .rearrange("(rc f) -> rc f", f=K_PASS),
+            )
+            logits_of[pair] = logits
 
         def load(n):
-            gi, unit = divmod(n, UNITS)
-            first_s = unit * UNIT_K
+            g, v = divmod(n, UNITS)
             x_sb = loads.tile([P, UNIT_K], BF16, name="x_sb", tag="x_sb")
-            nc.sync.dma_start(
-                out=x_sb[:], in_=x_rows[:, gi * S + first_s : gi * S + first_s + UNIT_K]
-            )
+            for sh in range(HALVES):
+                first = g * S + sh * HALF + v * UNIT_K
+                nc.sync.dma_start(out=x_sb[sh:P:2, :], in_=x[:, first : first + UNIT_K])
             x_loaded[n] = x_sb
-            for h in range(2):
-                g = gi + PAIRS * h
+            for sh in range(HALVES):
+                first = sh * HALF + v * UNIT_K
                 w_sb = loads.tile([P, UNIT_K], BF16, name="w_sb", tag="w_sb", bufs=2 * (LOAD_AHEAD + 1))
-                nc.sync.dma_start(out=w_sb[0:P:2, :], in_=W1[g, :, first_s : first_s + UNIT_K])
-                nc.sync.dma_start(out=w_sb[1:P:2, :], in_=W2[g, :, first_s : first_s + UNIT_K])
-                w_loaded[(n, h)] = w_sb
+                nc.sync.dma_start(out=w_sb[0:P:2, :], in_=W1[g, :, first : first + UNIT_K])
+                nc.sync.dma_start(out=w_sb[1:P:2, :], in_=W2[g, :, first : first + UNIT_K])
+                w_loaded[(n, sh)] = w_sb
 
-        logits_bf = const.tile([P, MASK_COLS], BF16, name="logits_bf")
-        nc.sync.dma_start(
-            out=logits_bf[:],
-            in_=W_masks.rearrange("g m s -> (g m s)").rearrange("(r f) -> r f", r=P),
-        )
-        for n in range(LOAD_AHEAD):
-            load(n)
+        load_logits(0)
+        load(0)
 
         ident = const.tile([P, P], F32, name="ident")
         make_identity(nc, ident[:])
-        ln_raw = const.tile([P, 4, G * H], BF16, name="ln_raw")
-        for n, vec in enumerate((ln1_w, ln2_w, ln1_b, ln2_b)):
-            nc.gpsimd.dma_start(
-                out=ln_raw[:, n, :], in_=vec.rearrange("g j -> (g j)").partition_broadcast(P)
+        zero = const.tile([P, PAIR_ROWS], F32, name="zero")
+        nc.vector.memset(zero[:], 0.0)
+        warm = const.tile([P, 1], F32, name="warm")
+        nc.scalar.activation(out=warm[:], in_=zero[:, 0:1], func=FUNC.Exp)
+        exp_scales = const.tile([P, 2], F32, name="exp_scales")
+        for col, value in enumerate((-ALPHA, -1.0)):
+            nc.vector.tensor_scalar(
+                out=exp_scales[:, col : col + 1], in0=zero[:, 0:1], scalar1=0.0, scalar2=value,
+                op0=ALU.mult, op1=ALU.add,
             )
+        norm_power = const.tile([P, 1], F32, name="norm_power")
+        nc.vector.tensor_scalar(
+            out=norm_power[:], in0=zero[:, 0:1], scalar1=0.0, scalar2=-1.0 / ALPHA,
+            op0=ALU.mult, op1=ALU.add,
+        )
+        rsqrt_power = const.tile([P, LN_ROWS], F32, name="rsqrt_power")
+        nc.vector.memset(rsqrt_power[:], -0.5)
+        row_of = const.tile([P, PAIR_ROWS], F32, name="row_of")
+        nc.vector.tensor_reduce(
+            out=row_of[:], in_=ident[:].rearrange("p (r c) -> p r c", c=PASSES), axis=AXIS_X, op=ALU.add
+        )
+        block = const.tile([P, P], F32, name="block")
+        nc.vector.tensor_copy(
+            out=block[:].rearrange("p (r c) -> p r c", c=PASSES),
+            in_=row_of[:].unsqueeze(2).to_broadcast([P, PAIR_ROWS, PASSES]),
+        )
+        other_rows = const.tile([P, P], F32, name="other_rows")
+        nc.vector.tensor_scalar(
+            out=other_rows[:], in0=block[:], scalar1=-1.0, scalar2=2.0**127, op0=ALU.add, op1=ALU.mult
+        )
         unzip = const.tile([P, P], F32, name="unzip")
         nc.vector.tensor_copy(
             out=unzip[:].rearrange("p (h a) -> p h a", h=2),
             in_=ident[:].rearrange("p (a h) -> p h a", h=2),
         )
-        ones = const.tile([P, P], F32, name="ones")
-        nc.vector.memset(ones[:], 1.0)
+        mask_order = const.tile([P, P], F32, name="mask_order")
+        by_pass = ident[:].rearrange("p (g2 m shv cp cc) -> p g2 shv cc m cp", g2=PAIR, m=M, shv=SHV, cp=2)
+        mask_cols = {}
+        col = 0
+        for cp in range(2):
+            for g2 in range(PAIR):
+                for first_m, last_m in ((0, M),) if cp == 0 else ((0, VECTOR_MASKS), (VECTOR_MASKS, M)):
+                    width = SHV * CC * (last_m - first_m)
+                    nc.vector.tensor_copy(
+                        out=mask_order[:, col : col + width].rearrange(
+                            "p (shv cc m) -> p shv cc m", shv=SHV, cc=CC
+                        ),
+                        in_=by_pass[:, g2, :, :, first_m:last_m, cp],
+                    )
+                    mask_cols[(cp, g2, first_m > 0)] = col
+                    col += width
         fold = const.tile([P, P], F32, name="fold")
         for half in range(2):
             nc.vector.tensor_tensor(
-                out=fold[:, half * H : (half + 1) * H],
-                in0=ident[:, 0:H],
-                in1=ident[:, H : 2 * H],
-                op=ALU.add,
+                out=fold[:, half * H : (half + 1) * H], in0=ident[:, 0:H], in1=ident[:, H : 2 * H], op=ALU.add
             )
-        part_max = const.tile([P, P], F32, name="part_max")
-        nc.vector.memset(part_max[:], 0.0)
-        part_sum = const.tile([P, P], F32, name="part_sum")
-        nc.vector.memset(part_sum[:], 0.0)
-        norm_power = const.tile([P, PAIR_ROWS], F32, name="norm_power")
-        nc.vector.tensor_scalar(
-            out=norm_power[:], in0=part_max[:, 0:PAIR_ROWS], scalar1=0.0, scalar2=-1.0 / ALPHA,
-            op0=ALU.mult, op1=ALU.add,
-        )
-        rsqrt_power = const.tile([P, LN_ROWS], F32, name="rsqrt_power")
-        nc.vector.tensor_scalar(
-            out=rsqrt_power[:], in0=part_max[:, 0:LN_ROWS], scalar1=0.0, scalar2=-0.5,
-            op0=ALU.mult, op1=ALU.add,
-        )
+        ln_rows = const.tile([P, 4 * G * H], BF16, name="ln_rows")
+        nc.gpsimd.memset(ln_rows[:], 0.0)
+        ones = const.tile([P, P], BF16, name="ones")
+        nc.gpsimd.memset(ones[:], 1.0)
+        affine = const.tile([P, 2, 2, G, H], F32, name="affine")
+        affine_flat = affine[:].rearrange("p k w g j -> p (k w g j)")
 
-        def transpose_and_group(rows, grouped):
-            words = rows[:].bitcast(F32)
-            grouped_words = grouped[:].bitcast(F32)
-            for half in range(UNIT_PASSES // 2):
+        for n in range(1, LOAD_AHEAD):
+            load(n)
+        for n, vec in enumerate((ln1_w, ln2_w, ln1_b, ln2_b)):
+            nc.sync.dma_start(
+                out=ln_rows[0:1, n * G * H : (n + 1) * G * H],
+                in_=vec.rearrange("g j -> (g j)").unsqueeze(0),
+            )
+
+        def spread_steps():
+            def spread(first):
                 bank = banks.tile([P, BANK], F32, name="bank", tag="bank")
-                for k in range(4):
-                    first = half * BANK + k * P
-                    nc.tensor.transpose(
-                        out=bank[:, k * P : (k + 1) * P],
-                        in_=words[:, first : first + P],
-                        identity=unzip[:],
-                    )
-                nc.scalar.copy(
-                    out=grouped_words[:, half * BANK : (half + 1) * BANK].rearrange(
-                        "p (c col u) -> p c col u", c=2, u=2
-                    ),
-                    in_=bank[:].rearrange("p (c u col) -> p c col u", c=2, u=2),
+                nc.tensor.matmul(
+                    out=bank[:], lhsT=ones[:], rhs=ln_rows[:, first : first + BANK], start=True, stop=True
                 )
+                nc.scalar.copy(out=affine_flat[:, first : first + BANK], in_=bank[:])
 
-        def prepare(n):
-            for h in range(2):
-                w_grouped = stage.tile([P, UNIT_K], BF16, name="w_grouped", tag="w_grouped", bufs=4, align_bytes=64)
-                transpose_and_group(w_loaded[(n, h)], w_grouped)
-                w_ready[(n, h)] = w_grouped
-            x_grouped = stage.tile([P, UNIT_K], BF16, name="x_grouped", tag="x_grouped")
-            transpose_and_group(x_loaded[n], x_grouped)
-            x_ready[n] = x_grouped
+            return [lambda first=first: spread(first) for first in range(0, 4 * G * H, BANK)]
 
-        def quantise(values, tag):
-            codes = quant.tile([P, UNIT_K // PACK], U32, name="codes_" + tag, tag="codes_" + tag, align_bytes=64)
-            scales = quant.tile([P, UNIT_K // PACK], U8, name="scales_" + tag, tag="scales_" + tag, align_bytes=64)
-            nc.vector.quantize_mx(out=codes[:].bitcast(FP8X4), scales=scales[:], in_=values[:])
-            return codes, scales
-
-        logit_words = logits_bf[:].bitcast(F32)
-        logits = const.tile([P, MASK_COLS], F32, name="logits")
-        logits_by_i = logits[:].rearrange("p (r i u e) -> p i r u e", i=ROW_PASSES, u=2, e=2)
-        for i in range(ROW_PASSES):
-            bank = banks.tile([P, BANK], F32, name="bank", tag="bank")
-            for u in range(2):
-                k = 2 * i + u
-                nc.tensor.transpose(
-                    out=bank[:, u * P : (u + 1) * P],
-                    in_=logit_words[:, k * P : (k + 1) * P],
-                    identity=ident[:],
-                )
-            nc.scalar.copy(
-                out=logits_by_i[:, i],
-                in_=bank[:, 0 : 2 * P].bitcast(BF16).rearrange("p (u r e) -> p r u e", u=2, e=2),
-            )
-
-        def entmax_steps(gi):
-            rows = logits[:].rearrange("p (h gi m k) -> p h gi m k", h=2, gi=PAIRS, m=M)[:, :, gi]
+        def entmax_steps(pair):
             kept = {}
 
-            def partition_maxima():
-                nc.vector.tensor_reduce(
-                    out=part_max[:, 0:PAIR_ROWS].rearrange("p (h m) -> p h m", h=2),
-                    in_=rows, axis=AXIS_X, op=ALU.max,
-                )
-                turned = banks.tile([P, BANK], F32, name="turned", tag="bank")
-                nc.tensor.transpose(out=turned[:, 0:P], in_=part_max[:], identity=ident[:])
-                kept["turned"] = turned
-
-            def row_maxima():
-                row_max = small.tile([P, 1], F32, name="row_max", tag="row_max")
-                nc.vector.tensor_reduce(out=row_max[:], in_=kept["turned"][:, 0:P], axis=AXIS_X, op=ALU.max)
-                max_bank = banks.tile([P, BANK], F32, name="max_bank", tag="bank")
+            def maxima():
+                logits = logits_of[pair]
+                pass_max = small.tile([P, 1], F32, name="pass_max", tag="pass_max")
+                nc.vector.tensor_reduce(out=pass_max[:], in_=logits[:], axis=AXIS_X, op=ALU.max)
+                bank = banks.tile([P, BANK], F32, name="bank", tag="bank")
                 nc.tensor.matmul(
-                    out=max_bank[:, 0:P], lhsT=row_max[:, 0:1].to_broadcast([P, P]), rhs=ident[:],
+                    out=bank[:, 0:P], lhsT=pass_max[:, 0:1].to_broadcast([P, P]), rhs=ident[:],
                     start=True, stop=True,
                 )
-                kept["max_bank"] = max_bank
+                kept["maxima"] = bank
 
             def exponentials():
-                shifted = small.tile([P, PAIR_ROWS * PER_ROW], F32, name="shifted", tag="shifted")
+                own = small.tile([P, P], F32, name="own", tag="own")
+                nc.vector.tensor_tensor(out=own[:], in0=kept["maxima"][:, 0:P], in1=other_rows[:], op=ALU.add)
+                row_max = small.tile([P, 1], F32, name="row_max", tag="row_max")
+                nc.vector.tensor_reduce(out=row_max[:], in_=own[:], axis=AXIS_X, op=ALU.max)
+                biases = small.tile([P, 2], F32, name="biases", tag="biases")
                 nc.vector.tensor_tensor(
-                    out=shifted[:].rearrange("p (h m k) -> p h m k", h=2, m=M),
-                    in0=rows,
-                    in1=kept["max_bank"][:, 0:PAIR_ROWS]
-                    .rearrange("p (h m) -> p h m", h=2)
-                    .unsqueeze(3)
-                    .to_broadcast([P, 2, M, PER_ROW]),
-                    op=ALU.subtract,
+                    out=biases[:], in0=row_max[:].to_broadcast([P, 2]), in1=exp_scales[:], op=ALU.mult
                 )
-                e_alpha = small.tile([P, PAIR_ROWS * PER_ROW], F32, name="e_alpha", tag="e_alpha")
-                nc.scalar.activation(out=e_alpha[:], in_=shifted[:], func=FUNC.Exp, scale=ALPHA)
-                e = small.tile([P, PAIR_ROWS * PER_ROW], F32, name="e", tag="e")
-                nc.scalar.activation(out=e[:], in_=shifted[:], func=FUNC.Exp)
-                kept["e_alpha"], kept["e"] = e_alpha, e
+                powers = small.tile([P, K_PASS], F32, name="powers", tag="powers")
+                pass_sum = small.tile([P, 1], F32, name="pass_sum", tag="pass_sum")
+                nc.scalar.activation(
+                    out=powers[:], in_=logits_of[pair][:], func=FUNC.Exp, scale=ALPHA, bias=biases[:, 0:1],
+                    accum_out=pass_sum[:],
+                )
+                e = small.tile([P, K_PASS], F32, name="e", tag="e")
+                nc.scalar.activation(
+                    out=e[:], in_=logits_of[pair][:], func=FUNC.Exp, bias=biases[:, 1:2]
+                )
+                bank = banks.tile([P, BANK], F32, name="bank", tag="bank")
+                nc.tensor.matmul(out=bank[:, 0:1], lhsT=block[:], rhs=pass_sum[:], start=True, stop=True)
+                kept["e"], kept["sums"] = e, bank
 
-            def norms():
-                nc.vector.tensor_reduce(
-                    out=part_sum[:, 0:PAIR_ROWS],
-                    in_=kept["e_alpha"][:].rearrange("p (row k) -> p row k", k=PER_ROW),
-                    axis=AXIS_X, op=ALU.add,
+            def scale():
+                padded = small.tile([P, 1], F32, name="padded", tag="padded")
+                nc.vector.tensor_scalar(
+                    out=padded[:], in0=kept["sums"][:, 0:1], scalar1=EPS, scalar2=None, op0=ALU.add
                 )
-                sum_bank = banks.tile([P, BANK], F32, name="sum_bank", tag="bank")
-                nc.tensor.matmul(out=sum_bank[:, 0:P], lhsT=ones[:], rhs=part_sum[:], start=True, stop=True)
-                padded = small.tile([P, PAIR_ROWS], F32, name="padded", tag="padded")
-                nc.scalar.activation(out=padded[:], in_=sum_bank[:, 0:PAIR_ROWS], func=FUNC.Copy, bias=EPS)
-                inv_norm = small.tile([P, PAIR_ROWS], F32, name="inv_norm", tag="inv_norm")
+                inv_norm = small.tile([P, 1], F32, name="inv_norm", tag="inv_norm")
                 nc.gpsimd.tensor_tensor(out=inv_norm[:], in0=padded[:], in1=norm_power[:], op=ALU.pow)
-                kept["inv_norm"] = inv_norm
+                by_row = small.tile([P, K_PASS], F32, name="by_row", tag="by_row")
+                nc.gpsimd.tensor_scalar(
+                    out=by_row[:], in0=kept["e"][:], scalar1=inv_norm[:, 0:1], scalar2=0.0,
+                    op0=ALU.mult, op1=ALU.add,
+                )
+                kept["by_row"] = by_row
 
-            def scale_masks():
-                mask = small.tile([P, 4, PASSES, 2, PACK], F32, name="mask", tag="mask")
-                e_view = kept["e"][:].rearrange("p (a m2 c t) -> p a m2 c t", m2=2, c=PASSES, t=PACK)
-                inv_view = kept["inv_norm"][:].rearrange("p (a m2) -> p a m2", m2=2)
-                for m2 in range(2):
-                    nc.vector.tensor_tensor(
-                        out=mask[:, :, :, m2, :],
-                        in0=e_view[:, :, m2],
-                        in1=inv_view[:, :, m2].unsqueeze(2).unsqueeze(3).to_broadcast([P, 4, PASSES, PACK]),
-                        op=ALU.mult,
-                    )
-                mask_of[gi] = mask
-
-            return [partition_maxima, row_maxima, exponentials, norms, scale_masks]
-
-        def scalar_multiply(n, h):
-            gi, unit = divmod(n, UNITS)
-            x_view = x_ready[n][:].rearrange("p (c h b t) -> p c h b t", c=UNIT_PASSES, h=2, t=PACK)
-            planes = stage.tile([P, UNIT_PASSES, PACK, B], BF16, name="planes", tag="planes", bufs=2)
-            for c in range(UNIT_PASSES):
+            def turn():
+                bank = banks.tile([P, P, PACK], F32, name="mask_bank", tag="bank")
                 for t in range(PACK):
-                    nc.scalar.activation(
-                        out=planes[:, c, t, :],
-                        in_=x_view[:, c, h, :, t],
-                        func=FUNC.Copy,
-                        scale=mask_of[gi][:, 2 * h + 1, unit * UNIT_PASSES + c, 1, t : t + 1],
+                    u, e = divmod(t, 2)
+                    nc.tensor.transpose(
+                        out=bank[:, :, t],
+                        in_=kept["by_row"][:, 2 * P * u + e : 2 * P * (u + 1) : 2],
+                        identity=mask_order[:],
                     )
-            shared = stage.tile([P, UNIT_K], BF16, name="shared", tag="shared", bufs=6, align_bytes=64)
-            nc.scalar.copy(
-                out=shared[:].rearrange("p (c m b t) -> p c m b t", c=UNIT_PASSES, m=2, t=PACK)[:, :, 1],
-                in_=planes[:].rearrange("p c t b -> p c b t"),
-            )
-            shared_of[(n, h)] = shared
+                mask = small.tile([P, P, PACK], F32, name="mask", tag="mask")
+                nc.scalar.copy(out=mask[:], in_=bank[:])
+                for g2 in range(PAIR):
+                    mask_of[PAIR * pair + g2] = mask
 
-        def multiply(n, h, mt):
-            gi, unit = divmod(n, UNITS)
-            x_view = x_ready[n][:].rearrange("p (c h b t) -> p c h b t", c=UNIT_PASSES, h=2, t=PACK)
-            if mt == 1:
-                weighted, masks_here = shared_of[(n, h)], 1
+            return [maxima, exponentials, scale, turn]
+
+        def masks(n, cp, sh, by_scalar):
+            g, v = divmod(n, UNITS)
+            masks_here = M if cp == 0 else SCALAR_MASKS if by_scalar else VECTOR_MASKS
+            first = mask_cols[(cp, g % PAIR, by_scalar)] + (sh * UNITS + v) * CC * masks_here
+            return mask_of[g][:, first : first + CC * masks_here, :].rearrange(
+                "p (cc m) t -> p cc m t", cc=CC
+            )
+
+        def turn_words(source, cp, bank_view, order):
+            words = source[:].bitcast(F32)
+            for cc in range(CC):
+                for u in range(2):
+                    first = ((cp * CC + cc) * 2 + u) * P
+                    nc.tensor.transpose(
+                        out=bank_view[:, cc, u, :], in_=words[:, first : first + P], identity=order[:]
+                    )
+
+        def turn_and_group(source, cp, grouped, order):
+            bank = banks.tile([P, CC, 2, P], F32, name="turned", tag="bank")
+            turn_words(source, cp, bank[:], order)
+            nc.scalar.copy(
+                out=grouped.bitcast(F32).rearrange("p (cc col u) -> p cc col u", cc=CC, u=2),
+                in_=bank[:].rearrange("p cc u col -> p cc col u"),
+            )
+
+        def prepare_w(n, sh, cp):
+            if sh == 0 and cp == 0:
+                w_grouped = stage.tile([P, HALVES * 2, CC * P * PACK], BF16, name="w_grouped", tag="w_grouped", align_bytes=64)
+                w_ready[n] = w_grouped
+            turn_and_group(w_loaded[(n, sh)], cp, w_ready[n][:, sh * 2 + cp, :], ident)
+
+        def prepare_x_scalar(n):
+            x_sb = stage.tile([P, CC * P * PACK], BF16, name="x_grouped", tag="x_grouped")
+            turn_and_group(x_loaded[n], 1, x_sb[:], unzip)
+            x_ready[n] = x_sb[:].rearrange("p (cc sh b t) -> p cc sh b t", cc=CC, sh=HALVES, t=PACK)
+
+        def prepare_x_vector(n):
+            bank = x_banks.tile([P, CC, P, 2], F32, name="x_bank", tag="x_bank")
+            turn_words(x_loaded[n], 0, bank[:].rearrange("p cc col u -> p cc u col"), unzip)
+            x_psum[n] = bank[:].bitcast(BF16).rearrange("p cc (sh b) t -> p cc sh b t", sh=HALVES)
+
+        def scalar_multiply(n, sh):
+            mask = masks(n, 1, sh, True)
+            planes = stage.tile([P, CC, SCALAR_MASKS, PACK, B], BF16, name="planes", tag="planes")
+            for cc in range(CC):
+                for m in range(SCALAR_MASKS):
+                    for t in range(PACK):
+                        nc.scalar.activation(
+                            out=planes[:, cc, m, t, :],
+                            in_=x_ready[n][:, cc, sh, :, t],
+                            func=FUNC.Copy,
+                            scale=mask[:, cc, m, t : t + 1],
+                        )
+            planes_of[(n, sh)] = planes
+
+        def scalar_regroup(n, sh):
+            shared = stage.tile([P, TILE], BF16, name="shared", tag="shared", bufs=5, align_bytes=64)
+            nc.scalar.copy(
+                out=shared[:].rearrange("p (cc m b t) -> p cc m b t", cc=CC, m=M, t=PACK)[:, :, VECTOR_MASKS:M],
+                in_=planes_of[(n, sh)][:].rearrange("p cc m t b -> p cc m b t"),
+            )
+            shared_of[(n, sh)] = shared
+
+        def prepare(n, step):
+            if step == 0:
+                prepare_x_scalar(n)
+                prepare_w(n, 0, 0)
+            elif step == 1:
+                prepare_w(n, 0, 1)
+                prepare_x_vector(n)
+                scalar_multiply(n, 0)
+            elif step == 2:
+                prepare_w(n, 1, 0)
+                prepare_w(n, 1, 1)
+                scalar_regroup(n, 0)
             else:
-                weighted = stage.tile([P, UNIT_K], BF16, name="weighted", tag="weighted", align_bytes=64)
-                masks_here = 2
-            shape = [P, UNIT_PASSES, masks_here, B, PACK]
+                scalar_multiply(n, 1)
+
+        def quantise(values, tag):
+            width = values.shape[1] // PACK
+            codes = quant.tile([P, width], U32, name="codes_" + tag, tag="codes_" + tag, align_bytes=64)
+            scales = quant.tile([P, width], U8, name="scales_" + tag, tag="scales_" + tag, align_bytes=64)
+            nc.vector.quantize_mx(out=codes[:].bitcast(FP8X4), scales=scales[:], in_=values)
+            return codes, scales
+
+        def quantise_w(n):
+            w_quantised[n] = quantise(w_ready[n][:].rearrange("p c f -> p (c f)"), "w")
+
+        def multiply(n, cp, sh):
+            if cp == 0:
+                weighted = stage.tile([P, TILE], BF16, name="weighted", tag="weighted", align_bytes=64)
+                masks_here, x_view = M, x_psum[n]
+            else:
+                weighted, masks_here, x_view = shared_of[(n, sh)], VECTOR_MASKS, x_ready[n]
+            shape = [P, CC, masks_here, B, PACK]
             nc.vector.tensor_tensor(
-                out=weighted[:].rearrange("p (c m b t) -> p c m b t", c=UNIT_PASSES, m=2, t=PACK)[
-                    :, :, 0:masks_here
-                ],
-                in0=x_view[:, :, h].unsqueeze(2).to_broadcast(shape),
-                in1=mask_of[gi][:, 2 * h + mt, unit * UNIT_PASSES : (unit + 1) * UNIT_PASSES, 0:masks_here]
-                .unsqueeze(3)
-                .to_broadcast(shape),
+                out=weighted[:].rearrange("p (cc m b t) -> p cc m b t", cc=CC, m=M, t=PACK)[:, :, 0:masks_here],
+                in0=x_view[:, :, sh].unsqueeze(2).to_broadcast(shape),
+                in1=masks(n, cp, sh, False).unsqueeze(3).to_broadcast(shape),
                 op=ALU.mult,
             )
             return weighted
 
-        def contract(n, h, mt, weighted):
-            unit = n % UNITS
-            if unit == 0:
-                acc_tile = sums.tile([P, P], F32, name="acc%d%d" % (h, mt), tag="acc%d%d" % (h, mt))
-                acc[(h, mt)] = acc_tile
-            a_codes, a_scales = quantise(weighted, "a")
-            w_codes, w_scales = w_quantised[(n, h)]
-            for c in range(UNIT_PASSES):
-                cols = slice(c * P, (c + 1) * P)
-                nc.tensor.matmul_mx(
-                    out=acc[(h, mt)][:],
-                    lhsT=a_codes[:, cols].bitcast(FP8X4),
-                    lhsT_scale=a_scales[:, cols],
-                    rhs=w_codes[:, cols].bitcast(FP8X4),
-                    rhs_scale=w_scales[:, cols],
-                    start=(unit == 0 and c == 0),
-                    stop=(unit == UNITS - 1 and c == UNIT_PASSES - 1),
-                )
-
-        gain = const.tile([P, G, 2, H], F32, name="gain")
-        shift = const.tile([P, G, 2, H], F32, name="shift")
-
-        def layer_norm_steps(gi):
-            scratch = small.tile([P, H], F32, name="scratch", tag="scratch")
-            row_sum = small.tile([P, LN_ROWS], F32, name="row_sum", tag="row_sum")
-            neg_mean = small.tile([P, LN_ROWS], F32, name="neg_mean", tag="neg_mean")
-            sq_sum = small.tile([P, LN_ROWS], F32, name="sq_sum", tag="sq_sum")
-            var_eps = small.tile([P, LN_ROWS], F32, name="var_eps", tag="var_eps")
-            rstd = small.tile([P, LN_ROWS], F32, name="rstd", tag="rstd")
-            raw = small.tile([P, LN_ROWS, H], F32, name="raw", tag="raw")
-            centred = small.tile([P, LN_ROWS, H], F32, name="centred", tag="centred")
-            normed = small.tile([P, LN_ROWS, H], F32, name="normed", tag="normed")
-            for h in range(2):
+        def contract(n, cp, sh, weighted):
+            v = n % UNITS
+            first = (v, cp, sh) == (0, 0, 0)
+            last = (v, cp, sh) == (UNITS - 1, 1, HALVES - 1)
+            if first:
                 for mt in range(2):
-                    first = 4 * h + 2 * mt
-                    nc.scalar.copy(
-                        out=raw[:, first : first + 2, :].rearrange("p w j -> p (w j)"), in_=acc[(h, mt)][:]
+                    acc_tile = sums.tile([P, P], F32, name="acc%d" % mt, tag="acc%d" % mt)
+                    acc[mt] = acc_tile
+            a_codes, a_scales = quantise(weighted[:], "a")
+            w_codes, w_scales = w_quantised[n]
+            for cc in range(CC):
+                for mt in range(2):
+                    a_cols = slice((cc * 2 + mt) * P, (cc * 2 + mt + 1) * P)
+                    w_pass = (sh * 2 + cp) * CC + cc
+                    w_cols = slice(w_pass * P, (w_pass + 1) * P)
+                    nc.tensor.matmul_mx(
+                        out=acc[mt][:],
+                        lhsT=a_codes[:, a_cols].bitcast(FP8X4),
+                        lhsT_scale=a_scales[:, a_cols],
+                        rhs=w_codes[:, w_cols].bitcast(FP8X4),
+                        rhs_scale=w_scales[:, w_cols],
+                        start=(first and cc == 0),
+                        stop=(last and cc == CC - 1),
                     )
-            for i in range(LN_ROWS):
-                nc.scalar.activation(
-                    out=scratch[:], in_=raw[:, i, :], func=FUNC.Identity, accum_out=row_sum[:, i : i + 1]
+
+        results = {}
+
+        def layer_norm_steps(g):
+            raw = small.tile([P, 2, H, 2], F32, name="raw", tag="raw")
+            for mt in range(2):
+                nc.scalar.copy(out=raw[:, mt].rearrange("p j w -> p (j w)"), in_=acc[mt][:])
+            stats = small.tile([P, LN_ROWS, 3], F32, name="stats", tag="stats")
+            rstd = small.tile([P, LN_ROWS], F32, name="rstd", tag="rstd")
+            normed = small.tile([P, 2, 2, H], F32, name="normed", tag="normed")
+            half_tanh = small.tile([P, 2, H], F32, name="half_tanh", tag="half_tanh")
+            half_relu = small.tile([P, 2, H], F32, name="half_relu", tag="half_relu")
+            gated = small.tile([P, 2, H], F32, name="gated", tag="gated")
+
+            def statistics():
+                for mt in range(2):
+                    nc.vector.bn_stats(
+                        out=stats[:, 2 * mt : 2 * mt + 2, :].rearrange("p w k -> p (w k)"),
+                        in_=raw[:, mt].rearrange("p j w -> p (j w)"),
+                    )
+                var_eps = small.tile([P, LN_ROWS], F32, name="var_eps", tag="var_eps")
+                nc.gpsimd.tensor_scalar(
+                    out=var_eps[:], in0=stats[:, :, 2], scalar1=1.0 / H, scalar2=EPS, op0=ALU.mult, op1=ALU.add
                 )
-            nc.scalar.mul(out=neg_mean[:], in_=row_sum[:], mul=-1.0 / H)
-            for i in range(LN_ROWS):
-                nc.scalar.activation(
-                    out=centred[:, i, :], in_=raw[:, i, :], func=FUNC.Identity, bias=neg_mean[:, i : i + 1]
-                )
-            for i in range(LN_ROWS):
-                nc.scalar.activation(
-                    out=scratch[:], in_=centred[:, i, :], func=FUNC.Square, accum_out=sq_sum[:, i : i + 1]
-                )
-            nc.scalar.activation(out=var_eps[:], in_=sq_sum[:], func=FUNC.Copy, scale=1.0 / H, bias=EPS)
-            nc.gpsimd.tensor_tensor(out=rstd[:], in0=var_eps[:], in1=rsqrt_power[:], op=ALU.pow)
+                nc.gpsimd.tensor_tensor(out=rstd[:], in0=var_eps[:], in1=rsqrt_power[:], op=ALU.pow)
 
-            normed_view = normed[:].rearrange("p (h mt w) j -> p h mt (w j)", h=2, mt=2)
-            by_w = normed[:].rearrange("p (hm w) j -> p hm w j", w=2)
-            half_tanh = small.tile([P, 4, H], F32, name="half_tanh", tag="half_tanh")
-            half_relu = small.tile([P, 4, H], F32, name="half_relu", tag="half_relu")
-            gated = small.tile([P, 2, 2, H], F32, name="gated", tag="gated")
+            def normalise():
+                for mt in range(2):
+                    for w in range(2):
+                        i = 2 * mt + w
+                        nc.vector.tensor_scalar(
+                            out=normed[:, mt, w, :], in0=raw[:, mt, :, w],
+                            scalar1=stats[:, i, 1:2], scalar2=rstd[:, i : i + 1],
+                            op0=ALU.subtract, op1=ALU.mult,
+                        )
+                for k, op in enumerate((ALU.mult, ALU.add)):
+                    nc.gpsimd.tensor_tensor(
+                        out=normed[:], in0=normed[:],
+                        in1=affine[:, k, :, g, :].unsqueeze(1).to_broadcast([P, 2, 2, H]), op=op,
+                    )
 
-            def divide():
-                for i in range(LN_ROWS):
-                    nc.scalar.mul(out=normed[:, i, :], in_=centred[:, i, :], mul=rstd[:, i : i + 1])
-
-            def affine(table, op):
-                nc.vector.tensor_tensor(
-                    out=normed_view,
-                    in0=normed_view,
-                    in1=table[:].rearrange("p g w j -> p g (w j)")[:, gi:G:PAIRS, :]
-                    .unsqueeze(2)
-                    .to_broadcast([P, 2, 2, 2 * H]),
-                    op=op,
-                )
-
-            def apply_gain():
-                affine(gain, ALU.mult)
-
-            def apply_shift():
-                affine(shift, ALU.add)
-                nc.scalar.activation(out=half_tanh[:], in_=by_w[:, :, 0, :], func=FUNC.Tanh, scale=0.5)
-                nc.scalar.activation(out=half_relu[:], in_=by_w[:, :, 1, :], func=FUNC.Relu, scale=0.5)
+            def activate():
+                nc.scalar.activation(out=half_tanh[:], in_=normed[:, :, 0, :], func=FUNC.Tanh, scale=0.5)
+                nc.scalar.activation(out=half_relu[:], in_=normed[:, :, 1, :], func=FUNC.Relu, scale=0.5)
 
             def gate():
                 nc.vector.scalar_tensor_tensor(
-                    out=gated[:].rearrange("p h mt j -> p (h mt) j"),
-                    in0=half_tanh[:], scalar=1.0, in1=half_relu[:], op0=ALU.add, op1=ALU.mult,
+                    out=gated[:], in0=half_tanh[:], scalar=1.0, in1=half_relu[:], op0=ALU.add, op1=ALU.mult
                 )
+                bank = banks.tile([P, BANK], F32, name="bank", tag="bank")
+                for mt in range(2):
+                    nc.tensor.matmul(
+                        out=bank[:, 0:H], lhsT=fold[:], rhs=gated[:, mt, :], start=(mt == 0), stop=(mt == 1)
+                    )
+                result = small.tile([P, H], F32, name="result", tag="result")
+                nc.scalar.copy(out=result[0:B], in_=bank[0:B, 0:H])
+                results[g] = result
 
-            def add_masks_and_store():
-                two_masks = small.tile([P, 2, H], F32, name="two_masks", tag="two_masks")
-                nc.vector.tensor_tensor(
-                    out=two_masks[:], in0=gated[:, :, 0, :], in1=gated[:, :, 1, :], op=ALU.add
-                )
-                out_bank = banks.tile([P, BANK], F32, name="out_bank", tag="bank")
-                nc.tensor.matmul(
-                    out=out_bank[:, 0:P], lhsT=fold[:], rhs=two_masks[:].rearrange("p h j -> p (h j)"),
-                    start=True, stop=True,
-                )
-                result = small.tile([P, 2, H], F32, name="result", tag="result")
-                nc.scalar.copy(out=result[0:B].rearrange("b h j -> b (h j)"), in_=out_bank[0:B, 0:P])
-                nc.sync.dma_start(out=out_view[:, :, gi, :], in_=result[0:B])
+            return [statistics, normalise, activate, gate]
 
-            return [divide, apply_gain, apply_shift, gate, add_masks_and_store]
+        def store(g):
+            nc.sync.dma_start(out=out[:, g * H : (g + 1) * H], in_=results[g][0:B])
 
-        prepare(0)
         first_masks = entmax_steps(0)
-        for step in first_masks[0:3]:
-            step()
-        for h in range(2):
-            w_quantised[(0, h)] = quantise(w_ready[(0, h)], "w")
-        for step in first_masks[3:]:
-            step()
-        nc.scalar.copy(out=gain[:], in_=ln_raw[:, 0:2, :].rearrange("p w (g j) -> p g w j", j=H))
-        nc.scalar.copy(out=shift[:], in_=ln_raw[:, 2:4, :].rearrange("p w (g j) -> p g w j", j=H))
-        for h in range(2):
-            scalar_multiply(0, h)
+        first_masks[0]()
+        prepare_w(0, 0, 0)
+        first_masks[1]()
+        prepare_x_scalar(0)
+        prepare_w(0, 0, 1)
+        first_masks[2]()
+        prepare_w(0, 1, 0)
+        prepare_x_vector(0)
+        prepare_w(0, 1, 1)
+        quantise_w(0)
+        first_masks[3]()
+        scalar_multiply(0, 0)
+        scalar_regroup(0, 0)
+        scalar_multiply(0, 1)
 
-        steps = []
+        steps = spread_steps()
         waiting = None
         for n in range(N_UNITS):
-            gi, unit = divmod(n, UNITS)
+            g, v = divmod(n, UNITS)
             if n + LOAD_AHEAD < N_UNITS:
                 load(n + LOAD_AHEAD)
-            if unit == 0 and gi + 1 < PAIRS:
-                steps.extend(entmax_steps(gi + 1))
-            if n + 1 < N_UNITS:
-                prepare(n + 1)
-            for h in range(2):
-                for mt in range(2):
-                    weighted = multiply(n, h, mt)
-                    if waiting is not None:
-                        contract(*waiting)
-                        if unit == 0 and (h, mt) == (0, 0):
-                            steps.extend(layer_norm_steps(gi - 1))
-                    waiting = (n, h, mt, weighted)
-                    if steps:
-                        steps[0]()
-                        steps = steps[1:]
+            if n % (PAIR * UNITS) == 0 and g + PAIR < G:
+                load_logits(g // PAIR + 1)
+            if n % (PAIR * UNITS) == 1 and g + PAIR < G:
+                steps.extend(entmax_steps(g // PAIR + 1))
+            if v == UNITS - 1 and g > 0:
+                steps.append(lambda done=g - 1: store(done))
+            for k in range(4):
+                cp, sh = divmod(k, HALVES)
+                weighted = multiply(n, cp, sh)
+                if k == 0:
+                    scalar_regroup(n, 1)
                 if n + 1 < N_UNITS:
-                    w_quantised[(n + 1, h)] = quantise(w_ready[(n + 1, h)], "w")
-                    scalar_multiply(n + 1, h)
+                    prepare(n + 1, k)
+                if waiting is not None:
+                    contract(*waiting)
+                    if k == 0 and v == 0:
+                        steps.extend(layer_norm_steps(g - 1))
+                waiting = (n, cp, sh, weighted)
+                if steps:
+                    steps[0]()
+                    steps = steps[1:]
+            if n + 1 < N_UNITS:
+                quantise_w(n + 1)
         contract(*waiting)
-        for step in layer_norm_steps(PAIRS - 1):
+        steps.extend(layer_norm_steps(G - 1))
+        for step in steps:
             step()
+        store(G - 1)

@@ -213,10 +213,7 @@ def tile_dynamicfeaturegroupinglayer_k_kernel(
                 inv_norm = small.tile([P, 1], F32, name="inv_norm", tag="inv_norm")
                 nc.gpsimd.tensor_tensor(out=inv_norm[:], in0=padded[:], in1=norm_power[:], op=ALU.pow)
                 by_row = small.tile([P, K_PASS], F32, name="by_row", tag="by_row")
-                nc.gpsimd.tensor_scalar(
-                    out=by_row[:], in0=kept["e"][:], scalar1=inv_norm[:, 0:1], scalar2=0.0,
-                    op0=ALU.mult, op1=ALU.add,
-                )
+                nc.scalar.activation(out=by_row[:], in_=kept["e"][:], func=FUNC.Copy, scale=inv_norm[:, 0:1])
                 kept["by_row"] = by_row
 
             def turn():
@@ -391,17 +388,17 @@ def tile_dynamicfeaturegroupinglayer_k_kernel(
             def normalise():
                 for mt in range(2):
                     for w in range(2):
-                        i = 2 * mt + w
-                        nc.vector.tensor_scalar(
-                            out=normed[:, mt, w, :], in0=raw[:, mt, :, w],
-                            scalar1=stats[:, i, 1:2], scalar2=rstd[:, i : i + 1],
-                            op0=ALU.subtract, op1=ALU.mult,
+                        nc.vector.scalar_tensor_tensor(
+                            out=normed[:, mt, w, :], in0=raw[:, mt, :, w], scalar=stats[:, 2 * mt + w, 1:2],
+                            in1=affine[:, 0, w, g, :], op0=ALU.subtract, op1=ALU.mult,
                         )
-                for k, op in enumerate((ALU.mult, ALU.add)):
-                    nc.gpsimd.tensor_tensor(
-                        out=normed[:], in0=normed[:],
-                        in1=affine[:, k, :, g, :].unsqueeze(1).to_broadcast([P, 2, 2, H]), op=op,
-                    )
+                for mt in range(2):
+                    for w in range(2):
+                        i = 2 * mt + w
+                        nc.vector.scalar_tensor_tensor(
+                            out=normed[:, mt, w, :], in0=normed[:, mt, w, :], scalar=rstd[:, i : i + 1],
+                            in1=affine[:, 1, w, g, :], op0=ALU.mult, op1=ALU.add,
+                        )
 
             def activate():
                 nc.scalar.activation(out=half_tanh[:], in_=normed[:, :, 0, :], func=FUNC.Tanh, scale=0.5)

@@ -31,8 +31,8 @@ PASSES = S // K_PASS
 SHV = HALVES * UNITS
 CC = 2
 TILE = CC * M * B * PACK
-SCALAR_MASKS = 2
-VECTOR_MASKS = M - SCALAR_MASKS
+SHARES = ((0, 1), (1, 2), (2, M))
+BY_VECTOR, BY_GPSIMD, BY_SCALAR = range(3)
 LOAD_AHEAD = 3
 PAIR = 2
 PAIR_ROWS = PAIR * M
@@ -123,21 +123,26 @@ def tile_dynamicfeaturegroupinglayer_k_kernel(
             in_=ident[:].rearrange("p (a h) -> p h a", h=2),
         )
         mask_order = const.tile([P, P], F32, name="mask_order")
-        by_pass = ident[:].rearrange("p (g2 m shv cp cc) -> p g2 shv cc m cp", g2=PAIR, m=M, shv=SHV, cp=2)
+        by_pass = ident[:].rearrange(
+            "p (g2 m shv cp cc) -> p g2 shv cc m cp", g2=PAIR, m=M, shv=SHV, cp=2
+        )
         mask_cols = {}
-        col = 0
-        for cp in range(2):
-            for g2 in range(PAIR):
-                for first_m, last_m in ((0, M),) if cp == 0 else ((0, VECTOR_MASKS), (VECTOR_MASKS, M)):
-                    width = SHV * CC * (last_m - first_m)
-                    nc.vector.tensor_copy(
-                        out=mask_order[:, col : col + width].rearrange(
-                            "p (shv cc m) -> p shv cc m", shv=SHV, cc=CC
-                        ),
-                        in_=by_pass[:, g2, :, :, first_m:last_m, cp],
-                    )
-                    mask_cols[(cp, g2, first_m > 0)] = col
-                    col += width
+
+        def order_masks():
+            col = 0
+            for cp in range(2):
+                for g2 in range(PAIR):
+                    for engine, (first_m, last_m) in enumerate(SHARES if cp == 1 else ((0, M),)):
+                        width = SHV * CC * (last_m - first_m)
+                        nc.vector.tensor_copy(
+                            out=mask_order[:, col : col + width].rearrange(
+                                "p (shv cc m) -> p shv cc m", shv=SHV, cc=CC
+                            ),
+                            in_=by_pass[:, g2, :, :, first_m:last_m, cp],
+                        )
+                        mask_cols[(cp, g2, engine)] = col
+                        col += width
+
         fold = const.tile([P, P], F32, name="fold")
         for half in range(2):
             nc.vector.tensor_tensor(
@@ -232,11 +237,12 @@ def tile_dynamicfeaturegroupinglayer_k_kernel(
 
             return [maxima, exponentials, scale, turn]
 
-        def masks(n, cp, sh, by_scalar):
+        def masks(n, cp, sh, engine):
             g, v = divmod(n, UNITS)
-            masks_here = M if cp == 0 else SCALAR_MASKS if by_scalar else VECTOR_MASKS
-            first = mask_cols[(cp, g % PAIR, by_scalar)] + (sh * UNITS + v) * CC * masks_here
-            return mask_of[g][:, first : first + CC * masks_here, :].rearrange(
+            first_m, last_m = SHARES[engine] if cp == 1 else (0, M)
+            width = CC * (last_m - first_m)
+            first = mask_cols[(cp, g % PAIR, engine)] + (sh * UNITS + v) * width
+            return mask_of[g][:, first : first + width, :].rearrange(
                 "p (cc m) t -> p cc m t", cc=CC
             )
 
@@ -274,10 +280,11 @@ def tile_dynamicfeaturegroupinglayer_k_kernel(
             x_psum[n] = bank[:].bitcast(BF16).rearrange("p cc (sh b) t -> p cc sh b t", sh=HALVES)
 
         def scalar_multiply(n, sh):
-            mask = masks(n, 1, sh, True)
-            planes = stage.tile([P, CC, SCALAR_MASKS, PACK, B], BF16, name="planes", tag="planes")
+            mask = masks(n, 1, sh, BY_SCALAR)
+            masks_here = M - SHARES[BY_SCALAR][0]
+            planes = stage.tile([P, CC, masks_here, PACK, B], BF16, name="planes", tag="planes")
             for cc in range(CC):
-                for m in range(SCALAR_MASKS):
+                for m in range(masks_here):
                     for t in range(PACK):
                         nc.scalar.activation(
                             out=planes[:, cc, m, t, :],
@@ -288,26 +295,41 @@ def tile_dynamicfeaturegroupinglayer_k_kernel(
             planes_of[(n, sh)] = planes
 
         def scalar_regroup(n, sh):
-            shared = stage.tile([P, TILE], BF16, name="shared", tag="shared", bufs=5, align_bytes=64)
             nc.scalar.copy(
-                out=shared[:].rearrange("p (cc m b t) -> p cc m b t", cc=CC, m=M, t=PACK)[:, :, VECTOR_MASKS:M],
+                out=by_mask(shared_of[(n, sh)])[:, :, slice(*SHARES[BY_SCALAR])],
                 in_=planes_of[(n, sh)][:].rearrange("p cc m t b -> p cc m b t"),
             )
+
+        def by_mask(tile):
+            return tile[:].rearrange("p (cc m b t) -> p cc m b t", cc=CC, m=M, t=PACK)
+
+        def gpsimd_multiply(n, sh):
+            shared = stage.tile([P, TILE], BF16, name="shared", tag="shared", bufs=3, align_bytes=64)
             shared_of[(n, sh)] = shared
+            first_m, last_m = SHARES[BY_GPSIMD]
+            shape = [P, CC, last_m - first_m, B, PACK]
+            nc.gpsimd.tensor_tensor(
+                out=by_mask(shared)[:, :, first_m:last_m],
+                in0=x_ready[n][:, :, sh].unsqueeze(2).to_broadcast(shape),
+                in1=masks(n, 1, sh, BY_GPSIMD).unsqueeze(3).to_broadcast(shape),
+                op=ALU.mult,
+            )
 
         def prepare(n, step):
             if step == 0:
                 prepare_x_scalar(n)
                 prepare_w(n, 0, 0)
             elif step == 1:
+                gpsimd_multiply(n, 0)
                 prepare_w(n, 0, 1)
                 prepare_x_vector(n)
-                scalar_multiply(n, 0)
-            elif step == 2:
                 prepare_w(n, 1, 0)
+            elif step == 2:
                 prepare_w(n, 1, 1)
-                scalar_regroup(n, 0)
+                scalar_multiply(n, 0)
             else:
+                gpsimd_multiply(n, 1)
+                scalar_regroup(n, 0)
                 scalar_multiply(n, 1)
 
         def quantise(values, tag):
@@ -325,12 +347,12 @@ def tile_dynamicfeaturegroupinglayer_k_kernel(
                 weighted = stage.tile([P, TILE], BF16, name="weighted", tag="weighted", align_bytes=64)
                 masks_here, x_view = M, x_psum[n]
             else:
-                weighted, masks_here, x_view = shared_of[(n, sh)], VECTOR_MASKS, x_ready[n]
+                weighted, masks_here, x_view = shared_of[(n, sh)], SHARES[BY_VECTOR][1], x_ready[n]
             shape = [P, CC, masks_here, B, PACK]
             nc.vector.tensor_tensor(
-                out=weighted[:].rearrange("p (cc m b t) -> p cc m b t", cc=CC, m=M, t=PACK)[:, :, 0:masks_here],
+                out=by_mask(weighted)[:, :, 0:masks_here],
                 in0=x_view[:, :, sh].unsqueeze(2).to_broadcast(shape),
-                in1=masks(n, cp, sh, False).unsqueeze(3).to_broadcast(shape),
+                in1=masks(n, cp, sh, BY_VECTOR).unsqueeze(3).to_broadcast(shape),
                 op=ALU.mult,
             )
             return weighted
@@ -417,7 +439,7 @@ def tile_dynamicfeaturegroupinglayer_k_kernel(
                 nc.scalar.copy(out=result[0:B], in_=bank[0:B, 0:H])
                 results[g] = result
 
-            return [statistics, normalise, activate, gate]
+            return [statistics, lambda: None, normalise, activate, gate]
 
         def store(g):
             nc.sync.dma_start(out=out[:, g * H : (g + 1) * H], in_=results[g][0:B])
@@ -426,6 +448,7 @@ def tile_dynamicfeaturegroupinglayer_k_kernel(
         first_masks[0]()
         prepare_w(0, 0, 0)
         first_masks[1]()
+        order_masks()
         prepare_x_scalar(0)
         prepare_w(0, 0, 1)
         first_masks[2]()
@@ -434,6 +457,8 @@ def tile_dynamicfeaturegroupinglayer_k_kernel(
         prepare_w(0, 1, 1)
         quantise_w(0)
         first_masks[3]()
+        for sh in range(HALVES):
+            gpsimd_multiply(0, sh)
         scalar_multiply(0, 0)
         scalar_regroup(0, 0)
         scalar_multiply(0, 1)
@@ -457,6 +482,8 @@ def tile_dynamicfeaturegroupinglayer_k_kernel(
                     scalar_regroup(n, 1)
                 if n + 1 < N_UNITS:
                     prepare(n + 1, k)
+                if k == 0 and n > 0:
+                    quantise_w(n)
                 if waiting is not None:
                     contract(*waiting)
                     if k == 0 and v == 0:
@@ -465,8 +492,6 @@ def tile_dynamicfeaturegroupinglayer_k_kernel(
                 if steps:
                     steps[0]()
                     steps = steps[1:]
-            if n + 1 < N_UNITS:
-                quantise_w(n + 1)
         contract(*waiting)
         steps.extend(layer_norm_steps(G - 1))
         for step in steps:

@@ -30,10 +30,10 @@ N_UNITS = G * UNITS
 PASSES = S // K_PASS
 SHV = HALVES * UNITS
 CC = 2
-TILE = CC * M * B * PACK
-SHARES = ((0, 1), (1, 2), (2, M))
+TILE = CC * HALVES * M * B * PACK
+SHARES = (((0, 0), (0, 2), (2, M)), ((0, 1), (1, 2), (2, M)))
 BY_VECTOR, BY_GPSIMD, BY_SCALAR = range(3)
-LOAD_AHEAD = 3
+LOAD_AHEAD = 4
 PAIR = 2
 PAIR_ROWS = PAIR * M
 LN_ROWS = 4
@@ -124,23 +124,32 @@ def tile_dynamicfeaturegroupinglayer_k_kernel(
         )
         mask_order = const.tile([P, P], F32, name="mask_order")
         by_pass = ident[:].rearrange(
-            "p (g2 m shv cp cc) -> p g2 shv cc m cp", g2=PAIR, m=M, shv=SHV, cp=2
+            "p (g2 m sh v cp cc) -> p cp g2 sh v cc m", g2=PAIR, m=M, sh=HALVES, v=UNITS, cp=2
         )
         mask_cols = {}
 
         def order_masks():
-            col = 0
-            for cp in range(2):
-                for g2 in range(PAIR):
-                    for engine, (first_m, last_m) in enumerate(SHARES if cp == 1 else ((0, M),)):
-                        width = SHV * CC * (last_m - first_m)
-                        nc.vector.tensor_copy(
-                            out=mask_order[:, col : col + width].rearrange(
-                                "p (shv cc m) -> p shv cc m", shv=SHV, cc=CC
-                            ),
-                            in_=by_pass[:, g2, :, :, first_m:last_m, cp],
-                        )
-                        mask_cols[(cp, g2, engine)] = col
+            for g2 in range(PAIR):
+                for sh in range(HALVES):
+                    nc.vector.tensor_copy(
+                        out=mask_order[:, 0 : P // 2].rearrange(
+                            "p (g2 v cc sh m) -> p g2 sh v cc m", g2=PAIR, v=UNITS, cc=CC, sh=HALVES
+                        )[:, g2, sh],
+                        in_=by_pass[:, 0, g2, sh],
+                    )
+            col = P // 2
+            for g2 in range(PAIR):
+                for sh in range(HALVES):
+                    for engine, (first_m, last_m) in enumerate(SHARES[sh]):
+                        width = UNITS * CC * (last_m - first_m)
+                        mask_cols[(g2, sh, engine)] = col
+                        if width > 0:
+                            nc.vector.tensor_copy(
+                                out=mask_order[:, col : col + width].rearrange(
+                                    "p (v cc m) -> p v cc m", v=UNITS, cc=CC
+                                ),
+                                in_=by_pass[:, 1, g2, sh, :, :, first_m:last_m],
+                            )
                         col += width
 
         fold = const.tile([P, P], F32, name="fold")
@@ -155,7 +164,9 @@ def tile_dynamicfeaturegroupinglayer_k_kernel(
         affine = const.tile([P, 2, 2, G, H], F32, name="affine")
         affine_flat = affine[:].rearrange("p k w g j -> p (k w g j)")
 
-        for n in range(1, LOAD_AHEAD):
+        load(1)
+        load_logits(1)
+        for n in range(2, LOAD_AHEAD):
             load(n)
         for n, vec in enumerate((ln1_w, ln2_w, ln1_b, ln2_b)):
             nc.sync.dma_start(
@@ -163,15 +174,12 @@ def tile_dynamicfeaturegroupinglayer_k_kernel(
                 in_=vec.rearrange("g j -> (g j)").unsqueeze(0),
             )
 
-        def spread_steps():
-            def spread(first):
-                bank = banks.tile([P, BANK], F32, name="bank", tag="bank")
-                nc.tensor.matmul(
-                    out=bank[:], lhsT=ones[:], rhs=ln_rows[:, first : first + BANK], start=True, stop=True
-                )
-                nc.scalar.copy(out=affine_flat[:, first : first + BANK], in_=bank[:])
-
-            return [lambda first=first: spread(first) for first in range(0, 4 * G * H, BANK)]
+        def spread(first):
+            bank = banks.tile([P, BANK], F32, name="bank", tag="bank")
+            nc.tensor.matmul(
+                out=bank[:], lhsT=ones[:], rhs=ln_rows[:, first : first + BANK], start=True, stop=True
+            )
+            nc.scalar.copy(out=affine_flat[:, first : first + BANK], in_=bank[:])
 
         def entmax_steps(pair):
             kept = {}
@@ -210,15 +218,21 @@ def tile_dynamicfeaturegroupinglayer_k_kernel(
                 nc.tensor.matmul(out=bank[:, 0:1], lhsT=block[:], rhs=pass_sum[:], start=True, stop=True)
                 kept["e"], kept["sums"] = e, bank
 
-            def scale():
+            def pad():
                 padded = small.tile([P, 1], F32, name="padded", tag="padded")
-                nc.vector.tensor_scalar(
-                    out=padded[:], in0=kept["sums"][:, 0:1], scalar1=EPS, scalar2=None, op0=ALU.add
-                )
+                nc.scalar.activation(out=padded[:], in_=kept["sums"][:, 0:1], func=FUNC.Copy, bias=EPS)
+                kept["padded"] = padded
+
+            def power():
                 inv_norm = small.tile([P, 1], F32, name="inv_norm", tag="inv_norm")
-                nc.gpsimd.tensor_tensor(out=inv_norm[:], in0=padded[:], in1=norm_power[:], op=ALU.pow)
+                nc.gpsimd.tensor_tensor(out=inv_norm[:], in0=kept["padded"][:], in1=norm_power[:], op=ALU.pow)
+                kept["inv_norm"] = inv_norm
+
+            def scale():
                 by_row = small.tile([P, K_PASS], F32, name="by_row", tag="by_row")
-                nc.scalar.activation(out=by_row[:], in_=kept["e"][:], func=FUNC.Copy, scale=inv_norm[:, 0:1])
+                nc.scalar.activation(
+                    out=by_row[:], in_=kept["e"][:], func=FUNC.Copy, scale=kept["inv_norm"][:, 0:1]
+                )
                 kept["by_row"] = by_row
 
             def turn():
@@ -235,16 +249,20 @@ def tile_dynamicfeaturegroupinglayer_k_kernel(
                 for g2 in range(PAIR):
                     mask_of[PAIR * pair + g2] = mask
 
-            return [maxima, exponentials, scale, turn]
+            return maxima, exponentials, pad, power, scale, turn
 
-        def masks(n, cp, sh, engine):
+        def vector_masks(n):
             g, v = divmod(n, UNITS)
-            first_m, last_m = SHARES[engine] if cp == 1 else (0, M)
+            width = CC * HALVES * M
+            first = (g % PAIR * UNITS + v) * width
+            return mask_of[g][:, first : first + width, :].rearrange("p (q m) t -> p q m t", m=M)
+
+        def shared_masks(n, sh, engine):
+            g, v = divmod(n, UNITS)
+            first_m, last_m = SHARES[sh][engine]
             width = CC * (last_m - first_m)
-            first = mask_cols[(cp, g % PAIR, engine)] + (sh * UNITS + v) * width
-            return mask_of[g][:, first : first + width, :].rearrange(
-                "p (cc m) t -> p cc m t", cc=CC
-            )
+            first = mask_cols[(g % PAIR, sh, engine)] + v * width
+            return mask_of[g][:, first : first + width, :].rearrange("p (cc m) t -> p cc m t", cc=CC)
 
         def turn_words(source, cp, bank_view, order):
             words = source[:].bitcast(F32)
@@ -265,26 +283,42 @@ def tile_dynamicfeaturegroupinglayer_k_kernel(
 
         def prepare_w(n, sh, cp):
             if sh == 0 and cp == 0:
-                w_grouped = stage.tile([P, HALVES * 2, CC * P * PACK], BF16, name="w_grouped", tag="w_grouped", align_bytes=64)
+                w_grouped = stage.tile([P, HALVES * 2, CC * P * PACK], BF16, name="w_grouped", tag="w_grouped", bufs=2, align_bytes=64)
                 w_ready[n] = w_grouped
             turn_and_group(w_loaded[(n, sh)], cp, w_ready[n][:, sh * 2 + cp, :], ident)
 
         def prepare_x_scalar(n):
-            x_sb = stage.tile([P, CC * P * PACK], BF16, name="x_grouped", tag="x_grouped")
+            x_sb = stage.tile([P, CC * P * PACK], BF16, name="x_grouped", tag="x_grouped", bufs=4)
             turn_and_group(x_loaded[n], 1, x_sb[:], unzip)
             x_ready[n] = x_sb[:].rearrange("p (cc sh b t) -> p cc sh b t", cc=CC, sh=HALVES, t=PACK)
 
         def prepare_x_vector(n):
             bank = x_banks.tile([P, CC, P, 2], F32, name="x_bank", tag="x_bank")
             turn_words(x_loaded[n], 0, bank[:].rearrange("p cc col u -> p cc u col"), unzip)
-            x_psum[n] = bank[:].bitcast(BF16).rearrange("p cc (sh b) t -> p cc sh b t", sh=HALVES)
+            x_psum[n] = bank[:].bitcast(BF16).rearrange("p cc (sh b) t -> p (cc sh) b t", sh=HALVES)
+
+        def by_mask(tile):
+            return tile[:].rearrange("p (cc sh m b t) -> p cc sh m b t", cc=CC, sh=HALVES, m=M, t=PACK)
+
+        def gpsimd_multiply(n, sh):
+            if sh == 0:
+                shared = stage.tile([P, TILE], BF16, name="shared", tag="shared", bufs=2, align_bytes=64)
+                shared_of[n] = shared
+            first_m, last_m = SHARES[sh][BY_GPSIMD]
+            shape = [P, CC, last_m - first_m, B, PACK]
+            nc.gpsimd.tensor_tensor(
+                out=by_mask(shared_of[n])[:, :, sh, first_m:last_m],
+                in0=x_ready[n][:, :, sh].unsqueeze(2).to_broadcast(shape),
+                in1=shared_masks(n, sh, BY_GPSIMD).unsqueeze(3).to_broadcast(shape),
+                op=ALU.mult,
+            )
 
         def scalar_multiply(n, sh):
-            mask = masks(n, 1, sh, BY_SCALAR)
-            masks_here = M - SHARES[BY_SCALAR][0]
-            planes = stage.tile([P, CC, masks_here, PACK, B], BF16, name="planes", tag="planes")
+            mask = shared_masks(n, sh, BY_SCALAR)
+            first_m, last_m = SHARES[sh][BY_SCALAR]
+            planes = stage.tile([P, CC, last_m - first_m, PACK, B], BF16, name="planes", tag="planes")
             for cc in range(CC):
-                for m in range(masks_here):
+                for m in range(last_m - first_m):
                     for t in range(PACK):
                         nc.scalar.activation(
                             out=planes[:, cc, m, t, :],
@@ -295,42 +329,11 @@ def tile_dynamicfeaturegroupinglayer_k_kernel(
             planes_of[(n, sh)] = planes
 
         def scalar_regroup(n, sh):
+            first_m, last_m = SHARES[sh][BY_SCALAR]
             nc.scalar.copy(
-                out=by_mask(shared_of[(n, sh)])[:, :, slice(*SHARES[BY_SCALAR])],
+                out=by_mask(shared_of[n])[:, :, sh, first_m:last_m],
                 in_=planes_of[(n, sh)][:].rearrange("p cc m t b -> p cc m b t"),
             )
-
-        def by_mask(tile):
-            return tile[:].rearrange("p (cc m b t) -> p cc m b t", cc=CC, m=M, t=PACK)
-
-        def gpsimd_multiply(n, sh):
-            shared = stage.tile([P, TILE], BF16, name="shared", tag="shared", bufs=3, align_bytes=64)
-            shared_of[(n, sh)] = shared
-            first_m, last_m = SHARES[BY_GPSIMD]
-            shape = [P, CC, last_m - first_m, B, PACK]
-            nc.gpsimd.tensor_tensor(
-                out=by_mask(shared)[:, :, first_m:last_m],
-                in0=x_ready[n][:, :, sh].unsqueeze(2).to_broadcast(shape),
-                in1=masks(n, 1, sh, BY_GPSIMD).unsqueeze(3).to_broadcast(shape),
-                op=ALU.mult,
-            )
-
-        def prepare(n, step):
-            if step == 0:
-                prepare_x_scalar(n)
-                prepare_w(n, 0, 0)
-            elif step == 1:
-                gpsimd_multiply(n, 0)
-                prepare_w(n, 0, 1)
-                prepare_x_vector(n)
-                prepare_w(n, 1, 0)
-            elif step == 2:
-                prepare_w(n, 1, 1)
-                scalar_multiply(n, 0)
-            else:
-                gpsimd_multiply(n, 1)
-                scalar_regroup(n, 0)
-                scalar_multiply(n, 1)
 
         def quantise(values, tag):
             width = values.shape[1] // PACK
@@ -342,52 +345,57 @@ def tile_dynamicfeaturegroupinglayer_k_kernel(
         def quantise_w(n):
             w_quantised[n] = quantise(w_ready[n][:].rearrange("p c f -> p (c f)"), "w")
 
-        def multiply(n, cp, sh):
-            if cp == 0:
-                weighted = stage.tile([P, TILE], BF16, name="weighted", tag="weighted", align_bytes=64)
-                masks_here, x_view = M, x_psum[n]
-            else:
-                weighted, masks_here, x_view = shared_of[(n, sh)], SHARES[BY_VECTOR][1], x_ready[n]
-            shape = [P, CC, masks_here, B, PACK]
+        def vector_multiply(n):
+            weighted = stage.tile([P, TILE], BF16, name="weighted", tag="weighted", bufs=2, align_bytes=64)
+            shape = [P, CC * HALVES, M, B, PACK]
             nc.vector.tensor_tensor(
-                out=by_mask(weighted)[:, :, 0:masks_here],
-                in0=x_view[:, :, sh].unsqueeze(2).to_broadcast(shape),
-                in1=masks(n, cp, sh, BY_VECTOR).unsqueeze(3).to_broadcast(shape),
+                out=weighted[:].rearrange("p (q m b t) -> p q m b t", q=CC * HALVES, m=M, t=PACK),
+                in0=x_psum[n].unsqueeze(2).to_broadcast(shape),
+                in1=vector_masks(n).unsqueeze(3).to_broadcast(shape),
                 op=ALU.mult,
             )
             return weighted
 
-        def contract(n, cp, sh, weighted):
+        def vector_share(n):
+            for sh in range(HALVES):
+                first_m, last_m = SHARES[sh][BY_VECTOR]
+                if last_m > first_m:
+                    shape = [P, CC, last_m - first_m, B, PACK]
+                    nc.vector.tensor_tensor(
+                        out=by_mask(shared_of[n])[:, :, sh, first_m:last_m],
+                        in0=x_ready[n][:, :, sh].unsqueeze(2).to_broadcast(shape),
+                        in1=shared_masks(n, sh, BY_VECTOR).unsqueeze(3).to_broadcast(shape),
+                        op=ALU.mult,
+                    )
+
+        def contract(n, cp, weighted):
             v = n % UNITS
-            first = (v, cp, sh) == (0, 0, 0)
-            last = (v, cp, sh) == (UNITS - 1, 1, HALVES - 1)
-            if first:
+            if (v, cp) == (0, 0):
                 for mt in range(2):
                     acc_tile = sums.tile([P, P], F32, name="acc%d" % mt, tag="acc%d" % mt)
                     acc[mt] = acc_tile
             a_codes, a_scales = quantise(weighted[:], "a")
             w_codes, w_scales = w_quantised[n]
-            for cc in range(CC):
+            for q in range(CC * HALVES):
+                cc, sh = divmod(q, HALVES)
+                w_pass = (sh * 2 + cp) * CC + cc
+                w_cols = slice(w_pass * P, (w_pass + 1) * P)
                 for mt in range(2):
-                    a_cols = slice((cc * 2 + mt) * P, (cc * 2 + mt + 1) * P)
-                    w_pass = (sh * 2 + cp) * CC + cc
-                    w_cols = slice(w_pass * P, (w_pass + 1) * P)
+                    a_cols = slice((q * 2 + mt) * P, (q * 2 + mt + 1) * P)
                     nc.tensor.matmul_mx(
                         out=acc[mt][:],
                         lhsT=a_codes[:, a_cols].bitcast(FP8X4),
                         lhsT_scale=a_scales[:, a_cols],
                         rhs=w_codes[:, w_cols].bitcast(FP8X4),
                         rhs_scale=w_scales[:, w_cols],
-                        start=(first and cc == 0),
-                        stop=(last and cc == CC - 1),
+                        start=(v, cp, q) == (0, 0, 0),
+                        stop=(v, cp, q) == (UNITS - 1, 1, CC * HALVES - 1),
                     )
 
         results = {}
 
         def layer_norm_steps(g):
             raw = small.tile([P, 2, H, 2], F32, name="raw", tag="raw")
-            for mt in range(2):
-                nc.scalar.copy(out=raw[:, mt].rearrange("p j w -> p (j w)"), in_=acc[mt][:])
             stats = small.tile([P, LN_ROWS, 3], F32, name="stats", tag="stats")
             rstd = small.tile([P, LN_ROWS], F32, name="rstd", tag="rstd")
             normed = small.tile([P, 2, 2, H], F32, name="normed", tag="normed")
@@ -395,12 +403,18 @@ def tile_dynamicfeaturegroupinglayer_k_kernel(
             half_relu = small.tile([P, 2, H], F32, name="half_relu", tag="half_relu")
             gated = small.tile([P, 2, H], F32, name="gated", tag="gated")
 
+            def empty():
+                for mt in range(2):
+                    nc.scalar.copy(out=raw[:, mt].rearrange("p j w -> p (j w)"), in_=acc[mt][:])
+
             def statistics():
                 for mt in range(2):
                     nc.vector.bn_stats(
                         out=stats[:, 2 * mt : 2 * mt + 2, :].rearrange("p w k -> p (w k)"),
                         in_=raw[:, mt].rearrange("p j w -> p (j w)"),
                     )
+
+            def power():
                 var_eps = small.tile([P, LN_ROWS], F32, name="var_eps", tag="var_eps")
                 nc.gpsimd.tensor_scalar(
                     out=var_eps[:], in0=stats[:, :, 2], scalar1=1.0 / H, scalar2=EPS, op0=ALU.mult, op1=ALU.add
@@ -422,7 +436,6 @@ def tile_dynamicfeaturegroupinglayer_k_kernel(
                             in1=affine[:, 1, w, g, :], op0=ALU.mult, op1=ALU.add,
                         )
 
-            def activate():
                 nc.scalar.activation(out=half_tanh[:], in_=normed[:, :, 0, :], func=FUNC.Tanh, scale=0.5)
                 nc.scalar.activation(out=half_relu[:], in_=normed[:, :, 1, :], func=FUNC.Relu, scale=0.5)
 
@@ -439,61 +452,102 @@ def tile_dynamicfeaturegroupinglayer_k_kernel(
                 nc.scalar.copy(out=result[0:B], in_=bank[0:B, 0:H])
                 results[g] = result
 
-            return [statistics, lambda: None, normalise, activate, gate]
+            return empty, statistics, power, normalise, gate
 
         def store(g):
             nc.sync.dma_start(out=out[:, g * H : (g + 1) * H], in_=results[g][0:B])
 
-        first_masks = entmax_steps(0)
-        first_masks[0]()
+        maxima, exponentials, pad, power, scale, turn = entmax_steps(0)
+        maxima()
         prepare_w(0, 0, 0)
-        first_masks[1]()
+        exponentials()
         order_masks()
         prepare_x_scalar(0)
+        pad()
+        power()
         prepare_w(0, 0, 1)
-        first_masks[2]()
-        prepare_w(0, 1, 0)
         prepare_x_vector(0)
+        scale()
+        prepare_w(0, 1, 0)
+        turn()
         prepare_w(0, 1, 1)
         quantise_w(0)
-        first_masks[3]()
         for sh in range(HALVES):
             gpsimd_multiply(0, sh)
         scalar_multiply(0, 0)
+        prepare_x_scalar(1)
         scalar_regroup(0, 0)
         scalar_multiply(0, 1)
 
-        steps = spread_steps()
-        waiting = None
+        todo = {}
+
+        def put(n, slot, work):
+            todo.setdefault((n, slot), []).append(work)
+
+        def run(n, slot):
+            for work in todo.get((n, slot), []):
+                work()
+
+        for k, (n, slot) in enumerate(((0, 2), (0, 3), (1, 0), (1, 2), (1, 3))):
+            put(n, slot, lambda first=k * BANK: spread(first))
+        for pair in range(1, G // PAIR):
+            n = (pair - 1) * PAIR * UNITS
+            maxima, exponentials, pad, power, scale, turn = entmax_steps(pair)
+            put(n, 0, maxima)
+            put(n, 1, exponentials)
+            put(n, 3, pad)
+            put(n + 1, "gpsimd", power)
+            put(n + 1, 0, scale)
+            put(n + 1, 2, turn)
+
         for n in range(N_UNITS):
-            g, v = divmod(n, UNITS)
+            more = n + 1 < N_UNITS
             if n + LOAD_AHEAD < N_UNITS:
                 load(n + LOAD_AHEAD)
-            if n % (PAIR * UNITS) == 0 and g + PAIR < G:
-                load_logits(g // PAIR + 1)
-            if n % (PAIR * UNITS) == 1 and g + PAIR < G:
-                steps.extend(entmax_steps(g // PAIR + 1))
-            if v == UNITS - 1 and g > 0:
-                steps.append(lambda done=g - 1: store(done))
-            for k in range(4):
-                cp, sh = divmod(k, HALVES)
-                weighted = multiply(n, cp, sh)
-                if k == 0:
-                    scalar_regroup(n, 1)
-                if n + 1 < N_UNITS:
-                    prepare(n + 1, k)
-                if k == 0 and n > 0:
-                    quantise_w(n)
-                if waiting is not None:
-                    contract(*waiting)
-                    if k == 0 and v == 0:
-                        steps.extend(layer_norm_steps(g - 1))
-                waiting = (n, cp, sh, weighted)
-                if steps:
-                    steps[0]()
-                    steps = steps[1:]
-        contract(*waiting)
-        steps.extend(layer_norm_steps(G - 1))
-        for step in steps:
+            if n % (PAIR * UNITS) == 1 and n // UNITS + 2 * PAIR < G:
+                load_logits(n // UNITS // PAIR + 2)
+            if n > 0 and n % UNITS == 0:
+                done = n // UNITS - 1
+                empty, statistics, power, normalise, gate = layer_norm_steps(done)
+                put(n, 0, empty)
+                put(n, 3, statistics)
+                put(n + 1, "gpsimd", power)
+                put(n + 1, 2, normalise)
+                put(n + 2, 0, gate)
+                put(n + 3, 0, lambda done=done: store(done))
+            weighted = vector_multiply(n)
+            if more:
+                gpsimd_multiply(n + 1, 0)
+            run(n, "gpsimd")
+            if more:
+                gpsimd_multiply(n + 1, 1)
+            if n + 2 < N_UNITS:
+                prepare_x_scalar(n + 2)
+            scalar_regroup(n, 1)
+            if more:
+                prepare_w(n + 1, 0, 0)
+                prepare_w(n + 1, 0, 1)
+                prepare_x_vector(n + 1)
+            run(n, 0)
+            if more:
+                prepare_w(n + 1, 1, 0)
+                prepare_w(n + 1, 1, 1)
+            if n > 0:
+                quantise_w(n)
+            run(n, 1)
+            vector_share(n)
+            if more:
+                scalar_multiply(n + 1, 0)
+            contract(n, 0, weighted)
+            run(n, 2)
+            if more:
+                scalar_regroup(n + 1, 0)
+                scalar_multiply(n + 1, 1)
+            contract(n, 1, shared_of[n])
+            run(n, 3)
+
+        run(N_UNITS, 0)
+        run(N_UNITS + 1, 0)
+        for step in layer_norm_steps(G - 1):
             step()
         store(G - 1)

@@ -33,7 +33,7 @@ CC = 2
 TILE = CC * HALVES * M * B * PACK
 SHARES = (((0, 0), (0, 2), (2, M)), ((0, 1), (1, 2), (2, M)))
 BY_VECTOR, BY_GPSIMD, BY_SCALAR = range(3)
-LOAD_AHEAD = 4
+LOAD_AHEAD = 3
 PAIR = 2
 PAIR_ROWS = PAIR * M
 LN_ROWS = 4
@@ -184,18 +184,20 @@ def tile_dynamicfeaturegroupinglayer_k_kernel(
         def entmax_steps(pair):
             kept = {}
 
-            def maxima():
-                logits = logits_of[pair]
+            def pass_maxima():
                 pass_max = small.tile([P, 1], F32, name="pass_max", tag="pass_max")
-                nc.vector.tensor_reduce(out=pass_max[:], in_=logits[:], axis=AXIS_X, op=ALU.max)
+                nc.vector.tensor_reduce(out=pass_max[:], in_=logits_of[pair][:], axis=AXIS_X, op=ALU.max)
+                kept["pass_max"] = pass_max
+
+            def spread_maxima():
                 bank = banks.tile([P, BANK], F32, name="bank", tag="bank")
                 nc.tensor.matmul(
-                    out=bank[:, 0:P], lhsT=pass_max[:, 0:1].to_broadcast([P, P]), rhs=ident[:],
+                    out=bank[:, 0:P], lhsT=kept["pass_max"][:, 0:1].to_broadcast([P, P]), rhs=ident[:],
                     start=True, stop=True,
                 )
                 kept["maxima"] = bank
 
-            def exponentials():
+            def row_maxima():
                 own = small.tile([P, P], F32, name="own", tag="own")
                 nc.vector.tensor_tensor(out=own[:], in0=kept["maxima"][:, 0:P], in1=other_rows[:], op=ALU.add)
                 row_max = small.tile([P, 1], F32, name="row_max", tag="row_max")
@@ -204,23 +206,28 @@ def tile_dynamicfeaturegroupinglayer_k_kernel(
                 nc.vector.tensor_tensor(
                     out=biases[:], in0=row_max[:].to_broadcast([P, 2]), in1=exp_scales[:], op=ALU.mult
                 )
+                kept["biases"] = biases
+
+            def exponentials():
                 powers = small.tile([P, K_PASS], F32, name="powers", tag="powers")
                 pass_sum = small.tile([P, 1], F32, name="pass_sum", tag="pass_sum")
                 nc.scalar.activation(
-                    out=powers[:], in_=logits_of[pair][:], func=FUNC.Exp, scale=ALPHA, bias=biases[:, 0:1],
-                    accum_out=pass_sum[:],
+                    out=powers[:], in_=logits_of[pair][:], func=FUNC.Exp, scale=ALPHA,
+                    bias=kept["biases"][:, 0:1], accum_out=pass_sum[:],
                 )
                 e = small.tile([P, K_PASS], F32, name="e", tag="e")
                 nc.scalar.activation(
-                    out=e[:], in_=logits_of[pair][:], func=FUNC.Exp, bias=biases[:, 1:2]
+                    out=e[:], in_=logits_of[pair][:], func=FUNC.Exp, bias=kept["biases"][:, 1:2]
                 )
-                bank = banks.tile([P, BANK], F32, name="bank", tag="bank")
-                nc.tensor.matmul(out=bank[:, 0:1], lhsT=block[:], rhs=pass_sum[:], start=True, stop=True)
-                kept["e"], kept["sums"] = e, bank
+                kept["e"], kept["pass_sum"] = e, pass_sum
 
-            def pad():
+            def row_sums():
+                bank = banks.tile([P, BANK], F32, name="bank", tag="bank")
+                nc.tensor.matmul(
+                    out=bank[:, 0:1], lhsT=block[:], rhs=kept["pass_sum"][:], start=True, stop=True
+                )
                 padded = small.tile([P, 1], F32, name="padded", tag="padded")
-                nc.scalar.activation(out=padded[:], in_=kept["sums"][:, 0:1], func=FUNC.Copy, bias=EPS)
+                nc.scalar.activation(out=padded[:], in_=bank[:, 0:1], func=FUNC.Copy, bias=EPS)
                 kept["padded"] = padded
 
             def power():
@@ -244,12 +251,17 @@ def tile_dynamicfeaturegroupinglayer_k_kernel(
                         in_=kept["by_row"][:, 2 * P * u + e : 2 * P * (u + 1) : 2],
                         identity=mask_order[:],
                     )
+                kept["mask"] = bank
+
+            def keep():
                 mask = small.tile([P, P, PACK], F32, name="mask", tag="mask")
-                nc.scalar.copy(out=mask[:], in_=bank[:])
+                nc.scalar.copy(out=mask[:], in_=kept["mask"][:])
                 for g2 in range(PAIR):
                     mask_of[PAIR * pair + g2] = mask
 
-            return maxima, exponentials, pad, power, scale, turn
+            return (
+                pass_maxima, spread_maxima, row_maxima, exponentials, row_sums, power, scale, turn, keep
+            )
 
         def vector_masks(n):
             g, v = divmod(n, UNITS)
@@ -288,7 +300,7 @@ def tile_dynamicfeaturegroupinglayer_k_kernel(
             turn_and_group(w_loaded[(n, sh)], cp, w_ready[n][:, sh * 2 + cp, :], ident)
 
         def prepare_x_scalar(n):
-            x_sb = stage.tile([P, CC * P * PACK], BF16, name="x_grouped", tag="x_grouped", bufs=4)
+            x_sb = stage.tile([P, CC * P * PACK], BF16, name="x_grouped", tag="x_grouped")
             turn_and_group(x_loaded[n], 1, x_sb[:], unzip)
             x_ready[n] = x_sb[:].rearrange("p (cc sh b t) -> p cc sh b t", cc=CC, sh=HALVES, t=PACK)
 
@@ -302,7 +314,7 @@ def tile_dynamicfeaturegroupinglayer_k_kernel(
 
         def gpsimd_multiply(n, sh):
             if sh == 0:
-                shared = stage.tile([P, TILE], BF16, name="shared", tag="shared", bufs=2, align_bytes=64)
+                shared = stage.tile([P, TILE], BF16, name="shared", tag="shared", bufs=1, align_bytes=64)
                 shared_of[n] = shared
             first_m, last_m = SHARES[sh][BY_GPSIMD]
             shape = [P, CC, last_m - first_m, B, PACK]
@@ -368,20 +380,22 @@ def tile_dynamicfeaturegroupinglayer_k_kernel(
                         op=ALU.mult,
                     )
 
-        def contract(n, cp, weighted):
+        def contract(n, cp, weighted, first_cc=0, last_cc=CC):
             v = n % UNITS
-            if (v, cp) == (0, 0):
+            if (v, cp, first_cc) == (0, 0, 0):
                 for mt in range(2):
                     acc_tile = sums.tile([P, P], F32, name="acc%d" % mt, tag="acc%d" % mt)
                     acc[mt] = acc_tile
-            a_codes, a_scales = quantise(weighted[:], "a")
+            width = TILE // CC
+            a_codes, a_scales = quantise(weighted[:, first_cc * width : last_cc * width], "a")
             w_codes, w_scales = w_quantised[n]
-            for q in range(CC * HALVES):
+            for q in range(first_cc * HALVES, last_cc * HALVES):
                 cc, sh = divmod(q, HALVES)
                 w_pass = (sh * 2 + cp) * CC + cc
                 w_cols = slice(w_pass * P, (w_pass + 1) * P)
                 for mt in range(2):
-                    a_cols = slice((q * 2 + mt) * P, (q * 2 + mt + 1) * P)
+                    a_tile = (q - first_cc * HALVES) * 2 + mt
+                    a_cols = slice(a_tile * P, (a_tile + 1) * P)
                     nc.tensor.matmul_mx(
                         out=acc[mt][:],
                         lhsT=a_codes[:, a_cols].bitcast(FP8X4),
@@ -395,23 +409,25 @@ def tile_dynamicfeaturegroupinglayer_k_kernel(
         results = {}
 
         def layer_norm_steps(g):
-            raw = small.tile([P, 2, H, 2], F32, name="raw", tag="raw")
             stats = small.tile([P, LN_ROWS, 3], F32, name="stats", tag="stats")
             rstd = small.tile([P, LN_ROWS], F32, name="rstd", tag="rstd")
             normed = small.tile([P, 2, 2, H], F32, name="normed", tag="normed")
             half_tanh = small.tile([P, 2, H], F32, name="half_tanh", tag="half_tanh")
             half_relu = small.tile([P, 2, H], F32, name="half_relu", tag="half_relu")
             gated = small.tile([P, 2, H], F32, name="gated", tag="gated")
+            sums_of = dict(acc)
+            kept = {}
 
             def empty():
                 for mt in range(2):
-                    nc.scalar.copy(out=raw[:, mt].rearrange("p j w -> p (j w)"), in_=acc[mt][:])
+                    raw = small.tile([P, P], F32, name="raw%d" % mt, tag="raw%d" % mt)
+                    nc.scalar.copy(out=raw[:], in_=sums_of[mt][:])
+                    sums_of[mt] = raw
 
             def statistics():
                 for mt in range(2):
                     nc.vector.bn_stats(
-                        out=stats[:, 2 * mt : 2 * mt + 2, :].rearrange("p w k -> p (w k)"),
-                        in_=raw[:, mt].rearrange("p j w -> p (j w)"),
+                        out=stats[:, 2 * mt : 2 * mt + 2, :].rearrange("p w k -> p (w k)"), in_=sums_of[mt][:]
                     )
 
             def power():
@@ -425,7 +441,7 @@ def tile_dynamicfeaturegroupinglayer_k_kernel(
                 for mt in range(2):
                     for w in range(2):
                         nc.vector.scalar_tensor_tensor(
-                            out=normed[:, mt, w, :], in0=raw[:, mt, :, w], scalar=stats[:, 2 * mt + w, 1:2],
+                            out=normed[:, mt, w, :], in0=sums_of[mt][:, w:P:2], scalar=stats[:, 2 * mt + w, 1:2],
                             in1=affine[:, 0, w, g, :], op0=ALU.subtract, op1=ALU.mult,
                         )
                 for mt in range(2):
@@ -436,6 +452,7 @@ def tile_dynamicfeaturegroupinglayer_k_kernel(
                             in1=affine[:, 1, w, g, :], op0=ALU.mult, op1=ALU.add,
                         )
 
+            def activate():
                 nc.scalar.activation(out=half_tanh[:], in_=normed[:, :, 0, :], func=FUNC.Tanh, scale=0.5)
                 nc.scalar.activation(out=half_relu[:], in_=normed[:, :, 1, :], func=FUNC.Relu, scale=0.5)
 
@@ -443,40 +460,45 @@ def tile_dynamicfeaturegroupinglayer_k_kernel(
                 nc.vector.scalar_tensor_tensor(
                     out=gated[:], in0=half_tanh[:], scalar=1.0, in1=half_relu[:], op0=ALU.add, op1=ALU.mult
                 )
+
+            def add_masks():
                 bank = banks.tile([P, BANK], F32, name="bank", tag="bank")
+                kept["sums"] = bank
                 for mt in range(2):
                     nc.tensor.matmul(
                         out=bank[:, 0:H], lhsT=fold[:], rhs=gated[:, mt, :], start=(mt == 0), stop=(mt == 1)
                     )
+
+            def finish():
                 result = small.tile([P, H], F32, name="result", tag="result")
-                nc.scalar.copy(out=result[0:B], in_=bank[0:B, 0:H])
+                nc.scalar.copy(out=result[0:B], in_=kept["sums"][0:B, 0:H])
                 results[g] = result
 
-            return empty, statistics, power, normalise, gate
+            return empty, statistics, power, normalise, activate, gate, add_masks, finish
 
         def store(g):
             nc.sync.dma_start(out=out[:, g * H : (g + 1) * H], in_=results[g][0:B])
 
-        maxima, exponentials, pad, power, scale, turn = entmax_steps(0)
-        maxima()
-        prepare_w(0, 0, 0)
-        exponentials()
+        (
+            pass_maxima, spread_maxima, row_maxima, exponentials, row_sums, power, scale, turn, keep
+        ) = entmax_steps(0)
+        pass_maxima()
+        spread_maxima()
+        row_maxima()
         order_masks()
+        exponentials()
+        row_sums()
         prepare_x_scalar(0)
-        pad()
         power()
-        prepare_w(0, 0, 1)
+        prepare_w(0, 0, 0)
         prepare_x_vector(0)
         scale()
-        prepare_w(0, 1, 0)
+        prepare_w(0, 0, 1)
         turn()
+        keep()
+        prepare_w(0, 1, 0)
         prepare_w(0, 1, 1)
-        quantise_w(0)
-        for sh in range(HALVES):
-            gpsimd_multiply(0, sh)
         scalar_multiply(0, 0)
-        prepare_x_scalar(1)
-        scalar_regroup(0, 0)
         scalar_multiply(0, 1)
 
         todo = {}
@@ -488,17 +510,22 @@ def tile_dynamicfeaturegroupinglayer_k_kernel(
             for work in todo.get((n, slot), []):
                 work()
 
-        for k, (n, slot) in enumerate(((0, 2), (0, 3), (1, 0), (1, 2), (1, 3))):
+        for k, (n, slot) in enumerate(((1, 0), (1, 2), (1, 3), (2, 0), (2, 2))):
             put(n, slot, lambda first=k * BANK: spread(first))
         for pair in range(1, G // PAIR):
             n = (pair - 1) * PAIR * UNITS
-            maxima, exponentials, pad, power, scale, turn = entmax_steps(pair)
-            put(n, 0, maxima)
-            put(n, 1, exponentials)
-            put(n, 3, pad)
-            put(n + 1, "gpsimd", power)
-            put(n + 1, 0, scale)
-            put(n + 1, 2, turn)
+            (
+                pass_maxima, spread_maxima, row_maxima, exponentials, row_sums, power, scale, turn, keep
+            ) = entmax_steps(pair)
+            put(n, 0, pass_maxima)
+            put(n, 1, spread_maxima)
+            put(n, 2, row_maxima)
+            put(n, 3, exponentials)
+            put(n + 1, 1, row_sums)
+            put(n + 2, "gpsimd", power)
+            put(n + 2, 1, scale)
+            put(n + 2, 3, turn)
+            put(n + 2, 3, keep)
 
         for n in range(N_UNITS):
             more = n + 1 < N_UNITS
@@ -508,32 +535,32 @@ def tile_dynamicfeaturegroupinglayer_k_kernel(
                 load_logits(n // UNITS // PAIR + 2)
             if n > 0 and n % UNITS == 0:
                 done = n // UNITS - 1
-                empty, statistics, power, normalise, gate = layer_norm_steps(done)
+                empty, statistics, power, normalise, activate, gate, add_masks, finish = layer_norm_steps(done)
                 put(n, 0, empty)
                 put(n, 3, statistics)
                 put(n + 1, "gpsimd", power)
                 put(n + 1, 2, normalise)
+                put(n + 1, 3, activate)
                 put(n + 2, 0, gate)
+                put(n + 2, 2, add_masks)
+                put(n + 2, 3, finish)
                 put(n + 3, 0, lambda done=done: store(done))
             weighted = vector_multiply(n)
-            if more:
-                gpsimd_multiply(n + 1, 0)
+            gpsimd_multiply(n, 0)
             run(n, "gpsimd")
+            gpsimd_multiply(n, 1)
             if more:
-                gpsimd_multiply(n + 1, 1)
-            if n + 2 < N_UNITS:
-                prepare_x_scalar(n + 2)
-            scalar_regroup(n, 1)
-            if more:
+                prepare_x_scalar(n + 1)
                 prepare_w(n + 1, 0, 0)
                 prepare_w(n + 1, 0, 1)
-                prepare_x_vector(n + 1)
-            run(n, 0)
+            scalar_regroup(n, 0)
+            scalar_regroup(n, 1)
             if more:
+                prepare_x_vector(n + 1)
                 prepare_w(n + 1, 1, 0)
                 prepare_w(n + 1, 1, 1)
-            if n > 0:
-                quantise_w(n)
+            run(n, 0)
+            quantise_w(n)
             run(n, 1)
             vector_share(n)
             if more:
@@ -541,13 +568,16 @@ def tile_dynamicfeaturegroupinglayer_k_kernel(
             contract(n, 0, weighted)
             run(n, 2)
             if more:
-                scalar_regroup(n + 1, 0)
                 scalar_multiply(n + 1, 1)
-            contract(n, 1, shared_of[n])
+                contract(n, 1, shared_of[n])
+            else:
+                for cc in range(CC):
+                    contract(n, 1, shared_of[n], cc, cc + 1)
             run(n, 3)
 
-        run(N_UNITS, 0)
+        for slot in (0, 2, 3):
+            run(N_UNITS, slot)
         run(N_UNITS + 1, 0)
-        for step in layer_norm_steps(G - 1):
+        for step in layer_norm_steps(G - 1)[1:]:
             step()
         store(G - 1)

@@ -31,7 +31,10 @@ PASSES = S // K_PASS
 SHV = HALVES * UNITS
 CC = 2
 TILE = CC * HALVES * M * B * PACK
-SHARES = (((0, 0), (0, 2), (2, M)), ((0, 1), (1, 2), (2, M)))
+SHARES = (
+    (((0, 0), (0, 2), (2, M)), ((0, 0), (0, 2), (2, M))),
+    (((0, 1), (1, 2), (2, M)), ((0, 0), (0, 1), (1, M))),
+)
 BY_VECTOR, BY_GPSIMD, BY_SCALAR = range(3)
 LOAD_AHEAD = 3
 PAIR = 2
@@ -139,18 +142,17 @@ def tile_dynamicfeaturegroupinglayer_k_kernel(
                     )
             col = P // 2
             for g2 in range(PAIR):
-                for sh in range(HALVES):
-                    for engine, (first_m, last_m) in enumerate(SHARES[sh]):
-                        width = UNITS * CC * (last_m - first_m)
-                        mask_cols[(g2, sh, engine)] = col
-                        if width > 0:
-                            nc.vector.tensor_copy(
-                                out=mask_order[:, col : col + width].rearrange(
-                                    "p (v cc m) -> p v cc m", v=UNITS, cc=CC
-                                ),
-                                in_=by_pass[:, 1, g2, sh, :, :, first_m:last_m],
-                            )
-                        col += width
+                for v in range(UNITS):
+                    for sh in range(HALVES):
+                        for engine, (first_m, last_m) in enumerate(SHARES[v][sh]):
+                            width = CC * (last_m - first_m)
+                            mask_cols[(g2, v, sh, engine)] = col
+                            if width > 0:
+                                nc.vector.tensor_copy(
+                                    out=mask_order[:, col : col + width].rearrange("p (cc m) -> p cc m", cc=CC),
+                                    in_=by_pass[:, 1, g2, sh, v, :, first_m:last_m],
+                                )
+                            col += width
 
         fold = const.tile([P, P], F32, name="fold")
         for half in range(2):
@@ -271,9 +273,9 @@ def tile_dynamicfeaturegroupinglayer_k_kernel(
 
         def shared_masks(n, sh, engine):
             g, v = divmod(n, UNITS)
-            first_m, last_m = SHARES[sh][engine]
+            first_m, last_m = SHARES[v][sh][engine]
             width = CC * (last_m - first_m)
-            first = mask_cols[(g % PAIR, sh, engine)] + v * width
+            first = mask_cols[(g % PAIR, v, sh, engine)]
             return mask_of[g][:, first : first + width, :].rearrange("p (cc m) t -> p cc m t", cc=CC)
 
         def turn_words(source, cp, bank_view, order):
@@ -285,23 +287,23 @@ def tile_dynamicfeaturegroupinglayer_k_kernel(
                         out=bank_view[:, cc, u, :], in_=words[:, first : first + P], identity=order[:]
                     )
 
-        def turn_and_group(source, cp, grouped, order):
+        def turn_and_group(source, cp, grouped, order, copy):
             bank = banks.tile([P, CC, 2, P], F32, name="turned", tag="bank")
             turn_words(source, cp, bank[:], order)
-            nc.scalar.copy(
+            copy(
                 out=grouped.bitcast(F32).rearrange("p (cc col u) -> p cc col u", cc=CC, u=2),
                 in_=bank[:].rearrange("p cc u col -> p cc col u"),
             )
 
-        def prepare_w(n, sh, cp):
+        def prepare_w(n, sh, cp, copy=nc.scalar.copy):
             if sh == 0 and cp == 0:
                 w_grouped = stage.tile([P, HALVES * 2, CC * P * PACK], BF16, name="w_grouped", tag="w_grouped", bufs=2, align_bytes=64)
                 w_ready[n] = w_grouped
-            turn_and_group(w_loaded[(n, sh)], cp, w_ready[n][:, sh * 2 + cp, :], ident)
+            turn_and_group(w_loaded[(n, sh)], cp, w_ready[n][:, sh * 2 + cp, :], ident, copy)
 
-        def prepare_x_scalar(n):
+        def prepare_x_scalar(n, copy=nc.scalar.copy):
             x_sb = stage.tile([P, CC * P * PACK], BF16, name="x_grouped", tag="x_grouped")
-            turn_and_group(x_loaded[n], 1, x_sb[:], unzip)
+            turn_and_group(x_loaded[n], 1, x_sb[:], unzip, copy)
             x_ready[n] = x_sb[:].rearrange("p (cc sh b t) -> p cc sh b t", cc=CC, sh=HALVES, t=PACK)
 
         def prepare_x_vector(n):
@@ -316,7 +318,7 @@ def tile_dynamicfeaturegroupinglayer_k_kernel(
             if sh == 0:
                 shared = stage.tile([P, TILE], BF16, name="shared", tag="shared", bufs=1, align_bytes=64)
                 shared_of[n] = shared
-            first_m, last_m = SHARES[sh][BY_GPSIMD]
+            first_m, last_m = SHARES[n % UNITS][sh][BY_GPSIMD]
             shape = [P, CC, last_m - first_m, B, PACK]
             nc.gpsimd.tensor_tensor(
                 out=by_mask(shared_of[n])[:, :, sh, first_m:last_m],
@@ -327,7 +329,7 @@ def tile_dynamicfeaturegroupinglayer_k_kernel(
 
         def scalar_multiply(n, sh):
             mask = shared_masks(n, sh, BY_SCALAR)
-            first_m, last_m = SHARES[sh][BY_SCALAR]
+            first_m, last_m = SHARES[n % UNITS][sh][BY_SCALAR]
             planes = stage.tile([P, CC, last_m - first_m, PACK, B], BF16, name="planes", tag="planes")
             for cc in range(CC):
                 for m in range(last_m - first_m):
@@ -341,7 +343,7 @@ def tile_dynamicfeaturegroupinglayer_k_kernel(
             planes_of[(n, sh)] = planes
 
         def scalar_regroup(n, sh):
-            first_m, last_m = SHARES[sh][BY_SCALAR]
+            first_m, last_m = SHARES[n % UNITS][sh][BY_SCALAR]
             nc.scalar.copy(
                 out=by_mask(shared_of[n])[:, :, sh, first_m:last_m],
                 in_=planes_of[(n, sh)][:].rearrange("p cc m t b -> p cc m b t"),
@@ -370,7 +372,7 @@ def tile_dynamicfeaturegroupinglayer_k_kernel(
 
         def vector_share(n):
             for sh in range(HALVES):
-                first_m, last_m = SHARES[sh][BY_VECTOR]
+                first_m, last_m = SHARES[n % UNITS][sh][BY_VECTOR]
                 if last_m > first_m:
                     shape = [P, CC, last_m - first_m, B, PACK]
                     nc.vector.tensor_tensor(
@@ -474,7 +476,7 @@ def tile_dynamicfeaturegroupinglayer_k_kernel(
                 nc.scalar.copy(out=result[0:B], in_=kept["sums"][0:B, 0:H])
                 results[g] = result
 
-            return empty, statistics, power, normalise, activate, gate, add_masks, finish
+            return statistics, empty, power, normalise, activate, gate, add_masks, finish
 
         def store(g):
             nc.sync.dma_start(out=out[:, g * H : (g + 1) * H], in_=results[g][0:B])
@@ -487,17 +489,18 @@ def tile_dynamicfeaturegroupinglayer_k_kernel(
         row_maxima()
         order_masks()
         exponentials()
+        prepare_w(0, 0, 0, nc.vector.tensor_copy)
+        prepare_w(0, 0, 1, nc.vector.tensor_copy)
         row_sums()
-        prepare_x_scalar(0)
+        prepare_x_scalar(0, nc.vector.tensor_copy)
         power()
-        prepare_w(0, 0, 0)
-        prepare_x_vector(0)
+        prepare_w(0, 1, 0, nc.vector.tensor_copy)
+        prepare_w(0, 1, 1, nc.vector.tensor_copy)
         scale()
-        prepare_w(0, 0, 1)
+        prepare_x_vector(0)
         turn()
         keep()
-        prepare_w(0, 1, 0)
-        prepare_w(0, 1, 1)
+        quantise_w(0)
         scalar_multiply(0, 0)
         scalar_multiply(0, 1)
 
@@ -535,9 +538,9 @@ def tile_dynamicfeaturegroupinglayer_k_kernel(
                 load_logits(n // UNITS // PAIR + 2)
             if n > 0 and n % UNITS == 0:
                 done = n // UNITS - 1
-                empty, statistics, power, normalise, activate, gate, add_masks, finish = layer_norm_steps(done)
+                statistics, empty, power, normalise, activate, gate, add_masks, finish = layer_norm_steps(done)
+                put(n, 0, statistics)
                 put(n, 0, empty)
-                put(n, 3, statistics)
                 put(n + 1, "gpsimd", power)
                 put(n + 1, 2, normalise)
                 put(n + 1, 3, activate)
@@ -560,7 +563,8 @@ def tile_dynamicfeaturegroupinglayer_k_kernel(
                 prepare_w(n + 1, 1, 0)
                 prepare_w(n + 1, 1, 1)
             run(n, 0)
-            quantise_w(n)
+            if n > 0:
+                quantise_w(n)
             run(n, 1)
             vector_share(n)
             if more:
@@ -578,6 +582,7 @@ def tile_dynamicfeaturegroupinglayer_k_kernel(
         for slot in (0, 2, 3):
             run(N_UNITS, slot)
         run(N_UNITS + 1, 0)
-        for step in layer_norm_steps(G - 1)[1:]:
+        statistics, empty, power, normalise, activate, gate, add_masks, finish = layer_norm_steps(G - 1)
+        for step in (statistics, power, normalise, activate, gate, add_masks, finish):
             step()
         store(G - 1)

@@ -314,6 +314,9 @@ def tile_dynamicfeaturegroupinglayer_k_kernel(
         def by_mask(tile):
             return tile[:].rearrange("p (cc sh m b t) -> p cc sh m b t", cc=CC, sh=HALVES, m=M, t=PACK)
 
+        def words_by_mask(tile):
+            return tile[:].bitcast(F32).rearrange("p (cc sh m b u) -> p cc sh m b u", cc=CC, sh=HALVES, m=M, u=2)
+
         def gpsimd_multiply(n, sh):
             if sh == 0:
                 shared = stage.tile([P, TILE], BF16, name="shared", tag="shared", bufs=1, align_bytes=64)
@@ -330,12 +333,12 @@ def tile_dynamicfeaturegroupinglayer_k_kernel(
         def scalar_multiply(n, sh):
             mask = shared_masks(n, sh, BY_SCALAR)
             first_m, last_m = SHARES[n % UNITS][sh][BY_SCALAR]
-            planes = stage.tile([P, CC, last_m - first_m, PACK, B], BF16, name="planes", tag="planes")
+            planes = stage.tile([P, CC, last_m - first_m, 2, B, 2], BF16, name="planes", tag="planes")
             for cc in range(CC):
                 for m in range(last_m - first_m):
                     for t in range(PACK):
                         nc.scalar.activation(
-                            out=planes[:, cc, m, t, :],
+                            out=planes[:, cc, m, t // 2, :, t % 2],
                             in_=x_ready[n][:, cc, sh, :, t],
                             func=FUNC.Copy,
                             scale=mask[:, cc, m, t : t + 1],
@@ -345,8 +348,8 @@ def tile_dynamicfeaturegroupinglayer_k_kernel(
         def scalar_regroup(n, sh):
             first_m, last_m = SHARES[n % UNITS][sh][BY_SCALAR]
             nc.scalar.copy(
-                out=by_mask(shared_of[n])[:, :, sh, first_m:last_m],
-                in_=planes_of[(n, sh)][:].rearrange("p cc m t b -> p cc m b t"),
+                out=words_by_mask(shared_of[n])[:, :, sh, first_m:last_m],
+                in_=planes_of[(n, sh)][:].bitcast(F32).rearrange("p cc m u b one -> p cc m b (u one)"),
             )
 
         def quantise(values, tag):
@@ -503,6 +506,8 @@ def tile_dynamicfeaturegroupinglayer_k_kernel(
         quantise_w(0)
         scalar_multiply(0, 0)
         scalar_multiply(0, 1)
+        prepare_x_scalar(1)
+        prepare_w(1, 0, 0)
 
         todo = {}
 
@@ -552,13 +557,10 @@ def tile_dynamicfeaturegroupinglayer_k_kernel(
             gpsimd_multiply(n, 0)
             run(n, "gpsimd")
             gpsimd_multiply(n, 1)
-            if more:
-                prepare_x_scalar(n + 1)
-                prepare_w(n + 1, 0, 0)
-                prepare_w(n + 1, 0, 1)
             scalar_regroup(n, 0)
             scalar_regroup(n, 1)
             if more:
+                prepare_w(n + 1, 0, 1)
                 prepare_x_vector(n + 1)
                 prepare_w(n + 1, 1, 0)
                 prepare_w(n + 1, 1, 1)
@@ -573,6 +575,9 @@ def tile_dynamicfeaturegroupinglayer_k_kernel(
             run(n, 2)
             if more:
                 scalar_multiply(n + 1, 1)
+                if n + 2 < N_UNITS:
+                    prepare_x_scalar(n + 2)
+                    prepare_w(n + 2, 0, 0)
                 contract(n, 1, shared_of[n])
             else:
                 for cc in range(CC):

@@ -31,11 +31,8 @@ PASSES = S // K_PASS
 SHV = HALVES * UNITS
 CC = 2
 TILE = CC * HALVES * M * B * PACK
-SHARES = (
-    (((0, 0), (0, 2), (2, M)), ((0, 0), (0, 2), (2, M))),
-    (((0, 1), (1, 2), (2, M)), ((0, 0), (0, 1), (1, M))),
-)
-BY_VECTOR, BY_GPSIMD, BY_SCALAR = range(3)
+GPSIMD_MASKS = (2, 1)
+VECTOR_END = ((2, 2), (2, 1))
 LOAD_AHEAD = 3
 PAIR = 2
 PAIR_ROWS = PAIR * M
@@ -129,9 +126,11 @@ def tile_dynamicfeaturegroupinglayer_k_kernel(
         by_pass = ident[:].rearrange(
             "p (g2 m sh v cp cc) -> p cp g2 sh v cc m", g2=PAIR, m=M, sh=HALVES, v=UNITS, cp=2
         )
-        mask_cols = {}
+        gpsimd_cols = {}
+        shared_cols = {}
 
         def order_masks():
+            col = P // 2
             for g2 in range(PAIR):
                 for sh in range(HALVES):
                     nc.vector.tensor_copy(
@@ -140,19 +139,28 @@ def tile_dynamicfeaturegroupinglayer_k_kernel(
                         )[:, g2, sh],
                         in_=by_pass[:, 0, g2, sh],
                     )
-            col = P // 2
-            for g2 in range(PAIR):
                 for v in range(UNITS):
+                    here = GPSIMD_MASKS[v]
+                    gpsimd_cols[(g2, v)] = col
                     for sh in range(HALVES):
-                        for engine, (first_m, last_m) in enumerate(SHARES[v][sh]):
-                            width = CC * (last_m - first_m)
-                            mask_cols[(g2, v, sh, engine)] = col
-                            if width > 0:
+                        nc.vector.tensor_copy(
+                            out=mask_order[:, col : col + CC * HALVES * here].rearrange(
+                                "p (cc sh m) -> p cc sh m", cc=CC, sh=HALVES
+                            )[:, :, sh],
+                            in_=by_pass[:, 1, g2, sh, v, :, 0:here],
+                        )
+                    col += CC * HALVES * here
+                    for sh in range(HALVES):
+                        middle = VECTOR_END[v][sh]
+                        for first_m, last_m in ((here, middle), (middle, M)):
+                            if last_m > first_m:
+                                width = CC * (last_m - first_m)
+                                shared_cols[(g2, v, sh, first_m)] = col
                                 nc.vector.tensor_copy(
                                     out=mask_order[:, col : col + width].rearrange("p (cc m) -> p cc m", cc=CC),
                                     in_=by_pass[:, 1, g2, sh, v, :, first_m:last_m],
                                 )
-                            col += width
+                                col += width
 
         fold = const.tile([P, P], F32, name="fold")
         for half in range(2):
@@ -271,11 +279,16 @@ def tile_dynamicfeaturegroupinglayer_k_kernel(
             first = (g % PAIR * UNITS + v) * width
             return mask_of[g][:, first : first + width, :].rearrange("p (q m) t -> p q m t", m=M)
 
-        def shared_masks(n, sh, engine):
+        def gpsimd_masks(n):
             g, v = divmod(n, UNITS)
-            first_m, last_m = SHARES[v][sh][engine]
+            first = gpsimd_cols[(g % PAIR, v)]
+            width = CC * HALVES * GPSIMD_MASKS[v]
+            return mask_of[g][:, first : first + width, :].rearrange("p (q m) t -> p q m t", q=CC * HALVES)
+
+        def shared_masks(n, sh, first_m, last_m):
+            g, v = divmod(n, UNITS)
             width = CC * (last_m - first_m)
-            first = mask_cols[(g % PAIR, v, sh, engine)]
+            first = shared_cols[(g % PAIR, v, sh, first_m)]
             return mask_of[g][:, first : first + width, :].rearrange("p (cc m) t -> p cc m t", cc=CC)
 
         def turn_words(source, cp, bank_view, order):
@@ -304,51 +317,61 @@ def tile_dynamicfeaturegroupinglayer_k_kernel(
         def prepare_x_scalar(n, copy=nc.scalar.copy):
             x_sb = stage.tile([P, CC * P * PACK], BF16, name="x_grouped", tag="x_grouped")
             turn_and_group(x_loaded[n], 1, x_sb[:], unzip, copy)
-            x_ready[n] = x_sb[:].rearrange("p (cc sh b t) -> p cc sh b t", cc=CC, sh=HALVES, t=PACK)
+            x_ready[n] = x_sb[:].rearrange("p (q b t) -> p q b t", q=CC * HALVES, t=PACK)
 
         def prepare_x_vector(n):
             bank = x_banks.tile([P, CC, P, 2], F32, name="x_bank", tag="x_bank")
             turn_words(x_loaded[n], 0, bank[:].rearrange("p cc col u -> p cc u col"), unzip)
             x_psum[n] = bank[:].bitcast(BF16).rearrange("p cc (sh b) t -> p (cc sh) b t", sh=HALVES)
 
-        def by_mask(tile):
-            return tile[:].rearrange("p (cc sh m b t) -> p cc sh m b t", cc=CC, sh=HALVES, m=M, t=PACK)
-
-        def words_by_mask(tile):
-            return tile[:].bitcast(F32).rearrange("p (cc sh m b u) -> p cc sh m b u", cc=CC, sh=HALVES, m=M, u=2)
-
-        def gpsimd_multiply(n, sh):
-            if sh == 0:
-                shared = stage.tile([P, TILE], BF16, name="shared", tag="shared", bufs=1, align_bytes=64)
-                shared_of[n] = shared
-            first_m, last_m = SHARES[n % UNITS][sh][BY_GPSIMD]
-            shape = [P, CC, last_m - first_m, B, PACK]
+        def gpsimd_multiply(n):
+            shared = stage.tile([P, TILE], BF16, name="shared", tag="shared", bufs=1, align_bytes=64)
+            shared_of[n] = shared
+            masks_here = GPSIMD_MASKS[n % UNITS]
+            shape = [P, CC * HALVES, masks_here, B, PACK]
             nc.gpsimd.tensor_tensor(
-                out=by_mask(shared_of[n])[:, :, sh, first_m:last_m],
-                in0=x_ready[n][:, :, sh].unsqueeze(2).to_broadcast(shape),
-                in1=shared_masks(n, sh, BY_GPSIMD).unsqueeze(3).to_broadcast(shape),
+                out=shared[:].rearrange("p (q m b t) -> p q m b t", q=CC * HALVES, m=M, t=PACK)[:, :, 0:masks_here],
+                in0=x_ready[n].unsqueeze(2).to_broadcast(shape),
+                in1=gpsimd_masks(n).unsqueeze(3).to_broadcast(shape),
                 op=ALU.mult,
             )
 
+        def vector_share(n):
+            first_m = GPSIMD_MASKS[n % UNITS]
+            for sh in range(HALVES):
+                last_m = VECTOR_END[n % UNITS][sh]
+                if last_m > first_m:
+                    shape = [P, CC, last_m - first_m, B, PACK]
+                    nc.vector.tensor_tensor(
+                        out=shared_of[n][:].rearrange(
+                            "p (cc sh m b t) -> p cc sh m b t", cc=CC, sh=HALVES, m=M, t=PACK
+                        )[:, :, sh, first_m:last_m],
+                        in0=x_ready[n][:, sh : CC * HALVES : HALVES].unsqueeze(2).to_broadcast(shape),
+                        in1=shared_masks(n, sh, first_m, last_m).unsqueeze(3).to_broadcast(shape),
+                        op=ALU.mult,
+                    )
+
         def scalar_multiply(n, sh):
-            mask = shared_masks(n, sh, BY_SCALAR)
-            first_m, last_m = SHARES[n % UNITS][sh][BY_SCALAR]
-            planes = stage.tile([P, CC, last_m - first_m, 2, B, 2], BF16, name="planes", tag="planes")
+            first_m = VECTOR_END[n % UNITS][sh]
+            mask = shared_masks(n, sh, first_m, M)
+            planes = stage.tile([P, CC, M - first_m, 2, B, 2], BF16, name="planes", tag="planes")
             for cc in range(CC):
-                for m in range(last_m - first_m):
+                for m in range(M - first_m):
                     for t in range(PACK):
+                        u, e = divmod(t, 2)
                         nc.scalar.activation(
-                            out=planes[:, cc, m, t // 2, :, t % 2],
-                            in_=x_ready[n][:, cc, sh, :, t],
+                            out=planes[:, cc, m, u, :, e],
+                            in_=x_ready[n][:, cc * HALVES + sh, :, t],
                             func=FUNC.Copy,
                             scale=mask[:, cc, m, t : t + 1],
                         )
             planes_of[(n, sh)] = planes
 
         def scalar_regroup(n, sh):
-            first_m, last_m = SHARES[n % UNITS][sh][BY_SCALAR]
             nc.scalar.copy(
-                out=words_by_mask(shared_of[n])[:, :, sh, first_m:last_m],
+                out=shared_of[n][:].bitcast(F32).rearrange(
+                    "p (cc sh m b u) -> p cc sh m b u", cc=CC, sh=HALVES, m=M, u=2
+                )[:, :, sh, VECTOR_END[n % UNITS][sh] : M],
                 in_=planes_of[(n, sh)][:].bitcast(F32).rearrange("p cc m u b one -> p cc m b (u one)"),
             )
 
@@ -372,18 +395,6 @@ def tile_dynamicfeaturegroupinglayer_k_kernel(
                 op=ALU.mult,
             )
             return weighted
-
-        def vector_share(n):
-            for sh in range(HALVES):
-                first_m, last_m = SHARES[n % UNITS][sh][BY_VECTOR]
-                if last_m > first_m:
-                    shape = [P, CC, last_m - first_m, B, PACK]
-                    nc.vector.tensor_tensor(
-                        out=by_mask(shared_of[n])[:, :, sh, first_m:last_m],
-                        in0=x_ready[n][:, :, sh].unsqueeze(2).to_broadcast(shape),
-                        in1=shared_masks(n, sh, BY_VECTOR).unsqueeze(3).to_broadcast(shape),
-                        op=ALU.mult,
-                    )
 
         def contract(n, cp, weighted, first_cc=0, last_cc=CC):
             v = n % UNITS
@@ -423,17 +434,18 @@ def tile_dynamicfeaturegroupinglayer_k_kernel(
             sums_of = dict(acc)
             kept = {}
 
-            def empty():
-                for mt in range(2):
-                    raw = small.tile([P, P], F32, name="raw%d" % mt, tag="raw%d" % mt)
-                    nc.scalar.copy(out=raw[:], in_=sums_of[mt][:])
-                    sums_of[mt] = raw
-
             def statistics():
                 for mt in range(2):
                     nc.vector.bn_stats(
                         out=stats[:, 2 * mt : 2 * mt + 2, :].rearrange("p w k -> p (w k)"), in_=sums_of[mt][:]
                     )
+                for mt in range(2):
+                    for w in range(2):
+                        nc.vector.scalar_tensor_tensor(
+                            out=normed[:, mt, w, :], in0=sums_of[mt][:, w:P:2],
+                            scalar=stats[:, 2 * mt + w, 1:2], in1=affine[:, 0, w, g, :],
+                            op0=ALU.subtract, op1=ALU.mult,
+                        )
 
             def power():
                 var_eps = small.tile([P, LN_ROWS], F32, name="var_eps", tag="var_eps")
@@ -443,12 +455,6 @@ def tile_dynamicfeaturegroupinglayer_k_kernel(
                 nc.gpsimd.tensor_tensor(out=rstd[:], in0=var_eps[:], in1=rsqrt_power[:], op=ALU.pow)
 
             def normalise():
-                for mt in range(2):
-                    for w in range(2):
-                        nc.vector.scalar_tensor_tensor(
-                            out=normed[:, mt, w, :], in0=sums_of[mt][:, w:P:2], scalar=stats[:, 2 * mt + w, 1:2],
-                            in1=affine[:, 0, w, g, :], op0=ALU.subtract, op1=ALU.mult,
-                        )
                 for mt in range(2):
                     for w in range(2):
                         i = 2 * mt + w
@@ -479,7 +485,7 @@ def tile_dynamicfeaturegroupinglayer_k_kernel(
                 nc.scalar.copy(out=result[0:B], in_=kept["sums"][0:B, 0:H])
                 results[g] = result
 
-            return statistics, empty, power, normalise, activate, gate, add_masks, finish
+            return statistics, power, normalise, activate, gate, add_masks, finish
 
         def store(g):
             nc.sync.dma_start(out=out[:, g * H : (g + 1) * H], in_=results[g][0:B])
@@ -518,10 +524,11 @@ def tile_dynamicfeaturegroupinglayer_k_kernel(
             for work in todo.get((n, slot), []):
                 work()
 
-        for k, (n, slot) in enumerate(((1, 0), (1, 2), (1, 3), (2, 0), (2, 2))):
+        for k, (n, slot) in enumerate(((0, 0), (0, 3), (1, 0), (1, 2), (1, 3))):
             put(n, slot, lambda first=k * BANK: spread(first))
         for pair in range(1, G // PAIR):
-            n = (pair - 1) * PAIR * UNITS
+            last = pair * PAIR * UNITS - (3 if pair > 1 else 2)
+            n = max(last - 3, 0)
             (
                 pass_maxima, spread_maxima, row_maxima, exponentials, row_sums, power, scale, turn, keep
             ) = entmax_steps(pair)
@@ -530,33 +537,31 @@ def tile_dynamicfeaturegroupinglayer_k_kernel(
             put(n, 2, row_maxima)
             put(n, 3, exponentials)
             put(n + 1, 1, row_sums)
-            put(n + 2, "gpsimd", power)
-            put(n + 2, 1, scale)
-            put(n + 2, 3, turn)
-            put(n + 2, 3, keep)
+            put(last, "gpsimd", power)
+            put(last, 1, scale)
+            put(last, 3, turn)
+            put(last, 3, keep)
 
         for n in range(N_UNITS):
             more = n + 1 < N_UNITS
             if n + LOAD_AHEAD < N_UNITS:
                 load(n + LOAD_AHEAD)
-            if n % (PAIR * UNITS) == 1 and n // UNITS + 2 * PAIR < G:
+            if n % (PAIR * UNITS) == 0 and n // UNITS + 2 * PAIR < G:
                 load_logits(n // UNITS // PAIR + 2)
             if n > 0 and n % UNITS == 0:
                 done = n // UNITS - 1
-                statistics, empty, power, normalise, activate, gate, add_masks, finish = layer_norm_steps(done)
+                statistics, power, normalise, activate, gate, add_masks, finish = layer_norm_steps(done)
                 put(n, 0, statistics)
-                put(n, 0, empty)
                 put(n + 1, "gpsimd", power)
                 put(n + 1, 2, normalise)
                 put(n + 1, 3, activate)
-                put(n + 2, 0, gate)
+                put(n + 2, 1, gate)
                 put(n + 2, 2, add_masks)
                 put(n + 2, 3, finish)
                 put(n + 3, 0, lambda done=done: store(done))
             weighted = vector_multiply(n)
-            gpsimd_multiply(n, 0)
+            gpsimd_multiply(n)
             run(n, "gpsimd")
-            gpsimd_multiply(n, 1)
             scalar_regroup(n, 0)
             scalar_regroup(n, 1)
             if more:
@@ -584,10 +589,9 @@ def tile_dynamicfeaturegroupinglayer_k_kernel(
                     contract(n, 1, shared_of[n], cc, cc + 1)
             run(n, 3)
 
-        for slot in (0, 2, 3):
+        for slot in (1, 2, 3):
             run(N_UNITS, slot)
         run(N_UNITS + 1, 0)
-        statistics, empty, power, normalise, activate, gate, add_masks, finish = layer_norm_steps(G - 1)
-        for step in (statistics, power, normalise, activate, gate, add_masks, finish):
+        for step in layer_norm_steps(G - 1):
             step()
         store(G - 1)

@@ -31,12 +31,13 @@ PASSES = S // K_PASS
 SHV = HALVES * UNITS
 CC = 2
 TILE = CC * HALVES * M * B * PACK
-GPSIMD_MASKS = (2, 1)
-VECTOR_END = ((2, 2), (2, 1))
+M2 = M // 2
 LOAD_AHEAD = 3
 PAIR = 2
 PAIR_ROWS = PAIR * M
+MASK_BATCHES = ((0,), (1, 2), (3, 4))
 LN_ROWS = 4
+LN_BATCHES = ((0, 1, 2, 3), (4, 5, 6, 7), (8,), (9,))
 
 
 def tile_dynamicfeaturegroupinglayer_k_kernel(
@@ -58,15 +59,16 @@ def tile_dynamicfeaturegroupinglayer_k_kernel(
         x_psum, x_ready, w_ready, w_quantised = {}, {}, {}, {}
         acc, mask_of, planes_of, shared_of = {}, {}, {}, {}
 
-        def load_logits(pair):
-            logits = small.tile([P, K_PASS], BF16, name="logits", tag="logits")
-            nc.sync.dma_start(
-                out=logits[:],
-                in_=W_masks[PAIR * pair : PAIR * (pair + 1)]
-                .rearrange("g m s -> (g m s)")
-                .rearrange("(rc f) -> rc f", f=K_PASS),
-            )
-            logits_of[pair] = logits
+        def load_logits(pairs):
+            logits = small.tile([P, len(pairs), K_PASS], BF16, name="logits", tag="logits%d" % len(pairs))
+            for i, pair in enumerate(pairs):
+                nc.sync.dma_start(
+                    out=logits[:, i, :],
+                    in_=W_masks[PAIR * pair : PAIR * (pair + 1)]
+                    .rearrange("g m s -> (g m s)")
+                    .rearrange("(rc f) -> rc f", f=K_PASS),
+                )
+            logits_of[pairs] = logits
 
         def load(n):
             g, v = divmod(n, UNITS)
@@ -82,7 +84,7 @@ def tile_dynamicfeaturegroupinglayer_k_kernel(
                 nc.sync.dma_start(out=w_sb[1:P:2, :], in_=W2[g, :, first : first + UNIT_K])
                 w_loaded[(n, sh)] = w_sb
 
-        load_logits(0)
+        load_logits(MASK_BATCHES[0])
         load(0)
 
         ident = const.tile([P, P], F32, name="ident")
@@ -97,12 +99,12 @@ def tile_dynamicfeaturegroupinglayer_k_kernel(
                 out=exp_scales[:, col : col + 1], in0=zero[:, 0:1], scalar1=0.0, scalar2=value,
                 op0=ALU.mult, op1=ALU.add,
             )
-        norm_power = const.tile([P, 1], F32, name="norm_power")
+        norm_power = const.tile([P, 2], F32, name="norm_power")
         nc.vector.tensor_scalar(
-            out=norm_power[:], in0=zero[:, 0:1], scalar1=0.0, scalar2=-1.0 / ALPHA,
+            out=norm_power[:], in0=zero[:, 0:2], scalar1=0.0, scalar2=-1.0 / ALPHA,
             op0=ALU.mult, op1=ALU.add,
         )
-        rsqrt_power = const.tile([P, LN_ROWS], F32, name="rsqrt_power")
+        rsqrt_power = const.tile([P, 4 * LN_ROWS], F32, name="rsqrt_power")
         nc.vector.memset(rsqrt_power[:], -0.5)
         row_of = const.tile([P, PAIR_ROWS], F32, name="row_of")
         nc.vector.tensor_reduce(
@@ -123,155 +125,136 @@ def tile_dynamicfeaturegroupinglayer_k_kernel(
             in_=ident[:].rearrange("p (a h) -> p h a", h=2),
         )
         mask_order = const.tile([P, P], F32, name="mask_order")
-        by_pass = ident[:].rearrange(
-            "p (g2 m sh v cp cc) -> p cp g2 sh v cc m", g2=PAIR, m=M, sh=HALVES, v=UNITS, cp=2
-        )
-        gpsimd_cols = {}
-        shared_cols = {}
 
         def order_masks():
-            col = P // 2
+            by_pass = ident[:].rearrange(
+                "p (g2 m sh v cp cc) -> p cp g2 sh v cc m", g2=PAIR, m=M, sh=HALVES, v=UNITS, cp=2
+            )
+            vector_order = mask_order[:, 0 : P // 2].rearrange(
+                "p (g2 v cc sh m) -> p g2 sh v cc m", g2=PAIR, v=UNITS, cc=CC, sh=HALVES
+            )
+            shared_order = mask_order[:, P // 2 : P].rearrange(
+                "p (mh g2 v cc sh ml) -> p mh g2 sh v cc ml", mh=2, g2=PAIR, v=UNITS, cc=CC, sh=HALVES
+            )
             for g2 in range(PAIR):
                 for sh in range(HALVES):
-                    nc.vector.tensor_copy(
-                        out=mask_order[:, 0 : P // 2].rearrange(
-                            "p (g2 v cc sh m) -> p g2 sh v cc m", g2=PAIR, v=UNITS, cc=CC, sh=HALVES
-                        )[:, g2, sh],
-                        in_=by_pass[:, 0, g2, sh],
-                    )
-                for v in range(UNITS):
-                    here = GPSIMD_MASKS[v]
-                    gpsimd_cols[(g2, v)] = col
-                    for sh in range(HALVES):
+                    nc.vector.tensor_copy(out=vector_order[:, g2, sh], in_=by_pass[:, 0, g2, sh])
+                    for mh in range(2):
                         nc.vector.tensor_copy(
-                            out=mask_order[:, col : col + CC * HALVES * here].rearrange(
-                                "p (cc sh m) -> p cc sh m", cc=CC, sh=HALVES
-                            )[:, :, sh],
-                            in_=by_pass[:, 1, g2, sh, v, :, 0:here],
+                            out=shared_order[:, mh, g2, sh],
+                            in_=by_pass[:, 1, g2, sh, :, :, mh * M2 : (mh + 1) * M2],
                         )
-                    col += CC * HALVES * here
-                    for sh in range(HALVES):
-                        middle = VECTOR_END[v][sh]
-                        for first_m, last_m in ((here, middle), (middle, M)):
-                            if last_m > first_m:
-                                width = CC * (last_m - first_m)
-                                shared_cols[(g2, v, sh, first_m)] = col
-                                nc.vector.tensor_copy(
-                                    out=mask_order[:, col : col + width].rearrange("p (cc m) -> p cc m", cc=CC),
-                                    in_=by_pass[:, 1, g2, sh, v, :, first_m:last_m],
-                                )
-                                col += width
 
         fold = const.tile([P, P], F32, name="fold")
         for half in range(2):
             nc.vector.tensor_tensor(
                 out=fold[:, half * H : (half + 1) * H], in0=ident[:, 0:H], in1=ident[:, H : 2 * H], op=ALU.add
             )
-        ln_rows = const.tile([P, 4 * G * H], BF16, name="ln_rows")
-        nc.gpsimd.memset(ln_rows[:], 0.0)
-        ones = const.tile([P, P], BF16, name="ones")
-        nc.gpsimd.memset(ones[:], 1.0)
-        affine = const.tile([P, 2, 2, G, H], F32, name="affine")
-        affine_flat = affine[:].rearrange("p k w g j -> p (k w g j)")
+        affine = const.tile([P, 2, 2, G * H], BF16, name="affine")
 
         load(1)
-        load_logits(1)
+        load_logits(MASK_BATCHES[1])
         for n in range(2, LOAD_AHEAD):
             load(n)
         for n, vec in enumerate((ln1_w, ln2_w, ln1_b, ln2_b)):
             nc.sync.dma_start(
-                out=ln_rows[0:1, n * G * H : (n + 1) * G * H],
-                in_=vec.rearrange("g j -> (g j)").unsqueeze(0),
+                out=affine[:, n // 2, n % 2, :], in_=vec.rearrange("g j -> (g j)").partition_broadcast(P)
             )
 
-        def spread(first):
-            bank = banks.tile([P, BANK], F32, name="bank", tag="bank")
-            nc.tensor.matmul(
-                out=bank[:], lhsT=ones[:], rhs=ln_rows[:, first : first + BANK], start=True, stop=True
-            )
-            nc.scalar.copy(out=affine_flat[:, first : first + BANK], in_=bank[:])
-
-        def entmax_steps(pair):
+        def entmax_steps(pairs):
+            count = len(pairs)
             kept = {}
 
+            def stat(name, *shape):
+                tile = small.tile([P, count] + list(shape), F32, name=name, tag="%s%d" % (name, count))
+                kept[name] = tile
+                return tile
+
             def pass_maxima():
-                pass_max = small.tile([P, 1], F32, name="pass_max", tag="pass_max")
-                nc.vector.tensor_reduce(out=pass_max[:], in_=logits_of[pair][:], axis=AXIS_X, op=ALU.max)
-                kept["pass_max"] = pass_max
+                nc.vector.tensor_reduce(
+                    out=stat("pass_max")[:], in_=logits_of[pairs][:], axis=AXIS_X, op=ALU.max
+                )
 
             def spread_maxima():
                 bank = banks.tile([P, BANK], F32, name="bank", tag="bank")
-                nc.tensor.matmul(
-                    out=bank[:, 0:P], lhsT=kept["pass_max"][:, 0:1].to_broadcast([P, P]), rhs=ident[:],
-                    start=True, stop=True,
-                )
+                for i in range(count):
+                    nc.tensor.matmul(
+                        out=bank[:, i * P : (i + 1) * P],
+                        lhsT=kept["pass_max"][:, i : i + 1].to_broadcast([P, P]),
+                        rhs=ident[:], start=True, stop=True,
+                    )
                 kept["maxima"] = bank
 
             def row_maxima():
-                own = small.tile([P, P], F32, name="own", tag="own")
-                nc.vector.tensor_tensor(out=own[:], in0=kept["maxima"][:, 0:P], in1=other_rows[:], op=ALU.add)
-                row_max = small.tile([P, 1], F32, name="row_max", tag="row_max")
-                nc.vector.tensor_reduce(out=row_max[:], in_=own[:], axis=AXIS_X, op=ALU.max)
-                biases = small.tile([P, 2], F32, name="biases", tag="biases")
+                own = stat("own", P)
                 nc.vector.tensor_tensor(
-                    out=biases[:], in0=row_max[:].to_broadcast([P, 2]), in1=exp_scales[:], op=ALU.mult
+                    out=own[:],
+                    in0=kept["maxima"][:, 0 : count * P].rearrange("p (i n) -> p i n", i=count),
+                    in1=other_rows[:].unsqueeze(1).to_broadcast([P, count, P]), op=ALU.add,
                 )
-                kept["biases"] = biases
+                row_max = stat("row_max")
+                nc.vector.tensor_reduce(out=row_max[:], in_=own[:], axis=AXIS_X, op=ALU.max)
+                nc.vector.tensor_tensor(
+                    out=stat("biases", 2)[:], in0=row_max[:].unsqueeze(2).to_broadcast([P, count, 2]),
+                    in1=exp_scales[:].unsqueeze(1).to_broadcast([P, count, 2]), op=ALU.mult,
+                )
+                stat("e", K_PASS)
+                stat("pass_sum")
 
-            def exponentials():
+            def exponentials(i):
                 powers = small.tile([P, K_PASS], F32, name="powers", tag="powers")
-                pass_sum = small.tile([P, 1], F32, name="pass_sum", tag="pass_sum")
                 nc.scalar.activation(
-                    out=powers[:], in_=logits_of[pair][:], func=FUNC.Exp, scale=ALPHA,
-                    bias=kept["biases"][:, 0:1], accum_out=pass_sum[:],
+                    out=powers[:], in_=logits_of[pairs][:, i, :], func=FUNC.Exp, scale=ALPHA,
+                    bias=kept["biases"][:, i, 0:1], accum_out=kept["pass_sum"][:, i : i + 1],
                 )
-                e = small.tile([P, K_PASS], F32, name="e", tag="e")
                 nc.scalar.activation(
-                    out=e[:], in_=logits_of[pair][:], func=FUNC.Exp, bias=kept["biases"][:, 1:2]
+                    out=kept["e"][:, i, :], in_=logits_of[pairs][:, i, :], func=FUNC.Exp,
+                    bias=kept["biases"][:, i, 1:2],
                 )
-                kept["e"], kept["pass_sum"] = e, pass_sum
 
             def row_sums():
                 bank = banks.tile([P, BANK], F32, name="bank", tag="bank")
                 nc.tensor.matmul(
-                    out=bank[:, 0:1], lhsT=block[:], rhs=kept["pass_sum"][:], start=True, stop=True
+                    out=bank[:, 0:count], lhsT=block[:], rhs=kept["pass_sum"][:], start=True, stop=True
                 )
-                padded = small.tile([P, 1], F32, name="padded", tag="padded")
-                nc.scalar.activation(out=padded[:], in_=bank[:, 0:1], func=FUNC.Copy, bias=EPS)
-                kept["padded"] = padded
+                nc.scalar.activation(
+                    out=stat("padded")[:], in_=bank[:, 0:count], func=FUNC.Copy, bias=EPS
+                )
 
             def power():
-                inv_norm = small.tile([P, 1], F32, name="inv_norm", tag="inv_norm")
-                nc.gpsimd.tensor_tensor(out=inv_norm[:], in0=kept["padded"][:], in1=norm_power[:], op=ALU.pow)
-                kept["inv_norm"] = inv_norm
+                nc.gpsimd.tensor_tensor(
+                    out=stat("inv_norm")[:], in0=kept["padded"][:], in1=norm_power[:, 0:count], op=ALU.pow
+                )
 
-            def scale():
+            def scale(i):
                 by_row = small.tile([P, K_PASS], F32, name="by_row", tag="by_row")
                 nc.scalar.activation(
-                    out=by_row[:], in_=kept["e"][:], func=FUNC.Copy, scale=kept["inv_norm"][:, 0:1]
+                    out=by_row[:], in_=kept["e"][:, i, :], func=FUNC.Copy,
+                    scale=kept["inv_norm"][:, i : i + 1],
                 )
-                kept["by_row"] = by_row
+                kept[("by_row", i)] = by_row
 
-            def turn():
+            def turn(i):
                 bank = banks.tile([P, P, PACK], F32, name="mask_bank", tag="bank")
                 for t in range(PACK):
                     u, e = divmod(t, 2)
                     nc.tensor.transpose(
                         out=bank[:, :, t],
-                        in_=kept["by_row"][:, 2 * P * u + e : 2 * P * (u + 1) : 2],
+                        in_=kept[("by_row", i)][:, 2 * P * u + e : 2 * P * (u + 1) : 2],
                         identity=mask_order[:],
                     )
-                kept["mask"] = bank
-
-            def keep():
                 mask = small.tile([P, P, PACK], F32, name="mask", tag="mask")
-                nc.scalar.copy(out=mask[:], in_=kept["mask"][:])
+                nc.scalar.copy(out=mask[:], in_=bank[:])
                 for g2 in range(PAIR):
-                    mask_of[PAIR * pair + g2] = mask
+                    mask_of[PAIR * pairs[i] + g2] = mask
 
-            return (
-                pass_maxima, spread_maxima, row_maxima, exponentials, row_sums, power, scale, turn, keep
-            )
+            return {
+                "pass_maxima": pass_maxima, "spread_maxima": spread_maxima, "row_maxima": row_maxima,
+                "exponentials": [lambda i=i: exponentials(i) for i in range(count)],
+                "row_sums": row_sums, "power": power,
+                "scale": [lambda i=i: scale(i) for i in range(count)],
+                "turn": [lambda i=i: turn(i) for i in range(count)],
+            }
 
         def vector_masks(n):
             g, v = divmod(n, UNITS)
@@ -279,17 +262,11 @@ def tile_dynamicfeaturegroupinglayer_k_kernel(
             first = (g % PAIR * UNITS + v) * width
             return mask_of[g][:, first : first + width, :].rearrange("p (q m) t -> p q m t", m=M)
 
-        def gpsimd_masks(n):
+        def shared_masks(n, mh):
             g, v = divmod(n, UNITS)
-            first = gpsimd_cols[(g % PAIR, v)]
-            width = CC * HALVES * GPSIMD_MASKS[v]
-            return mask_of[g][:, first : first + width, :].rearrange("p (q m) t -> p q m t", q=CC * HALVES)
-
-        def shared_masks(n, sh, first_m, last_m):
-            g, v = divmod(n, UNITS)
-            width = CC * (last_m - first_m)
-            first = shared_cols[(g % PAIR, v, sh, first_m)]
-            return mask_of[g][:, first : first + width, :].rearrange("p (cc m) t -> p cc m t", cc=CC)
+            width = CC * HALVES * M2
+            first = P // 2 + ((mh * PAIR + g % PAIR) * UNITS + v) * width
+            return mask_of[g][:, first : first + width, :].rearrange("p (q ml) t -> p q ml t", ml=M2)
 
         def turn_words(source, cp, bank_view, order):
             words = source[:].bitcast(F32)
@@ -327,52 +304,34 @@ def tile_dynamicfeaturegroupinglayer_k_kernel(
         def gpsimd_multiply(n):
             shared = stage.tile([P, TILE], BF16, name="shared", tag="shared", bufs=1, align_bytes=64)
             shared_of[n] = shared
-            masks_here = GPSIMD_MASKS[n % UNITS]
-            shape = [P, CC * HALVES, masks_here, B, PACK]
+            shape = [P, CC * HALVES, M2, B, PACK]
             nc.gpsimd.tensor_tensor(
-                out=shared[:].rearrange("p (q m b t) -> p q m b t", q=CC * HALVES, m=M, t=PACK)[:, :, 0:masks_here],
+                out=shared[:].rearrange("p (q m b t) -> p q m b t", q=CC * HALVES, m=M, t=PACK)[:, :, 0:M2],
                 in0=x_ready[n].unsqueeze(2).to_broadcast(shape),
-                in1=gpsimd_masks(n).unsqueeze(3).to_broadcast(shape),
+                in1=shared_masks(n, 0).unsqueeze(3).to_broadcast(shape),
                 op=ALU.mult,
             )
 
-        def vector_share(n):
-            first_m = GPSIMD_MASKS[n % UNITS]
-            for sh in range(HALVES):
-                last_m = VECTOR_END[n % UNITS][sh]
-                if last_m > first_m:
-                    shape = [P, CC, last_m - first_m, B, PACK]
-                    nc.vector.tensor_tensor(
-                        out=shared_of[n][:].rearrange(
-                            "p (cc sh m b t) -> p cc sh m b t", cc=CC, sh=HALVES, m=M, t=PACK
-                        )[:, :, sh, first_m:last_m],
-                        in0=x_ready[n][:, sh : CC * HALVES : HALVES].unsqueeze(2).to_broadcast(shape),
-                        in1=shared_masks(n, sh, first_m, last_m).unsqueeze(3).to_broadcast(shape),
-                        op=ALU.mult,
-                    )
-
-        def scalar_multiply(n, sh):
-            first_m = VECTOR_END[n % UNITS][sh]
-            mask = shared_masks(n, sh, first_m, M)
-            planes = stage.tile([P, CC, M - first_m, 2, B, 2], BF16, name="planes", tag="planes")
-            for cc in range(CC):
-                for m in range(M - first_m):
+        def scalar_multiply(n, cc):
+            if cc == 0:
+                planes = stage.tile([P, CC * HALVES, M2, 2, B, 2], BF16, name="planes", tag="planes", bufs=2)
+                planes_of[n] = planes
+            mask = shared_masks(n, 1)
+            for q in range(cc * HALVES, (cc + 1) * HALVES):
+                for ml in range(M2):
                     for t in range(PACK):
                         u, e = divmod(t, 2)
                         nc.scalar.activation(
-                            out=planes[:, cc, m, u, :, e],
-                            in_=x_ready[n][:, cc * HALVES + sh, :, t],
-                            func=FUNC.Copy,
-                            scale=mask[:, cc, m, t : t + 1],
+                            out=planes_of[n][:, q, ml, u, :, e], in_=x_ready[n][:, q, :, t],
+                            func=FUNC.Copy, scale=mask[:, q, ml, t : t + 1],
                         )
-            planes_of[(n, sh)] = planes
 
-        def scalar_regroup(n, sh):
+        def scalar_regroup(n):
             nc.scalar.copy(
                 out=shared_of[n][:].bitcast(F32).rearrange(
-                    "p (cc sh m b u) -> p cc sh m b u", cc=CC, sh=HALVES, m=M, u=2
-                )[:, :, sh, VECTOR_END[n % UNITS][sh] : M],
-                in_=planes_of[(n, sh)][:].bitcast(F32).rearrange("p cc m u b one -> p cc m b (u one)"),
+                    "p (q m b u) -> p q m b u", q=CC * HALVES, m=M, u=2
+                )[:, :, M2:M],
+                in_=planes_of[n][:].bitcast(F32).rearrange("p q ml u b one -> p q ml b (u one)"),
             )
 
         def quantise(values, tag):
@@ -422,93 +381,108 @@ def tile_dynamicfeaturegroupinglayer_k_kernel(
                         stop=(v, cp, q) == (UNITS - 1, 1, CC * HALVES - 1),
                     )
 
-        results = {}
-
-        def layer_norm_steps(g):
-            stats = small.tile([P, LN_ROWS, 3], F32, name="stats", tag="stats")
-            rstd = small.tile([P, LN_ROWS], F32, name="rstd", tag="rstd")
-            normed = small.tile([P, 2, 2, H], F32, name="normed", tag="normed")
-            half_tanh = small.tile([P, 2, H], F32, name="half_tanh", tag="half_tanh")
-            half_relu = small.tile([P, 2, H], F32, name="half_relu", tag="half_relu")
-            gated = small.tile([P, 2, H], F32, name="gated", tag="gated")
-            sums_of = dict(acc)
+        def layer_norm_steps(groups):
+            count = len(groups)
             kept = {}
 
-            def statistics():
+            def stat(name, *shape):
+                tile = small.tile([P] + list(shape), F32, name=name, tag="%s%d" % (name, count))
+                kept[name] = tile
+                return tile
+
+            def statistics(i):
+                if i == 0:
+                    stat("stats", 2, count, 2, 3)
+                    stat("normed", 2, count, 2, H)
+                stats, normed = kept["stats"], kept["normed"]
                 for mt in range(2):
                     nc.vector.bn_stats(
-                        out=stats[:, 2 * mt : 2 * mt + 2, :].rearrange("p w k -> p (w k)"), in_=sums_of[mt][:]
+                        out=stats[:, mt, i].rearrange("p w k -> p (w k)"), in_=acc[mt][:]
                     )
                 for mt in range(2):
                     for w in range(2):
                         nc.vector.scalar_tensor_tensor(
-                            out=normed[:, mt, w, :], in0=sums_of[mt][:, w:P:2],
-                            scalar=stats[:, 2 * mt + w, 1:2], in1=affine[:, 0, w, g, :],
+                            out=normed[:, mt, i, w, :], in0=acc[mt][:, w:P:2],
+                            scalar=stats[:, mt, i, w, 1:2],
+                            in1=affine[:, 0, w, groups[i] * H : (groups[i] + 1) * H],
                             op0=ALU.subtract, op1=ALU.mult,
                         )
 
             def power():
-                var_eps = small.tile([P, LN_ROWS], F32, name="var_eps", tag="var_eps")
+                var_eps = stat("var_eps", 2, count, 2)
                 nc.gpsimd.tensor_scalar(
-                    out=var_eps[:], in0=stats[:, :, 2], scalar1=1.0 / H, scalar2=EPS, op0=ALU.mult, op1=ALU.add
+                    out=var_eps[:], in0=kept["stats"][:, :, :, :, 2], scalar1=1.0 / H, scalar2=EPS,
+                    op0=ALU.mult, op1=ALU.add,
                 )
-                nc.gpsimd.tensor_tensor(out=rstd[:], in0=var_eps[:], in1=rsqrt_power[:], op=ALU.pow)
+                nc.gpsimd.tensor_tensor(
+                    out=stat("rstd", 2, count, 2)[:].rearrange("p mt i w -> p (mt i w)"),
+                    in0=var_eps[:].rearrange("p mt i w -> p (mt i w)"),
+                    in1=rsqrt_power[:, 0 : count * LN_ROWS], op=ALU.pow,
+                )
 
-            def normalise():
+            def normalise(i):
+                normed, rstd = kept["normed"], kept["rstd"]
                 for mt in range(2):
                     for w in range(2):
-                        i = 2 * mt + w
                         nc.vector.scalar_tensor_tensor(
-                            out=normed[:, mt, w, :], in0=normed[:, mt, w, :], scalar=rstd[:, i : i + 1],
-                            in1=affine[:, 1, w, g, :], op0=ALU.mult, op1=ALU.add,
+                            out=normed[:, mt, i, w, :], in0=normed[:, mt, i, w, :],
+                            scalar=rstd[:, mt, i, w : w + 1],
+                            in1=affine[:, 1, w, groups[i] * H : (groups[i] + 1) * H],
+                            op0=ALU.mult, op1=ALU.add,
                         )
 
             def activate():
-                nc.scalar.activation(out=half_tanh[:], in_=normed[:, :, 0, :], func=FUNC.Tanh, scale=0.5)
-                nc.scalar.activation(out=half_relu[:], in_=normed[:, :, 1, :], func=FUNC.Relu, scale=0.5)
+                for name, w, func in (("half_tanh", 0, FUNC.Tanh), ("half_relu", 1, FUNC.Relu)):
+                    nc.scalar.activation(
+                        out=stat(name, 2 * count, H)[:],
+                        in_=kept["normed"][:].rearrange("p mt i w j -> p (mt i) w j")[:, :, w, :],
+                        func=func, scale=0.5,
+                    )
 
             def gate():
                 nc.vector.scalar_tensor_tensor(
-                    out=gated[:], in0=half_tanh[:], scalar=1.0, in1=half_relu[:], op0=ALU.add, op1=ALU.mult
+                    out=stat("gated", 2 * count, H)[:], in0=kept["half_tanh"][:], scalar=1.0,
+                    in1=kept["half_relu"][:], op0=ALU.add, op1=ALU.mult,
                 )
 
             def add_masks():
                 bank = banks.tile([P, BANK], F32, name="bank", tag="bank")
-                kept["sums"] = bank
+                gated = kept["gated"][:].rearrange("p (mt i) j -> p mt (i j)", mt=2)
                 for mt in range(2):
                     nc.tensor.matmul(
-                        out=bank[:, 0:H], lhsT=fold[:], rhs=gated[:, mt, :], start=(mt == 0), stop=(mt == 1)
+                        out=bank[:, 0 : count * H], lhsT=fold[:], rhs=gated[:, mt],
+                        start=(mt == 0), stop=(mt == 1),
                     )
+                result = stat("result", count * H)
+                nc.scalar.copy(out=result[0:B], in_=bank[0:B, 0 : count * H])
 
-            def finish():
-                result = small.tile([P, H], F32, name="result", tag="result")
-                nc.scalar.copy(out=result[0:B], in_=kept["sums"][0:B, 0:H])
-                results[g] = result
+            def store():
+                nc.sync.dma_start(
+                    out=out[:, groups[0] * H : (groups[-1] + 1) * H], in_=kept["result"][0:B]
+                )
 
-            return statistics, power, normalise, activate, gate, add_masks, finish
+            return {
+                "statistics": [lambda i=i: statistics(i) for i in range(count)], "power": power,
+                "normalise": [lambda i=i: normalise(i) for i in range(count)],
+                "activate": activate, "gate": gate, "add_masks": add_masks, "store": store,
+            }
 
-        def store(g):
-            nc.sync.dma_start(out=out[:, g * H : (g + 1) * H], in_=results[g][0:B])
-
-        (
-            pass_maxima, spread_maxima, row_maxima, exponentials, row_sums, power, scale, turn, keep
-        ) = entmax_steps(0)
-        pass_maxima()
-        spread_maxima()
-        row_maxima()
+        first_masks = entmax_steps(MASK_BATCHES[0])
+        first_masks["pass_maxima"]()
+        first_masks["spread_maxima"]()
+        first_masks["row_maxima"]()
         order_masks()
-        exponentials()
+        first_masks["exponentials"][0]()
         prepare_w(0, 0, 0, nc.vector.tensor_copy)
         prepare_w(0, 0, 1, nc.vector.tensor_copy)
-        row_sums()
+        first_masks["row_sums"]()
         prepare_x_scalar(0, nc.vector.tensor_copy)
-        power()
+        first_masks["power"]()
         prepare_w(0, 1, 0, nc.vector.tensor_copy)
         prepare_w(0, 1, 1, nc.vector.tensor_copy)
-        scale()
+        first_masks["scale"][0]()
         prepare_x_vector(0)
-        turn()
-        keep()
+        first_masks["turn"][0]()
         quantise_w(0)
         scalar_multiply(0, 0)
         scalar_multiply(0, 1)
@@ -524,46 +498,44 @@ def tile_dynamicfeaturegroupinglayer_k_kernel(
             for work in todo.get((n, slot), []):
                 work()
 
-        for k, (n, slot) in enumerate(((0, 0), (0, 3), (1, 0), (1, 2), (1, 3))):
-            put(n, slot, lambda first=k * BANK: spread(first))
-        for pair in range(1, G // PAIR):
-            last = pair * PAIR * UNITS - (3 if pair > 1 else 2)
-            n = max(last - 3, 0)
-            (
-                pass_maxima, spread_maxima, row_maxima, exponentials, row_sums, power, scale, turn, keep
-            ) = entmax_steps(pair)
-            put(n, 0, pass_maxima)
-            put(n, 1, spread_maxima)
-            put(n, 2, row_maxima)
-            put(n, 3, exponentials)
-            put(n + 1, 1, row_sums)
-            put(last, "gpsimd", power)
-            put(last, 1, scale)
-            put(last, 3, turn)
-            put(last, 3, keep)
+        for pairs in MASK_BATCHES[1:]:
+            n = (pairs[0] - 1) * PAIR * UNITS
+            steps = entmax_steps(pairs)
+            put(n, 0, steps["pass_maxima"])
+            put(n, 1, steps["spread_maxima"])
+            put(n, 2, steps["row_maxima"])
+            put(n, 3, steps["exponentials"][0])
+            put(n + 1, 1, steps["exponentials"][1])
+            put(n + 1, 3, steps["row_sums"])
+            put(n + 2, "gpsimd", steps["power"])
+            put(n + 2, 1, steps["scale"][0])
+            put(n + 2, 3, steps["turn"][0])
+            put(n + 3, 1, steps["scale"][1])
+            put(n + 3, 3, steps["turn"][1])
+        for groups in LN_BATCHES[:-1]:
+            steps = layer_norm_steps(groups)
+            for i, g in enumerate(groups):
+                put((g + 1) * UNITS, 0, steps["statistics"][i])
+            n = (groups[-1] + 1) * UNITS + 1
+            put(n, "gpsimd", steps["power"])
+            for i in range(len(groups)):
+                put(n, 2, steps["normalise"][i])
+            put(n, 3, steps["activate"])
+            put(n + 1, 1, steps["gate"])
+            put(n + 1, 2, steps["add_masks"])
+            put(n + 2, 0, steps["store"])
+        last_norm = layer_norm_steps(LN_BATCHES[-1])
 
         for n in range(N_UNITS):
             more = n + 1 < N_UNITS
             if n + LOAD_AHEAD < N_UNITS:
                 load(n + LOAD_AHEAD)
-            if n % (PAIR * UNITS) == 0 and n // UNITS + 2 * PAIR < G:
-                load_logits(n // UNITS // PAIR + 2)
-            if n > 0 and n % UNITS == 0:
-                done = n // UNITS - 1
-                statistics, power, normalise, activate, gate, add_masks, finish = layer_norm_steps(done)
-                put(n, 0, statistics)
-                put(n + 1, "gpsimd", power)
-                put(n + 1, 2, normalise)
-                put(n + 1, 3, activate)
-                put(n + 2, 1, gate)
-                put(n + 2, 2, add_masks)
-                put(n + 2, 3, finish)
-                put(n + 3, 0, lambda done=done: store(done))
+            if n == 4:
+                load_logits(MASK_BATCHES[2])
             weighted = vector_multiply(n)
             gpsimd_multiply(n)
             run(n, "gpsimd")
-            scalar_regroup(n, 0)
-            scalar_regroup(n, 1)
+            scalar_regroup(n)
             if more:
                 prepare_w(n + 1, 0, 1)
                 prepare_x_vector(n + 1)
@@ -573,7 +545,6 @@ def tile_dynamicfeaturegroupinglayer_k_kernel(
             if n > 0:
                 quantise_w(n)
             run(n, 1)
-            vector_share(n)
             if more:
                 scalar_multiply(n + 1, 0)
             contract(n, 0, weighted)
@@ -589,9 +560,11 @@ def tile_dynamicfeaturegroupinglayer_k_kernel(
                     contract(n, 1, shared_of[n], cc, cc + 1)
             run(n, 3)
 
-        for slot in (1, 2, 3):
+        last_norm["statistics"][0]()
+        last_norm["power"]()
+        for slot in (1, 2):
             run(N_UNITS, slot)
         run(N_UNITS + 1, 0)
-        for step in layer_norm_steps(G - 1):
-            step()
-        store(G - 1)
+        last_norm["normalise"][0]()
+        for step in ("activate", "gate", "add_masks", "store"):
+            last_norm[step]()

@@ -32,6 +32,7 @@ SHV = HALVES * UNITS
 CC = 2
 TILE = CC * HALVES * M * B * PACK
 M2 = M // 2
+GPSIMD_Q = (4, 3)
 LOAD_AHEAD = 3
 PAIR = 2
 PAIR_ROWS = PAIR * M
@@ -304,35 +305,51 @@ def tile_dynamicfeaturegroupinglayer_k_kernel(
         def gpsimd_multiply(n):
             shared = stage.tile([P, TILE], BF16, name="shared", tag="shared", bufs=1, align_bytes=64)
             shared_of[n] = shared
-            shape = [P, CC * HALVES, M2, B, PACK]
+            blocks = GPSIMD_Q[n % UNITS]
+            shape = [P, blocks, M2, B, PACK]
             nc.gpsimd.tensor_tensor(
-                out=shared[:].rearrange("p (q m b t) -> p q m b t", q=CC * HALVES, m=M, t=PACK)[:, :, 0:M2],
-                in0=x_ready[n].unsqueeze(2).to_broadcast(shape),
-                in1=shared_masks(n, 0).unsqueeze(3).to_broadcast(shape),
+                out=shared[:].rearrange("p (q m b t) -> p q m b t", q=CC * HALVES, m=M, t=PACK)[
+                    :, 0:blocks, 0:M2
+                ],
+                in0=x_ready[n][:, 0:blocks].unsqueeze(2).to_broadcast(shape),
+                in1=shared_masks(n, 0)[:, 0:blocks].unsqueeze(3).to_broadcast(shape),
                 op=ALU.mult,
             )
 
-        def scalar_multiply(n, cc):
-            if cc == 0:
-                planes = stage.tile([P, CC * HALVES, M2, 2, B, 2], BF16, name="planes", tag="planes", bufs=2)
+        def scalar_slices(n):
+            both = [(q, m) for q in range(CC * HALVES) for m in range(M2, M)]
+            return both + [(q, m) for q in range(GPSIMD_Q[n % UNITS], CC * HALVES) for m in range(M2)]
+
+        def scalar_multiply(n, part):
+            slices = scalar_slices(n)
+            if part == 0:
+                planes = stage.tile([P, len(slices), 2, B, 2], BF16, name="planes", tag="planes", bufs=2)
                 planes_of[n] = planes
-            mask = shared_masks(n, 1)
-            for q in range(cc * HALVES, (cc + 1) * HALVES):
-                for ml in range(M2):
-                    for t in range(PACK):
-                        u, e = divmod(t, 2)
-                        nc.scalar.activation(
-                            out=planes_of[n][:, q, ml, u, :, e], in_=x_ready[n][:, q, :, t],
-                            func=FUNC.Copy, scale=mask[:, q, ml, t : t + 1],
-                        )
+            half = len(slices) // 2
+            for i in range(part * half, (part + 1) * half):
+                q, m = slices[i]
+                mh, ml = divmod(m, M2)
+                for t in range(PACK):
+                    u, e = divmod(t, 2)
+                    nc.scalar.activation(
+                        out=planes_of[n][:, i, u, :, e], in_=x_ready[n][:, q, :, t],
+                        func=FUNC.Copy, scale=shared_masks(n, mh)[:, q, ml, t : t + 1],
+                    )
 
         def scalar_regroup(n):
+            words = shared_of[n][:].bitcast(F32).rearrange("p (q m b u) -> p q m b u", q=CC * HALVES, m=M, u=2)
+            planes = planes_of[n][:].bitcast(F32).rearrange("p i u b one -> p i b (u one)")
+            both = CC * HALVES * M2
             nc.scalar.copy(
-                out=shared_of[n][:].bitcast(F32).rearrange(
-                    "p (q m b u) -> p q m b u", q=CC * HALVES, m=M, u=2
-                )[:, :, M2:M],
-                in_=planes_of[n][:].bitcast(F32).rearrange("p q ml u b one -> p q ml b (u one)"),
+                out=words[:, :, M2:M],
+                in_=planes[:, 0:both].rearrange("p (q ml) b u -> p q ml b u", ml=M2),
             )
+            first = GPSIMD_Q[n % UNITS]
+            if first < CC * HALVES:
+                nc.scalar.copy(
+                    out=words[:, first:, 0:M2],
+                    in_=planes[:, both:].rearrange("p (q ml) b u -> p q ml b u", ml=M2),
+                )
 
         def quantise(values, tag):
             width = values.shape[1] // PACK

@@ -32,13 +32,14 @@ SHV = HALVES * UNITS
 CC = 2
 TILE = CC * HALVES * M * B * PACK
 M2 = M // 2
-GPSIMD_Q = (4, 3)
+GPSIMD_B = (52, 48)
 LOAD_AHEAD = 3
 PAIR = 2
 PAIR_ROWS = PAIR * M
 MASK_BATCHES = ((0,), (1, 2), (3, 4))
 LN_ROWS = 4
-LN_BATCHES = ((0, 1, 2, 3), (4, 5, 6, 7), (8,), (9,))
+LN_BATCHES = ((0, 1, 2), (3, 4, 5), (6, 7), (8,), (9,))
+LN_MOST = max(len(groups) for groups in LN_BATCHES)
 
 
 def tile_dynamicfeaturegroupinglayer_k_kernel(
@@ -105,7 +106,7 @@ def tile_dynamicfeaturegroupinglayer_k_kernel(
             out=norm_power[:], in0=zero[:, 0:2], scalar1=0.0, scalar2=-1.0 / ALPHA,
             op0=ALU.mult, op1=ALU.add,
         )
-        rsqrt_power = const.tile([P, 4 * LN_ROWS], F32, name="rsqrt_power")
+        rsqrt_power = const.tile([P, LN_MOST * LN_ROWS], F32, name="rsqrt_power")
         nc.vector.memset(rsqrt_power[:], -0.5)
         row_of = const.tile([P, PAIR_ROWS], F32, name="row_of")
         nc.vector.tensor_reduce(
@@ -146,21 +147,32 @@ def tile_dynamicfeaturegroupinglayer_k_kernel(
                             in_=by_pass[:, 1, g2, sh, :, :, mh * M2 : (mh + 1) * M2],
                         )
 
-        fold = const.tile([P, P], F32, name="fold")
-        for half in range(2):
-            nc.vector.tensor_tensor(
-                out=fold[:, half * H : (half + 1) * H], in0=ident[:, 0:H], in1=ident[:, H : 2 * H], op=ALU.add
-            )
-        affine = const.tile([P, 2, 2, G * H], BF16, name="affine")
+        fold = const.tile([P, H], F32, name="fold")
+        nc.vector.tensor_tensor(out=fold[:], in0=ident[:, 0:H], in1=ident[:, H : 2 * H], op=ALU.add)
+        ln_rows = const.tile([P, H], BF16, name="ln_rows")
+        nc.gpsimd.memset(ln_rows[:], 0.0)
+        gated_tiles = []
+        for k in range(2):
+            gated = const.tile([P, (LN_MOST + 1) * P - H], F32, name="gated%d" % k)
+            nc.gpsimd.memset(gated[:], 0.0)
+            gated_tiles.append(gated)
 
         load(1)
         load_logits(MASK_BATCHES[1])
         for n in range(2, LOAD_AHEAD):
             load(n)
-        for n, vec in enumerate((ln1_w, ln2_w, ln1_b, ln2_b)):
-            nc.sync.dma_start(
-                out=affine[:, n // 2, n % 2, :], in_=vec.rearrange("g j -> (g j)").partition_broadcast(P)
+        for k, vec in enumerate((ln1_w, ln2_w, ln1_b, ln2_b)):
+            nc.sync.dma_start(out=ln_rows[k * G : (k + 1) * G, :], in_=vec[:])
+        half_affine = const.tile([P, 4 * G], F32, name="half_affine")
+
+        def turn_affine():
+            twice = const.tile([P, 2, H], F32, name="twice")
+            nc.scalar.copy(out=twice[:], in_=ln_rows[:].unsqueeze(1).to_broadcast([P, 2, H]))
+            bank = banks.tile([P, BANK], F32, name="bank", tag="bank")
+            nc.tensor.transpose(
+                out=bank[:, 0:P], in_=twice[:].rearrange("p mt j -> p (mt j)"), identity=ident[:]
             )
+            nc.scalar.activation(out=half_affine[:], in_=bank[:, 0 : 4 * G], func=FUNC.Copy, scale=0.5)
 
         def entmax_steps(pairs):
             count = len(pairs)
@@ -305,51 +317,43 @@ def tile_dynamicfeaturegroupinglayer_k_kernel(
         def gpsimd_multiply(n):
             shared = stage.tile([P, TILE], BF16, name="shared", tag="shared", bufs=1, align_bytes=64)
             shared_of[n] = shared
-            blocks = GPSIMD_Q[n % UNITS]
-            shape = [P, blocks, M2, B, PACK]
-            nc.gpsimd.tensor_tensor(
-                out=shared[:].rearrange("p (q m b t) -> p q m b t", q=CC * HALVES, m=M, t=PACK)[
-                    :, 0:blocks, 0:M2
+            low_masks(nc.gpsimd, n, 0, GPSIMD_B[n % UNITS])
+
+        def vector_share(n):
+            low_masks(nc.vector, n, GPSIMD_B[n % UNITS], B)
+
+        def low_masks(engine, n, first_b, last_b):
+            shape = [P, CC * HALVES, M2, last_b - first_b, PACK]
+            engine.tensor_tensor(
+                out=shared_of[n][:].rearrange("p (q m b t) -> p q m b t", q=CC * HALVES, m=M, t=PACK)[
+                    :, :, 0:M2, first_b:last_b
                 ],
-                in0=x_ready[n][:, 0:blocks].unsqueeze(2).to_broadcast(shape),
-                in1=shared_masks(n, 0)[:, 0:blocks].unsqueeze(3).to_broadcast(shape),
+                in0=x_ready[n][:, :, first_b:last_b].unsqueeze(2).to_broadcast(shape),
+                in1=shared_masks(n, 0).unsqueeze(3).to_broadcast(shape),
                 op=ALU.mult,
             )
 
-        def scalar_slices(n):
-            both = [(q, m) for q in range(CC * HALVES) for m in range(M2, M)]
-            return both + [(q, m) for q in range(GPSIMD_Q[n % UNITS], CC * HALVES) for m in range(M2)]
-
-        def scalar_multiply(n, part):
-            slices = scalar_slices(n)
-            if part == 0:
-                planes = stage.tile([P, len(slices), 2, B, 2], BF16, name="planes", tag="planes", bufs=2)
+        def scalar_multiply(n, cc):
+            if cc == 0:
+                planes = stage.tile([P, CC * HALVES, M2, 2, B, 2], BF16, name="planes", tag="planes", bufs=2)
                 planes_of[n] = planes
-            half = len(slices) // 2
-            for i in range(part * half, (part + 1) * half):
-                q, m = slices[i]
-                mh, ml = divmod(m, M2)
-                for t in range(PACK):
-                    u, e = divmod(t, 2)
-                    nc.scalar.activation(
-                        out=planes_of[n][:, i, u, :, e], in_=x_ready[n][:, q, :, t],
-                        func=FUNC.Copy, scale=shared_masks(n, mh)[:, q, ml, t : t + 1],
-                    )
+            mask = shared_masks(n, 1)
+            for q in range(cc * HALVES, (cc + 1) * HALVES):
+                for ml in range(M2):
+                    for t in range(PACK):
+                        u, e = divmod(t, 2)
+                        nc.scalar.activation(
+                            out=planes_of[n][:, q, ml, u, :, e], in_=x_ready[n][:, q, :, t],
+                            func=FUNC.Copy, scale=mask[:, q, ml, t : t + 1],
+                        )
 
         def scalar_regroup(n):
-            words = shared_of[n][:].bitcast(F32).rearrange("p (q m b u) -> p q m b u", q=CC * HALVES, m=M, u=2)
-            planes = planes_of[n][:].bitcast(F32).rearrange("p i u b one -> p i b (u one)")
-            both = CC * HALVES * M2
             nc.scalar.copy(
-                out=words[:, :, M2:M],
-                in_=planes[:, 0:both].rearrange("p (q ml) b u -> p q ml b u", ml=M2),
+                out=shared_of[n][:].bitcast(F32).rearrange(
+                    "p (q m b u) -> p q m b u", q=CC * HALVES, m=M, u=2
+                )[:, :, M2:M],
+                in_=planes_of[n][:].bitcast(F32).rearrange("p q ml u b one -> p q ml b (u one)"),
             )
-            first = GPSIMD_Q[n % UNITS]
-            if first < CC * HALVES:
-                nc.scalar.copy(
-                    out=words[:, first:, 0:M2],
-                    in_=planes[:, both:].rearrange("p (q ml) b u -> p q ml b u", ml=M2),
-                )
 
         def quantise(values, tag):
             width = values.shape[1] // PACK
@@ -401,6 +405,7 @@ def tile_dynamicfeaturegroupinglayer_k_kernel(
         def layer_norm_steps(groups):
             count = len(groups)
             kept = {}
+            gated = gated_tiles[LN_BATCHES.index(groups) % 2]
 
             def stat(name, *shape):
                 tile = small.tile([P] + list(shape), F32, name=name, tag="%s%d" % (name, count))
@@ -409,67 +414,98 @@ def tile_dynamicfeaturegroupinglayer_k_kernel(
 
             def statistics(i):
                 if i == 0:
-                    stat("stats", 2, count, 2, 3)
-                    stat("normed", 2, count, 2, H)
-                stats, normed = kept["stats"], kept["normed"]
+                    stat("stats", count, 2, 2, 3)
                 for mt in range(2):
                     nc.vector.bn_stats(
-                        out=stats[:, mt, i].rearrange("p w k -> p (w k)"), in_=acc[mt][:]
+                        out=kept["stats"][:, i, mt].rearrange("p w k -> p (w k)"), in_=acc[mt][:]
                     )
+
+            def take_sums(i):
+                if i == 0:
+                    stat("raw", count, 2, P)
                 for mt in range(2):
-                    for w in range(2):
-                        nc.vector.scalar_tensor_tensor(
-                            out=normed[:, mt, i, w, :], in0=acc[mt][:, w:P:2],
-                            scalar=stats[:, mt, i, w, 1:2],
-                            in1=affine[:, 0, w, groups[i] * H : (groups[i] + 1) * H],
-                            op0=ALU.subtract, op1=ALU.mult,
-                        )
+                    nc.scalar.copy(out=kept["raw"][:, i, mt, :], in_=acc[mt][:])
 
             def power():
-                var_eps = stat("var_eps", 2, count, 2)
+                var_eps = stat("var_eps", count * LN_ROWS)
                 nc.gpsimd.tensor_scalar(
-                    out=var_eps[:], in0=kept["stats"][:, :, :, :, 2], scalar1=1.0 / H, scalar2=EPS,
-                    op0=ALU.mult, op1=ALU.add,
+                    out=var_eps[:], in0=kept["stats"][:].rearrange("p i mt w k -> p (i mt w) k")[:, :, 2],
+                    scalar1=1.0 / H, scalar2=EPS, op0=ALU.mult, op1=ALU.add,
                 )
                 nc.gpsimd.tensor_tensor(
-                    out=stat("rstd", 2, count, 2)[:].rearrange("p mt i w -> p (mt i w)"),
-                    in0=var_eps[:].rearrange("p mt i w -> p (mt i w)"),
+                    out=stat("rstd", count * LN_ROWS)[:], in0=var_eps[:],
                     in1=rsqrt_power[:, 0 : count * LN_ROWS], op=ALU.pow,
                 )
 
+            def offsets():
+                nc.vector.scalar_tensor_tensor(
+                    out=stat("offset", count * LN_ROWS)[:],
+                    in0=kept["stats"][:].rearrange("p i mt w k -> p (i mt w) k")[:, :, 1],
+                    scalar=-1.0, in1=kept["rstd"][:], op0=ALU.mult, op1=ALU.mult,
+                )
+
             def normalise(i):
-                normed, rstd = kept["normed"], kept["rstd"]
+                if i == 0:
+                    stat("z", count, 2, 2, H)
                 for mt in range(2):
                     for w in range(2):
-                        nc.vector.scalar_tensor_tensor(
-                            out=normed[:, mt, i, w, :], in0=normed[:, mt, i, w, :],
-                            scalar=rstd[:, mt, i, w : w + 1],
-                            in1=affine[:, 1, w, groups[i] * H : (groups[i] + 1) * H],
-                            op0=ALU.mult, op1=ALU.add,
+                        r = (2 * i + mt) * 2 + w
+                        nc.scalar.activation(
+                            out=kept["z"][:, i, w, mt, :], in_=kept["raw"][:, i, mt, w:P:2],
+                            func=FUNC.Identity, scale=kept["rstd"][:, r : r + 1],
+                            bias=kept["offset"][:, r : r + 1],
                         )
 
-            def activate():
-                for name, w, func in (("half_tanh", 0, FUNC.Tanh), ("half_relu", 1, FUNC.Relu)):
-                    nc.scalar.activation(
-                        out=stat(name, 2 * count, H)[:],
-                        in_=kept["normed"][:].rearrange("p mt i w j -> p (mt i) w j")[:, :, w, :],
-                        func=func, scale=0.5,
-                    )
+            def normalise_in_psum():
+                stat("z", count, 2, 2, H)
+                for mt in range(2):
+                    for w in range(2):
+                        r = 2 * mt + w
+                        nc.vector.tensor_scalar(
+                            out=kept["z"][:, 0, w, mt, :], in0=acc[mt][:, w:P:2],
+                            scalar1=kept["stats"][:, 0, mt, w, 1:2], scalar2=kept["rstd"][:, r : r + 1],
+                            op0=ALU.subtract, op1=ALU.mult,
+                        )
+
+            def turn(first):
+                bank = banks.tile([P, 2, 2, P], F32, name="turned", tag="bank")
+                for i in range(first, min(first + 2, count)):
+                    for w in range(2):
+                        nc.tensor.transpose(
+                            out=bank[:, i - first, w],
+                            in_=kept["z"][:, i, w].rearrange("p mt j -> p (mt j)"), identity=ident[:],
+                        )
+                kept["turned"] = bank
+
+            def activate(first):
+                if first == 0:
+                    stat("half_tanh", count, P)
+                    stat("half_relu", count, P)
+                for i in range(first, min(first + 2, count)):
+                    for name, w, func in (("half_tanh", 0, FUNC.Tanh), ("half_relu", 1, FUNC.Relu)):
+                        gain, shift = w * G + groups[i], (2 + w) * G + groups[i]
+                        nc.scalar.activation(
+                            out=kept[name][:, i, :], in_=kept["turned"][:, i - first, w],
+                            func=func, scale=half_affine[:, gain : gain + 1],
+                            bias=half_affine[:, shift : shift + 1],
+                        )
 
             def gate():
                 nc.vector.scalar_tensor_tensor(
-                    out=stat("gated", 2 * count, H)[:], in0=kept["half_tanh"][:], scalar=1.0,
-                    in1=kept["half_relu"][:], op0=ALU.add, op1=ALU.mult,
+                    out=gated[:, 0 : count * P], in0=kept["half_tanh"][:].rearrange("p i n -> p (i n)"),
+                    scalar=1.0, in1=kept["half_relu"][:].rearrange("p i n -> p (i n)"),
+                    op0=ALU.add, op1=ALU.mult,
                 )
 
             def add_masks():
                 bank = banks.tile([P, BANK], F32, name="bank", tag="bank")
-                gated = kept["gated"][:].rearrange("p (mt i) j -> p mt (i j)", mt=2)
-                for mt in range(2):
-                    nc.tensor.matmul(
-                        out=bank[:, 0 : count * H], lhsT=fold[:], rhs=gated[:, mt],
-                        start=(mt == 0), stop=(mt == 1),
-                    )
+                for i in range(count):
+                    for m2 in range(2):
+                        first = i * P + m2 * H
+                        nc.tensor.matmul(
+                            out=bank[:, i * H : (i + 1) * H], lhsT=gated[:, first : first + P],
+                            rhs=fold[:], start=(m2 == 0), stop=(m2 == 1),
+                        )
                 result = stat("result", count * H)
                 nc.scalar.copy(out=result[0:B], in_=bank[0:B, 0 : count * H])
 
@@ -478,10 +514,14 @@ def tile_dynamicfeaturegroupinglayer_k_kernel(
                     out=out[:, groups[0] * H : (groups[-1] + 1) * H], in_=kept["result"][0:B]
                 )
 
+            def each(step):
+                return [lambda i=i: step(i) for i in range(count)]
+
             return {
-                "statistics": [lambda i=i: statistics(i) for i in range(count)], "power": power,
-                "normalise": [lambda i=i: normalise(i) for i in range(count)],
-                "activate": activate, "gate": gate, "add_masks": add_masks, "store": store,
+                "statistics": each(statistics), "take_sums": each(take_sums), "power": power,
+                "offsets": offsets, "normalise": each(normalise), "normalise_in_psum": normalise_in_psum,
+                "turn": turn, "activate": activate, "gate": gate, "add_masks": add_masks,
+                "store": store,
             }
 
         first_masks = entmax_steps(MASK_BATCHES[0])
@@ -515,6 +555,7 @@ def tile_dynamicfeaturegroupinglayer_k_kernel(
             for work in todo.get((n, slot), []):
                 work()
 
+        put(1, 0, turn_affine)
         for pairs in MASK_BATCHES[1:]:
             n = (pairs[0] - 1) * PAIR * UNITS
             steps = entmax_steps(pairs)
@@ -527,19 +568,24 @@ def tile_dynamicfeaturegroupinglayer_k_kernel(
             put(n + 2, "gpsimd", steps["power"])
             put(n + 2, 1, steps["scale"][0])
             put(n + 2, 3, steps["turn"][0])
-            put(n + 3, 1, steps["scale"][1])
-            put(n + 3, 3, steps["turn"][1])
+            put(n + 4, 1, steps["scale"][1])
+            put(n + 5, 1, steps["turn"][1])
         for groups in LN_BATCHES[:-1]:
             steps = layer_norm_steps(groups)
             for i, g in enumerate(groups):
                 put((g + 1) * UNITS, 0, steps["statistics"][i])
+                put((g + 1) * UNITS, 0, steps["take_sums"][i])
             n = (groups[-1] + 1) * UNITS + 1
             put(n, "gpsimd", steps["power"])
+            put(n, 2, steps["offsets"])
             for i in range(len(groups)):
-                put(n, 2, steps["normalise"][i])
-            put(n, 3, steps["activate"])
-            put(n + 1, 1, steps["gate"])
-            put(n + 1, 2, steps["add_masks"])
+                put(n + i // 2, 3, steps["normalise"][i])
+            for first in range(0, len(groups), 2):
+                n += 1
+                put(n, 2, lambda steps=steps, first=first: steps["turn"](first))
+                put(n, 3, lambda steps=steps, first=first: steps["activate"](first))
+            put(n + 1, 2, steps["gate"])
+            put(n + 1, 3, steps["add_masks"])
             put(n + 2, 0, steps["store"])
         last_norm = layer_norm_steps(LN_BATCHES[-1])
 
@@ -562,6 +608,7 @@ def tile_dynamicfeaturegroupinglayer_k_kernel(
             if n > 0:
                 quantise_w(n)
             run(n, 1)
+            vector_share(n)
             if more:
                 scalar_multiply(n + 1, 0)
             contract(n, 0, weighted)
@@ -579,9 +626,14 @@ def tile_dynamicfeaturegroupinglayer_k_kernel(
 
         last_norm["statistics"][0]()
         last_norm["power"]()
-        for slot in (1, 2):
+        for slot in (0, 2, 3):
             run(N_UNITS, slot)
-        run(N_UNITS + 1, 0)
-        last_norm["normalise"][0]()
-        for step in ("activate", "gate", "add_masks", "store"):
-            last_norm[step]()
+        last_norm["normalise_in_psum"]()
+        last_norm["turn"](0)
+        run(N_UNITS + 1, 2)
+        last_norm["activate"](0)
+        last_norm["gate"]()
+        run(N_UNITS + 1, 3)
+        last_norm["add_masks"]()
+        run(N_UNITS + 2, 0)
+        last_norm["store"]()

@@ -32,7 +32,7 @@ SHV = HALVES * UNITS
 CC = 2
 TILE = CC * HALVES * M * B * PACK
 M2 = M // 2
-GPSIMD_B = (52, 48)
+GPSIMD_B = (52, 32)
 LOAD_AHEAD = 3
 PAIR = 2
 PAIR_ROWS = PAIR * M

@@ -32,7 +32,7 @@ SHV = HALVES * UNITS
 CC = 2
 TILE = CC * HALVES * M * B * PACK
 M2 = M // 2
-GPSIMD_B = (52, 32)
+GPSIMD_B = (48, 48)
 LOAD_AHEAD = 3
 PAIR = 2
 PAIR_ROWS = PAIR * M
@@ -52,8 +52,9 @@ def tile_dynamicfeaturegroupinglayer_k_kernel(
         stage = ctx.enter_context(tc.tile_pool(name="stage", bufs=3))
         quant = ctx.enter_context(tc.tile_pool(name="quant", bufs=4))
         small = ctx.enter_context(tc.tile_pool(name="small", bufs=2))
-        banks = ctx.enter_context(tc.psum_pool(name="banks", bufs=4))
-        x_banks = ctx.enter_context(tc.psum_pool(name="x_banks", bufs=2))
+        banks = ctx.enter_context(tc.psum_pool(name="banks", bufs=3))
+        x_banks = ctx.enter_context(tc.psum_pool(name="x_banks", bufs=1))
+        shared_x_banks = ctx.enter_context(tc.psum_pool(name="shared_x_banks", bufs=2))
         sums = ctx.enter_context(tc.psum_pool(name="sums", bufs=1))
         ctx.enter_context(tc.manual_schedule())
 
@@ -304,31 +305,36 @@ def tile_dynamicfeaturegroupinglayer_k_kernel(
                 w_ready[n] = w_grouped
             turn_and_group(w_loaded[(n, sh)], cp, w_ready[n][:, sh * 2 + cp, :], ident, copy)
 
-        def prepare_x_scalar(n, copy=nc.scalar.copy):
+        def turn_x(n, cp, pool):
+            bank = pool.tile([P, CC, P, 2], F32, name="x_bank%d" % cp, tag="x_bank%d" % cp)
+            turn_words(x_loaded[n], cp, bank[:].rearrange("p cc col u -> p cc u col"), unzip)
+            x_psum[(n, cp)] = bank[:].bitcast(BF16).rearrange("p cc (sh b) t -> p (cc sh) b t", sh=HALVES)
+            return bank
+
+        def prepare_x_shared(n, copy=nc.scalar.copy):
+            bank = turn_x(n, 1, shared_x_banks)
             x_sb = stage.tile([P, CC * P * PACK], BF16, name="x_grouped", tag="x_grouped")
-            turn_and_group(x_loaded[n], 1, x_sb[:], unzip, copy)
+            copy(out=x_sb[:].bitcast(F32), in_=bank[:].rearrange("p cc col u -> p (cc col u)"))
             x_ready[n] = x_sb[:].rearrange("p (q b t) -> p q b t", q=CC * HALVES, t=PACK)
 
         def prepare_x_vector(n):
-            bank = x_banks.tile([P, CC, P, 2], F32, name="x_bank", tag="x_bank")
-            turn_words(x_loaded[n], 0, bank[:].rearrange("p cc col u -> p cc u col"), unzip)
-            x_psum[n] = bank[:].bitcast(BF16).rearrange("p cc (sh b) t -> p (cc sh) b t", sh=HALVES)
+            turn_x(n, 0, x_banks)
 
         def gpsimd_multiply(n):
             shared = stage.tile([P, TILE], BF16, name="shared", tag="shared", bufs=1, align_bytes=64)
             shared_of[n] = shared
-            low_masks(nc.gpsimd, n, 0, GPSIMD_B[n % UNITS])
+            low_masks(nc.gpsimd, n, x_ready[n], 0, GPSIMD_B[n % UNITS])
 
         def vector_share(n):
-            low_masks(nc.vector, n, GPSIMD_B[n % UNITS], B)
+            low_masks(nc.vector, n, x_psum[(n, 1)], GPSIMD_B[n % UNITS], B)
 
-        def low_masks(engine, n, first_b, last_b):
+        def low_masks(engine, n, x_rows, first_b, last_b):
             shape = [P, CC * HALVES, M2, last_b - first_b, PACK]
             engine.tensor_tensor(
                 out=shared_of[n][:].rearrange("p (q m b t) -> p q m b t", q=CC * HALVES, m=M, t=PACK)[
                     :, :, 0:M2, first_b:last_b
                 ],
-                in0=x_ready[n][:, :, first_b:last_b].unsqueeze(2).to_broadcast(shape),
+                in0=x_rows[:, :, first_b:last_b].unsqueeze(2).to_broadcast(shape),
                 in1=shared_masks(n, 0).unsqueeze(3).to_broadcast(shape),
                 op=ALU.mult,
             )
@@ -370,7 +376,7 @@ def tile_dynamicfeaturegroupinglayer_k_kernel(
             shape = [P, CC * HALVES, M, B, PACK]
             nc.vector.tensor_tensor(
                 out=weighted[:].rearrange("p (q m b t) -> p q m b t", q=CC * HALVES, m=M, t=PACK),
-                in0=x_psum[n].unsqueeze(2).to_broadcast(shape),
+                in0=x_psum[(n, 0)].unsqueeze(2).to_broadcast(shape),
                 in1=vector_masks(n).unsqueeze(3).to_broadcast(shape),
                 op=ALU.mult,
             )
@@ -533,7 +539,7 @@ def tile_dynamicfeaturegroupinglayer_k_kernel(
         prepare_w(0, 0, 0, nc.vector.tensor_copy)
         prepare_w(0, 0, 1, nc.vector.tensor_copy)
         first_masks["row_sums"]()
-        prepare_x_scalar(0, nc.vector.tensor_copy)
+        prepare_x_shared(0, nc.vector.tensor_copy)
         first_masks["power"]()
         prepare_w(0, 1, 0, nc.vector.tensor_copy)
         prepare_w(0, 1, 1, nc.vector.tensor_copy)
@@ -543,7 +549,7 @@ def tile_dynamicfeaturegroupinglayer_k_kernel(
         quantise_w(0)
         scalar_multiply(0, 0)
         scalar_multiply(0, 1)
-        prepare_x_scalar(1)
+        prepare_x_shared(1)
         prepare_w(1, 0, 0)
 
         todo = {}
@@ -597,26 +603,26 @@ def tile_dynamicfeaturegroupinglayer_k_kernel(
                 load_logits(MASK_BATCHES[2])
             weighted = vector_multiply(n)
             gpsimd_multiply(n)
+            vector_share(n)
             run(n, "gpsimd")
             scalar_regroup(n)
             if more:
                 prepare_w(n + 1, 0, 1)
-                prepare_x_vector(n + 1)
                 prepare_w(n + 1, 1, 0)
                 prepare_w(n + 1, 1, 1)
             run(n, 0)
             if n > 0:
                 quantise_w(n)
             run(n, 1)
-            vector_share(n)
             if more:
                 scalar_multiply(n + 1, 0)
+                prepare_x_vector(n + 1)
             contract(n, 0, weighted)
             run(n, 2)
             if more:
                 scalar_multiply(n + 1, 1)
                 if n + 2 < N_UNITS:
-                    prepare_x_scalar(n + 2)
+                    prepare_x_shared(n + 2)
                     prepare_w(n + 2, 0, 0)
                 contract(n, 1, shared_of[n])
             else:

from contextlib import ExitStack

import concourse.mybir as mybir
from concourse.masks import make_identity

F32 = mybir.dt.float32
BF16 = mybir.dt.bfloat16
U32 = mybir.dt.uint32
U8 = mybir.dt.uint8
FP8X4 = mybir.dt.float8_e4m3fn_x4
ALU = mybir.AluOpType
FUNC = mybir.ActivationFunctionType
AXIS_X = mybir.AxisListType.X

B, G, M, S, H = 64, 10, 4, 8192, 64
ALPHA = 1.1
EPS = 1e-5
FLOPS = 2 * 2 * B * G * M * S * H

P = 128
PACK = 4
K_PASS = P * PACK
BANK = 512
HALVES = 2
HALF = S // HALVES
UNIT_K = 2048
UNITS = HALF // UNIT_K
UNIT_PASSES = UNIT_K // K_PASS
N_UNITS = G * UNITS
PASSES = S // K_PASS
SHV = HALVES * UNITS
CC = 2
TILE = CC * HALVES * M * B * PACK
M2 = M // 2
GPSIMD_B = (48, 48)
LOAD_AHEAD = 3
PAIR = 2
PAIR_ROWS = PAIR * M
MASK_BATCHES = ((0,), (1, 2), (3, 4))
LN_ROWS = 4
LN_BATCHES = ((0, 1, 2), (3, 4, 5), (6, 7), (8,), (9,))
LN_MOST = max(len(groups) for groups in LN_BATCHES)


def tile_dynamicfeaturegroupinglayer_k_kernel(
    tc, x, W_masks, W1, W2, ln1_w, ln1_b, ln2_w, ln2_b, out
):
    nc = tc.nc
    with ExitStack() as ctx:
        const = ctx.enter_context(tc.tile_pool(name="const", bufs=1))
        loads = ctx.enter_context(tc.tile_pool(name="loads", bufs=LOAD_AHEAD + 1))
        stage = ctx.enter_context(tc.tile_pool(name="stage", bufs=3))
        quant = ctx.enter_context(tc.tile_pool(name="quant", bufs=4))
        small = ctx.enter_context(tc.tile_pool(name="small", bufs=2))
        banks = ctx.enter_context(tc.psum_pool(name="banks", bufs=3))
        x_banks = ctx.enter_context(tc.psum_pool(name="x_banks", bufs=1))
        shared_x_banks = ctx.enter_context(tc.psum_pool(name="shared_x_banks", bufs=2))
        sums = ctx.enter_context(tc.psum_pool(name="sums", bufs=1))
        ctx.enter_context(tc.manual_schedule())

        x_loaded, w_loaded, logits_of = {}, {}, {}
        x_psum, x_ready, w_ready, w_quantised = {}, {}, {}, {}
        acc, mask_of, planes_of, shared_of = {}, {}, {}, {}

        def load_logits(pairs):
            logits = small.tile([P, len(pairs), K_PASS], BF16, name="logits", tag="logits%d" % len(pairs))
            for i, pair in enumerate(pairs):
                nc.sync.dma_start(
                    out=logits[:, i, :],
                    in_=W_masks[PAIR * pair : PAIR * (pair + 1)]
                    .rearrange("g m s -> (g m s)")
                    .rearrange("(rc f) -> rc f", f=K_PASS),
                )
            logits_of[pairs] = logits

        def load(n):
            g, v = divmod(n, UNITS)
            x_sb = loads.tile([P, UNIT_K], BF16, name="x_sb", tag="x_sb")
            for sh in range(HALVES):
                first = g * S + sh * HALF + v * UNIT_K
                nc.sync.dma_start(out=x_sb[sh:P:2, :], in_=x[:, first : first + UNIT_K])
            x_loaded[n] = x_sb
            for sh in range(HALVES):
                first = sh * HALF + v * UNIT_K
                w_sb = loads.tile([P, UNIT_K], BF16, name="w_sb", tag="w_sb", bufs=2 * (LOAD_AHEAD + 1))
                nc.sync.dma_start(out=w_sb[0:P:2, :], in_=W1[g, :, first : first + UNIT_K])
                nc.sync.dma_start(out=w_sb[1:P:2, :], in_=W2[g, :, first : first + UNIT_K])
                w_loaded[(n, sh)] = w_sb

        load_logits(MASK_BATCHES[0])
        load(0)

        ident = const.tile([P, P], F32, name="ident")
        make_identity(nc, ident[:])
        zero = const.tile([P, PAIR_ROWS], F32, name="zero")
        nc.vector.memset(zero[:], 0.0)
        warm = const.tile([P, 1], F32, name="warm")
        nc.scalar.activation(out=warm[:], in_=zero[:, 0:1], func=FUNC.Exp)
        exp_scales = const.tile([P, 2], F32, name="exp_scales")
        for col, value in enumerate((-ALPHA, -1.0)):
            nc.vector.tensor_scalar(
                out=exp_scales[:, col : col + 1], in0=zero[:, 0:1], scalar1=0.0, scalar2=value,
                op0=ALU.mult, op1=ALU.add,
            )
        norm_power = const.tile([P, 2], F32, name="norm_power")
        nc.vector.tensor_scalar(
            out=norm_power[:], in0=zero[:, 0:2], scalar1=0.0, scalar2=-1.0 / ALPHA,
            op0=ALU.mult, op1=ALU.add,
        )
        rsqrt_power = const.tile([P, LN_MOST * LN_ROWS], F32, name="rsqrt_power")
        nc.vector.memset(rsqrt_power[:], -0.5)
        row_of = const.tile([P, PAIR_ROWS], F32, name="row_of")
        nc.vector.tensor_reduce(
            out=row_of[:], in_=ident[:].rearrange("p (r c) -> p r c", c=PASSES), axis=AXIS_X, op=ALU.add
        )
        block = const.tile([P, P], F32, name="block")
        nc.vector.tensor_copy(
            out=block[:].rearrange("p (r c) -> p r c", c=PASSES),
            in_=row_of[:].unsqueeze(2).to_broadcast([P, PAIR_ROWS, PASSES]),
        )
        other_rows = const.tile([P, P], F32, name="other_rows")
        nc.vector.tensor_scalar(
            out=other_rows[:], in0=block[:], scalar1=-1.0, scalar2=2.0**127, op0=ALU.add, op1=ALU.mult
        )
        unzip = const.tile([P, P], F32, name="unzip")
        nc.vector.tensor_copy(
            out=unzip[:].rearrange("p (h a) -> p h a", h=2),
            in_=ident[:].rearrange("p (a h) -> p h a", h=2),
        )
        mask_order = const.tile([P, P], F32, name="mask_order")

        def order_masks():
            by_pass = ident[:].rearrange(
                "p (g2 m sh v cp cc) -> p cp g2 sh v cc m", g2=PAIR, m=M, sh=HALVES, v=UNITS, cp=2
            )
            vector_order = mask_order[:, 0 : P // 2].rearrange(
                "p (g2 v cc sh m) -> p g2 sh v cc m", g2=PAIR, v=UNITS, cc=CC, sh=HALVES
            )
            shared_order = mask_order[:, P // 2 : P].rearrange(
                "p (mh g2 v cc sh ml) -> p mh g2 sh v cc ml", mh=2, g2=PAIR, v=UNITS, cc=CC, sh=HALVES
            )
            for g2 in range(PAIR):
                for sh in range(HALVES):
                    nc.vector.tensor_copy(out=vector_order[:, g2, sh], in_=by_pass[:, 0, g2, sh])
                    for mh in range(2):
                        nc.vector.tensor_copy(
                            out=shared_order[:, mh, g2, sh],
                            in_=by_pass[:, 1, g2, sh, :, :, mh * M2 : (mh + 1) * M2],
                        )

        fold = const.tile([P, H], F32, name="fold")
        nc.vector.tensor_tensor(out=fold[:], in0=ident[:, 0:H], in1=ident[:, H : 2 * H], op=ALU.add)
        ln_rows = const.tile([P, H], BF16, name="ln_rows")
        nc.gpsimd.memset(ln_rows[:], 0.0)
        gated_tiles = []
        for k in range(2):
            gated = const.tile([P, (LN_MOST + 1) * P - H], F32, name="gated%d" % k)
            nc.gpsimd.memset(gated[:], 0.0)
            gated_tiles.append(gated)

        load(1)
        load_logits(MASK_BATCHES[1])
        for n in range(2, LOAD_AHEAD):
            load(n)
        for k, vec in enumerate((ln1_w, ln2_w, ln1_b, ln2_b)):
            nc.sync.dma_start(out=ln_rows[k * G : (k + 1) * G, :], in_=vec[:])
        half_affine = const.tile([P, 4 * G], F32, name="half_affine")

        def turn_affine():
            twice = const.tile([P, 2, H], F32, name="twice")
            nc.scalar.copy(out=twice[:], in_=ln_rows[:].unsqueeze(1).to_broadcast([P, 2, H]))
            bank = banks.tile([P, BANK], F32, name="bank", tag="bank")
            nc.tensor.transpose(
                out=bank[:, 0:P], in_=twice[:].rearrange("p mt j -> p (mt j)"), identity=ident[:]
            )
            nc.scalar.activation(out=half_affine[:], in_=bank[:, 0 : 4 * G], func=FUNC.Copy, scale=0.5)

        def entmax_steps(pairs):
            count = len(pairs)
            kept = {}

            def stat(name, *shape):
                tile = small.tile([P, count] + list(shape), F32, name=name, tag="%s%d" % (name, count))
                kept[name] = tile
                return tile

            def pass_maxima():
                nc.vector.tensor_reduce(
                    out=stat("pass_max")[:], in_=logits_of[pairs][:], axis=AXIS_X, op=ALU.max
                )

            def spread_maxima():
                bank = banks.tile([P, BANK], F32, name="bank", tag="bank")
                for i in range(count):
                    nc.tensor.matmul(
                        out=bank[:, i * P : (i + 1) * P],
                        lhsT=kept["pass_max"][:, i : i + 1].to_broadcast([P, P]),
                        rhs=ident[:], start=True, stop=True,
                    )
                kept["maxima"] = bank

            def row_maxima():
                own = stat("own", P)
                nc.vector.tensor_tensor(
                    out=own[:],
                    in0=kept["maxima"][:, 0 : count * P].rearrange("p (i n) -> p i n", i=count),
                    in1=other_rows[:].unsqueeze(1).to_broadcast([P, count, P]), op=ALU.add,
                )
                row_max = stat("row_max")
                nc.vector.tensor_reduce(out=row_max[:], in_=own[:], axis=AXIS_X, op=ALU.max)
                nc.vector.tensor_tensor(
                    out=stat("biases", 2)[:], in0=row_max[:].unsqueeze(2).to_broadcast([P, count, 2]),
                    in1=exp_scales[:].unsqueeze(1).to_broadcast([P, count, 2]), op=ALU.mult,
                )
                stat("e", K_PASS)
                stat("pass_sum")

            def exponentials(i):
                powers = small.tile([P, K_PASS], F32, name="powers", tag="powers")
                nc.scalar.activation(
                    out=powers[:], in_=logits_of[pairs][:, i, :], func=FUNC.Exp, scale=ALPHA,
                    bias=kept["biases"][:, i, 0:1], accum_out=kept["pass_sum"][:, i : i + 1],
                )
                nc.scalar.activation(
                    out=kept["e"][:, i, :], in_=logits_of[pairs][:, i, :], func=FUNC.Exp,
                    bias=kept["biases"][:, i, 1:2],
                )

            def row_sums():
                bank = banks.tile([P, BANK], F32, name="bank", tag="bank")
                nc.tensor.matmul(
                    out=bank[:, 0:count], lhsT=block[:], rhs=kept["pass_sum"][:], start=True, stop=True
                )
                nc.scalar.activation(
                    out=stat("padded")[:], in_=bank[:, 0:count], func=FUNC.Copy, bias=EPS
                )

            def power():
                nc.gpsimd.tensor_tensor(
                    out=stat("inv_norm")[:], in0=kept["padded"][:], in1=norm_power[:, 0:count], op=ALU.pow
                )

            def scale(i):
                by_row = small.tile([P, K_PASS], F32, name="by_row", tag="by_row")
                nc.scalar.activation(
                    out=by_row[:], in_=kept["e"][:, i, :], func=FUNC.Copy,
                    scale=kept["inv_norm"][:, i : i + 1],
                )
                kept[("by_row", i)] = by_row

            def turn(i):
                bank = banks.tile([P, P, PACK], F32, name="mask_bank", tag="bank")
                for t in range(PACK):
                    u, e = divmod(t, 2)
                    nc.tensor.transpose(
                        out=bank[:, :, t],
                        in_=kept[("by_row", i)][:, 2 * P * u + e : 2 * P * (u + 1) : 2],
                        identity=mask_order[:],
                    )
                mask = small.tile([P, P, PACK], F32, name="mask", tag="mask")
                nc.scalar.copy(out=mask[:], in_=bank[:])
                for g2 in range(PAIR):
                    mask_of[PAIR * pairs[i] + g2] = mask

            return {
                "pass_maxima": pass_maxima, "spread_maxima": spread_maxima, "row_maxima": row_maxima,
                "exponentials": [lambda i=i: exponentials(i) for i in range(count)],
                "row_sums": row_sums, "power": power,
                "scale": [lambda i=i: scale(i) for i in range(count)],
                "turn": [lambda i=i: turn(i) for i in range(count)],
            }

        def vector_masks(n):
            g, v = divmod(n, UNITS)
            width = CC * HALVES * M
            first = (g % PAIR * UNITS + v) * width
            return mask_of[g][:, first : first + width, :].rearrange("p (q m) t -> p q m t", m=M)

        def shared_masks(n, mh):
            g, v = divmod(n, UNITS)
            width = CC * HALVES * M2
            first = P // 2 + ((mh * PAIR + g % PAIR) * UNITS + v) * width
            return mask_of[g][:, first : first + width, :].rearrange("p (q ml) t -> p q ml t", ml=M2)

        def turn_words(source, cp, bank_view, order):
            words = source[:].bitcast(F32)
            for cc in range(CC):
                for u in range(2):
                    first = ((cp * CC + cc) * 2 + u) * P
                    nc.tensor.transpose(
                        out=bank_view[:, cc, u, :], in_=words[:, first : first + P], identity=order[:]
                    )

        def turn_and_group(source, cp, grouped, order, copy):
            bank = banks.tile([P, CC, 2, P], F32, name="turned", tag="bank")
            turn_words(source, cp, bank[:], order)
            copy(
                out=grouped.bitcast(F32).rearrange("p (cc col u) -> p cc col u", cc=CC, u=2),
                in_=bank[:].rearrange("p cc u col -> p cc col u"),
            )

        def prepare_w(n, sh, cp, copy=nc.scalar.copy):
            if sh == 0 and cp == 0:
                w_grouped = stage.tile([P, HALVES * 2, CC * P * PACK], BF16, name="w_grouped", tag="w_grouped", bufs=2, align_bytes=64)
                w_ready[n] = w_grouped
            turn_and_group(w_loaded[(n, sh)], cp, w_ready[n][:, sh * 2 + cp, :], ident, copy)

        def turn_x(n, cp, pool):
            bank = pool.tile([P, CC, P, 2], F32, name="x_bank%d" % cp, tag="x_bank%d" % cp)
            turn_words(x_loaded[n], cp, bank[:].rearrange("p cc col u -> p cc u col"), unzip)
            x_psum[(n, cp)] = bank[:].bitcast(BF16).rearrange("p cc (sh b) t -> p (cc sh) b t", sh=HALVES)
            return bank

        def prepare_x_shared(n, copy=nc.scalar.copy):
            bank = turn_x(n, 1, shared_x_banks)
            x_sb = stage.tile([P, CC * P * PACK], BF16, name="x_grouped", tag="x_grouped")
            copy(out=x_sb[:].bitcast(F32), in_=bank[:].rearrange("p cc col u -> p (cc col u)"))
            x_ready[n] = x_sb[:].rearrange("p (q b t) -> p q b t", q=CC * HALVES, t=PACK)

        def prepare_x_vector(n):
            turn_x(n, 0, x_banks)

        def gpsimd_multiply(n):
            shared = stage.tile([P, TILE], BF16, name="shared", tag="shared", bufs=1, align_bytes=64)
            shared_of[n] = shared
            low_masks(nc.gpsimd, n, x_ready[n], 0, GPSIMD_B[n % UNITS])

        def vector_share(n):
            low_masks(nc.vector, n, x_psum[(n, 1)], GPSIMD_B[n % UNITS], B)

        def low_masks(engine, n, x_rows, first_b, last_b):
            shape = [P, CC * HALVES, M2, last_b - first_b, PACK]
            engine.tensor_tensor(
                out=shared_of[n][:].rearrange("p (q m b t) -> p q m b t", q=CC * HALVES, m=M, t=PACK)[
                    :, :, 0:M2, first_b:last_b
                ],
                in0=x_rows[:, :, first_b:last_b].unsqueeze(2).to_broadcast(shape),
                in1=shared_masks(n, 0).unsqueeze(3).to_broadcast(shape),
                op=ALU.mult,
            )

        def scalar_multiply(n, cc):
            if cc == 0:
                planes = stage.tile([P, CC * HALVES, M2, 2, B, 2], BF16, name="planes", tag="planes", bufs=2)
                planes_of[n] = planes
            mask = shared_masks(n, 1)
            for q in range(cc * HALVES, (cc + 1) * HALVES):
                for ml in range(M2):
                    for t in range(PACK):
                        u, e = divmod(t, 2)
                        nc.scalar.activation(
                            out=planes_of[n][:, q, ml, u, :, e], in_=x_ready[n][:, q, :, t],
                            func=FUNC.Copy, scale=mask[:, q, ml, t : t + 1],
                        )

        def scalar_regroup(n):
            nc.scalar.copy(
                out=shared_of[n][:].bitcast(F32).rearrange(
                    "p (q m b u) -> p q m b u", q=CC * HALVES, m=M, u=2
                )[:, :, M2:M],
                in_=planes_of[n][:].bitcast(F32).rearrange("p q ml u b one -> p q ml b (u one)"),
            )

        def quantise(values, tag):
            width = values.shape[1] // PACK
            codes = quant.tile([P, width], U32, name="codes_" + tag, tag="codes_" + tag, align_bytes=64)
            scales = quant.tile([P, width], U8, name="scales_" + tag, tag="scales_" + tag, align_bytes=64)
            nc.vector.quantize_mx(out=codes[:].bitcast(FP8X4), scales=scales[:], in_=values)
            return codes, scales

        def quantise_w(n):
            w_quantised[n] = quantise(w_ready[n][:].rearrange("p c f -> p (c f)"), "w")

        def vector_multiply(n):
            weighted = stage.tile([P, TILE], BF16, name="weighted", tag="weighted", bufs=2, align_bytes=64)
            shape = [P, CC * HALVES, M, B, PACK]
            nc.vector.tensor_tensor(
                out=weighted[:].rearrange("p (q m b t) -> p q m b t", q=CC * HALVES, m=M, t=PACK),
                in0=x_psum[(n, 0)].unsqueeze(2).to_broadcast(shape),
                in1=vector_masks(n).unsqueeze(3).to_broadcast(shape),
                op=ALU.mult,
            )
            return weighted

        def contract(n, cp, weighted, first_cc=0, last_cc=CC):
            v = n % UNITS
            if (v, cp, first_cc) == (0, 0, 0):
                for mt in range(2):
                    acc_tile = sums.tile([P, P], F32, name="acc%d" % mt, tag="acc%d" % mt)
                    acc[mt] = acc_tile
            width = TILE // CC
            a_codes, a_scales = quantise(weighted[:, first_cc * width : last_cc * width], "a")
            w_codes, w_scales = w_quantised[n]
            for q in range(first_cc * HALVES, last_cc * HALVES):
                cc, sh = divmod(q, HALVES)
                w_pass = (sh * 2 + cp) * CC + cc
                w_cols = slice(w_pass * P, (w_pass + 1) * P)
                for mt in range(2):
                    a_tile = (q - first_cc * HALVES) * 2 + mt
                    a_cols = slice(a_tile * P, (a_tile + 1) * P)
                    nc.tensor.matmul_mx(
                        out=acc[mt][:],
                        lhsT=a_codes[:, a_cols].bitcast(FP8X4),
                        lhsT_scale=a_scales[:, a_cols],
                        rhs=w_codes[:, w_cols].bitcast(FP8X4),
                        rhs_scale=w_scales[:, w_cols],
                        start=(v, cp, q) == (0, 0, 0),
                        stop=(v, cp, q) == (UNITS - 1, 1, CC * HALVES - 1),
                    )

        def layer_norm_steps(groups):
            count = len(groups)
            kept = {}
            gated = gated_tiles[LN_BATCHES.index(groups) % 2]

            def stat(name, *shape):
                tile = small.tile([P] + list(shape), F32, name=name, tag="%s%d" % (name, count))
                kept[name] = tile
                return tile

            def statistics(i):
                if i == 0:
                    stat("stats", count, 2, 2, 3)
                for mt in range(2):
                    nc.vector.bn_stats(
                        out=kept["stats"][:, i, mt].rearrange("p w k -> p (w k)"), in_=acc[mt][:]
                    )

            def take_sums(i):
                if i == 0:
                    stat("raw", count, 2, P)
                for mt in range(2):
                    nc.scalar.copy(out=kept["raw"][:, i, mt, :], in_=acc[mt][:])

            def power():
                var_eps = stat("var_eps", count * LN_ROWS)
                nc.gpsimd.tensor_scalar(
                    out=var_eps[:], in0=kept["stats"][:].rearrange("p i mt w k -> p (i mt w) k")[:, :, 2],
                    scalar1=1.0 / H, scalar2=EPS, op0=ALU.mult, op1=ALU.add,
                )
                nc.gpsimd.tensor_tensor(
                    out=stat("rstd", count * LN_ROWS)[:], in0=var_eps[:],
                    in1=rsqrt_power[:, 0 : count * LN_ROWS], op=ALU.pow,
                )

            def offsets():
                nc.vector.scalar_tensor_tensor(
                    out=stat("offset", count * LN_ROWS)[:],
                    in0=kept["stats"][:].rearrange("p i mt w k -> p (i mt w) k")[:, :, 1],
                    scalar=-1.0, in1=kept["rstd"][:], op0=ALU.mult, op1=ALU.mult,
                )

            def normalise(i):
                if i == 0:
                    stat("z", count, 2, 2, H)
                for mt in range(2):
                    for w in range(2):
                        r = (2 * i + mt) * 2 + w
                        nc.scalar.activation(
                            out=kept["z"][:, i, w, mt, :], in_=kept["raw"][:, i, mt, w:P:2],
                            func=FUNC.Identity, scale=kept["rstd"][:, r : r + 1],
                            bias=kept["offset"][:, r : r + 1],
                        )

            def normalise_in_psum():
                stat("z", count, 2, 2, H)
                for mt in range(2):
                    for w in range(2):
                        r = 2 * mt + w
                        nc.vector.tensor_scalar(
                            out=kept["z"][:, 0, w, mt, :], in0=acc[mt][:, w:P:2],
                            scalar1=kept["stats"][:, 0, mt, w, 1:2], scalar2=kept["rstd"][:, r : r + 1],
                            op0=ALU.subtract, op1=ALU.mult,
                        )

            def turn(first):
                bank = banks.tile([P, 2, 2, P], F32, name="turned", tag="bank")
                for i in range(first, min(first + 2, count)):
                    for w in range(2):
                        nc.tensor.transpose(
                            out=bank[:, i - first, w],
                            in_=kept["z"][:, i, w].rearrange("p mt j -> p (mt j)"), identity=ident[:],
                        )
                kept["turned"] = bank

            def activate(first):
                if first == 0:
                    stat("half_tanh", count, P)
                    stat("half_relu", count, P)
                for i in range(first, min(first + 2, count)):
                    for name, w, func in (("half_tanh", 0, FUNC.Tanh), ("half_relu", 1, FUNC.Relu)):
                        gain, shift = w * G + groups[i], (2 + w) * G + groups[i]
                        nc.scalar.activation(
                            out=kept[name][:, i, :], in_=kept["turned"][:, i - first, w],
                            func=func, scale=half_affine[:, gain : gain + 1],
                            bias=half_affine[:, shift : shift + 1],
                        )

            def gate():
                nc.vector.scalar_tensor_tensor(
                    out=gated[:, 0 : count * P], in0=kept["half_tanh"][:].rearrange("p i n -> p (i n)"),
                    scalar=1.0, in1=kept["half_relu"][:].rearrange("p i n -> p (i n)"),
                    op0=ALU.add, op1=ALU.mult,
                )

            def add_masks():
                bank = banks.tile([P, BANK], F32, name="bank", tag="bank")
                for i in range(count):
                    for m2 in range(2):
                        first = i * P + m2 * H
                        nc.tensor.matmul(
                            out=bank[:, i * H : (i + 1) * H], lhsT=gated[:, first : first + P],
                            rhs=fold[:], start=(m2 == 0), stop=(m2 == 1),
                        )
                result = stat("result", count * H)
                nc.scalar.copy(out=result[0:B], in_=bank[0:B, 0 : count * H])

            def store():
                nc.sync.dma_start(
                    out=out[:, groups[0] * H : (groups[-1] + 1) * H], in_=kept["result"][0:B]
                )

            def each(step):
                return [lambda i=i: step(i) for i in range(count)]

            return {
                "statistics": each(statistics), "take_sums": each(take_sums), "power": power,
                "offsets": offsets, "normalise": each(normalise), "normalise_in_psum": normalise_in_psum,
                "turn": turn, "activate": activate, "gate": gate, "add_masks": add_masks,
                "store": store,
            }

        first_masks = entmax_steps(MASK_BATCHES[0])
        first_masks["pass_maxima"]()
        first_masks["spread_maxima"]()
        first_masks["row_maxima"]()
        order_masks()
        first_masks["exponentials"][0]()
        prepare_w(0, 0, 0, nc.vector.tensor_copy)
        prepare_w(0, 0, 1, nc.vector.tensor_copy)
        first_masks["row_sums"]()
        prepare_x_shared(0, nc.vector.tensor_copy)
        first_masks["power"]()
        prepare_w(0, 1, 0, nc.vector.tensor_copy)
        prepare_w(0, 1, 1, nc.vector.tensor_copy)
        first_masks["scale"][0]()
        prepare_x_vector(0)
        first_masks["turn"][0]()
        quantise_w(0)
        scalar_multiply(0, 0)
        scalar_multiply(0, 1)
        prepare_x_shared(1)
        prepare_w(1, 0, 0)

        todo = {}

        def put(n, slot, work):
            todo.setdefault((n, slot), []).append(work)

        def run(n, slot):
            for work in todo.get((n, slot), []):
                work()

        put(1, 0, turn_affine)
        for pairs in MASK_BATCHES[1:]:
            n = (pairs[0] - 1) * PAIR * UNITS
            steps = entmax_steps(pairs)
            put(n, 0, steps["pass_maxima"])
            put(n, 1, steps["spread_maxima"])
            put(n, 2, steps["row_maxima"])
            put(n, 3, steps["exponentials"][0])
            put(n + 1, 1, steps["exponentials"][1])
            put(n + 1, 3, steps["row_sums"])
            put(n + 2, "gpsimd", steps["power"])
            put(n + 2, 1, steps["scale"][0])
            put(n + 2, 3, steps["turn"][0])
            put(n + 4, 1, steps["scale"][1])
            put(n + 5, 1, steps["turn"][1])
        for groups in LN_BATCHES[:-1]:
            steps = layer_norm_steps(groups)
            for i, g in enumerate(groups):
                put((g + 1) * UNITS, 0, steps["statistics"][i])
                put((g + 1) * UNITS, 0, steps["take_sums"][i])
            n = (groups[-1] + 1) * UNITS + 1
            put(n, "gpsimd", steps["power"])
            put(n, 2, steps["offsets"])
            for i in range(len(groups)):
                put(n + i // 2, 3, steps["normalise"][i])
            for first in range(0, len(groups), 2):
                n += 1
                put(n, 2, lambda steps=steps, first=first: steps["turn"](first))
                put(n, 3, lambda steps=steps, first=first: steps["activate"](first))
            put(n + 1, 2, steps["gate"])
            put(n + 1, 3, steps["add_masks"])
            put(n + 2, 0, steps["store"])
        last_norm = layer_norm_steps(LN_BATCHES[-1])

        for n in range(N_UNITS):
            more = n + 1 < N_UNITS
            if n + LOAD_AHEAD < N_UNITS:
                load(n + LOAD_AHEAD)
            if n == 4:
                load_logits(MASK_BATCHES[2])
            weighted = vector_multiply(n)
            gpsimd_multiply(n)
            vector_share(n)
            run(n, "gpsimd")
            scalar_regroup(n)
            if more:
                prepare_w(n + 1, 0, 1)
                prepare_w(n + 1, 1, 0)
                prepare_w(n + 1, 1, 1)
            run(n, 0)
            if n > 0:
                quantise_w(n)
            run(n, 1)
            if more:
                scalar_multiply(n + 1, 0)
                prepare_x_vector(n + 1)
            contract(n, 0, weighted)
            run(n, 2)
            if more:
                scalar_multiply(n + 1, 1)
                if n + 2 < N_UNITS:
                    prepare_x_shared(n + 2)
                    prepare_w(n + 2, 0, 0)
                contract(n, 1, shared_of[n])
            else:
                for cc in range(CC):
                    contract(n, 1, shared_of[n], cc, cc + 1)
            run(n, 3)

        last_norm["statistics"][0]()
        last_norm["power"]()
        for slot in (0, 2, 3):
            run(N_UNITS, slot)
        last_norm["normalise_in_psum"]()
        last_norm["turn"](0)
        run(N_UNITS + 1, 2)
        last_norm["activate"](0)
        last_norm["gate"]()
        run(N_UNITS + 1, 3)
        last_norm["add_masks"]()
        run(N_UNITS + 2, 0)
        last_norm["store"]()
